import numpy as np
import ml_dtypes


def mxq(x, axis, fmt="e4m3"):
    dtype, down = {"e4m3": (ml_dtypes.float8_e4m3fn, 7), "e5m2": (ml_dtypes.float8_e5m2, 14)}[fmt]
    v = np.moveaxis(np.asarray(x, np.float32).astype(ml_dtypes.bfloat16).astype(np.float64), axis, -1)
    blocks = v.reshape(v.shape[:-1] + (-1, 32))
    amax = np.abs(blocks).max(-1, keepdims=True)
    byte = np.maximum(np.where(amax > 0, np.frexp(amax)[1] - 1 + 127, 0) - down, 1)
    scale = np.exp2(byte - 127.0)
    codes = (blocks / scale).astype(np.float32).astype(dtype).astype(np.float64)
    return np.moveaxis((codes * scale).reshape(v.shape), -1, axis)


WIDE = False


def mx_kscale(k):
    if not WIDE:
        return np.ones(k)
    levels = np.array([10, -10, 5, -5, 0])
    if k % 512:
        return np.exp2(np.random.permutation(np.resize(levels, k // 32))).repeat(32)
    a = np.empty((k // 512, 16))
    for p in range(k // 512):
        a[p, :8] = np.random.permutation(np.resize(levels, 8))
        for g in range(8):
            far = levels[np.abs(levels - a[p, g]) >= 10]
            a[p, g + 8] = far[np.random.randint(len(far))]
    return np.exp2(a.ravel()).repeat(32)


BF16 = ml_dtypes.bfloat16


def bf(x):
    return np.asarray(x, np.float32).astype(BF16)


def f64(x):
    return np.asarray(x).astype(np.float64)


E2M1 = np.array([0.0, 0.5, 1.0, 1.5, 2.0, 3.0, 4.0, 6.0, -0.0, -0.5, -1.0, -1.5, -2.0, -3.0, -4.0, -6.0])


def pack_weight(w, fmt):
    k, n = w.shape
    w = f64(bf(w)).reshape(k // 32, 32, n)
    amax = np.abs(w).max(1)
    if fmt == "e4m3":
        byte = np.frexp(amax)[1] - 1 + 127 - 7
    else:
        mant, ex = np.frexp(amax / 6.0)
        byte = np.where(mant > 0.5, ex, ex - 1) + 127
    byte = np.clip(np.where(amax > 0, byte, 1), 1, 254)
    scaled = (w * np.exp2(127.0 - byte)[:, None, :]).reshape(k, n).astype(np.float32)
    by_word = np.ascontiguousarray(scaled.reshape(k // 512, 128, 4, n).transpose(0, 1, 3, 2))
    if fmt == "e4m3":
        words = by_word.astype(ml_dtypes.float8_e4m3fn).view(np.uint8)
    else:
        c = by_word.astype(ml_dtypes.float4_e2m1fn).view(np.uint8) & 0xF
        words = c[..., 0::2] | (c[..., 1::2] << 4)
    return np.ascontiguousarray(words), np.ascontiguousarray(byte.astype(np.uint8).reshape(k // 512, 16, n))


def unpack_weight(words, scales, fmt):
    g, p, n, _ = words.shape
    if fmt == "e4m3":
        vals = np.ascontiguousarray(words).view(ml_dtypes.float8_e4m3fn).astype(np.float64)
    else:
        nib = np.empty((g, p, n, 4), np.uint8)
        nib[..., 0::2] = words & 0xF
        nib[..., 1::2] = words >> 4
        vals = E2M1[nib]
    vals = vals * np.repeat(np.exp2(scales.astype(np.float64) - 127.0), 8, axis=1)[..., None]
    return vals.transpose(0, 1, 3, 2).reshape(g * 512, n)
def pack4(w):
    words, scales = pack_weight(w, "e2m1")
    return words.reshape(words.shape[0], 128, -1), scales


def unpack4(words, scales):
    return unpack_weight(words.reshape(words.shape[0], 128, -1, 2), scales, "e2m1")


B, N, C = 64, 16, 512
NEG_SLOPE = 0.2


def leaky(v):
    return np.where(v >= 0, v, NEG_SLOPE * v)


def draw0():
    s, t = mx_kscale(C), mx_kscale(C)
    w1 = np.random.standard_normal((2, C, C)) * 0.7 / np.sqrt(C) / s[None, :, None] * t
    F = bf(np.random.standard_normal((B, N, C)) * s)
    W1_words, W1_scales = pack4(w1.reshape(2 * C, C))
    b1 = bf(np.random.standard_normal(C) * 0.2 * t)
    W2_words, W2_scales = pack4(np.random.standard_normal((C, C)) / np.sqrt(C) / t[:, None])
    b2 = bf(np.random.standard_normal(C) * 0.2)
    return {"F": F,
            "W1_words": W1_words,
            "W1_scales": W1_scales,
            "b1": b1,
            "W2_words": W2_words,
            "W2_scales": W2_scales,
            "b2": b2}


def core(F, W1_words, W1_scales, b1, W2_words, W2_scales, b2):
    Fq = mxq(f64(F), 2, "e4m3")
    W1 = unpack4(W1_words, W1_scales)
    A = Fq @ W1[:C]
    Bp = Fq @ W1[C:]
    h = leaky(A[:, :, None, :] + Bp[:, None, :, :] + f64(b1))
    h = leaky((mxq(h, 3, "e4m3") @ unpack4(W2_words, W2_scales)) + f64(b2))
    return h.sum(-2)


def e4m3fn_bytes(y):
    return np.clip(np.asarray(y, np.float64), -448.0, 448.0).astype(np.float32).astype(ml_dtypes.float8_e4m3fn).view(np.uint8)


def e4m3fn_values(b):
    return np.asarray(b, np.uint8).view(ml_dtypes.float8_e4m3fn).astype(np.float64)


def setup_inputs():
    d = draw0()
    x0 = np.asarray(d['F']).astype(np.float64)
    s = (np.max(np.abs(x0), axis=(0, 1), keepdims=True) / 448.0).astype(np.float32)
    out = {}
    for k, v in d.items():
        if k == 'F':
            out['F_bytes'] = e4m3fn_bytes(x0 / s.astype(np.float64))
            out['F_scale'] = s
        else:
            out[k] = v
    return out


def reference(F_bytes, F_scale, W1_words, W1_scales, b1, W2_words, W2_scales, b2):
    return core(e4m3fn_values(F_bytes) * F_scale.astype(np.float64), W1_words, W1_scales, b1, W2_words, W2_scales, b2)

@@ -1,0 +1,380 @@
+from contextlib import ExitStack
+
+import concourse.mybir as mybir
+from concourse.masks import make_identity
+
+F32 = mybir.dt.float32
+BF16 = mybir.dt.bfloat16
+I32 = mybir.dt.int32
+U8 = mybir.dt.uint8
+FP8 = mybir.dt.float8_e4m3fn
+FP8X4 = mybir.dt.float8_e4m3fn_x4
+FP4X4 = mybir.dt.float4_e2m1fn_x4
+ALU = mybir.AluOpType
+ACT = mybir.ActivationFunctionType
+
+P = 128
+SETS, NODES, C = 64, 16, 512
+SLOPE = 0.2
+FLOPS = 2 * SETS * NODES * C * 2 * C + 2 * SETS * NODES * NODES * C * C
+
+UNIT = 512
+GROUPS = 2
+UNITS = GROUPS * NODES
+AHEAD = 3
+JA = 3
+BLOCK = UNIT // 4
+SPLIT = [0, 0, 32] + [64] * 29
+
+
+def on_scalar(u):
+    return SPLIT[u]
+
+
+def tile_nonlocalmp_pa_t_w4_kernel(tc, F_bytes, F_scale, W1_words, W1_scales, b1, W2_words, W2_scales, b2, out):
+    nc = tc.nc
+    with ExitStack() as ctx:
+        ctx.enter_context(tc.manual_schedule())
+        const = ctx.enter_context(tc.tile_pool(name="const", bufs=1))
+        work = ctx.enter_context(tc.tile_pool(name="work", bufs=3))
+        ps = ctx.enter_context(tc.psum_pool(name="ps", bufs=1))
+
+        fbytes = const.tile([P, 8 * C], U8, align_bytes=64)
+        f_src = F_bytes.rearrange("b (h m) k -> (b h) (m k)", h=2)
+        nc.sync.dma_start(out=fbytes[:, 0 : 4 * C], in_=f_src[:, 0 : 4 * C])
+        fsc = const.tile([P, 4], F32)
+        nc.sync.dma_start(out=fsc[:], in_=F_scale.rearrange("a c (p t) -> p (a c t)", t=4))
+        w1raw = const.tile([P, 2, 2 * C], U8, align_bytes=64)
+        for g in range(2):
+            nc.sync.dma_start(out=w1raw[:, g, :].bitcast(I32), in_=W1_words[g].bitcast(I32))
+        w1sraw = const.tile([P, 2, C], U8, align_bytes=64)
+        w2s = const.tile([P, C], U8, align_bytes=64)
+        nc.vector.memset(w1sraw[:].rearrange("p g n -> p (g n)").bitcast(I32), 0)
+        nc.vector.memset(w2s[:].bitcast(I32), 0)
+        w1s_src = W1_scales.rearrange("g (q r) n -> r q g n", r=4)
+        w2s_src = W2_scales.rearrange("g (q r) n -> r q (g n)", r=4)
+        for r in range(4):
+            nc.sync.dma_start(out=w1sraw[r:P:32, :, :].bitcast(I32), in_=w1s_src[r].bitcast(I32))
+        b1raw = const.tile([P, 4], BF16)
+        nc.sync.dma_start(out=b1raw[:], in_=b1.rearrange("(p t) -> p t", t=4))
+        nc.sync.dma_start(out=fbytes[:, 4 * C : 8 * C], in_=f_src[:, 4 * C : 8 * C])
+        w2 = const.tile([P, 2 * C], U8, align_bytes=64)
+        nc.sync.dma_start(out=w2[:].bitcast(I32), in_=W2_words[0].bitcast(I32))
+        for r in range(4):
+            nc.sync.dma_start(out=w2s[r:P:32, :].bitcast(I32), in_=w2s_src[r].bitcast(I32))
+        b2raw = const.tile([P, P], BF16)
+        nc.sync.dma_start(out=b2raw[0:4, :], in_=b2.rearrange("(c p) -> c p", p=P))
+
+        ident = const.tile([P, P], F32)
+        make_identity(nc, ident[:])
+        warm = const.tile([P, 1], F32)
+        nc.vector.memset(warm[:], 0.0)
+        nc.scalar.activation(out=warm[:], in_=warm[:], func=ACT.Relu)
+        b2f = const.tile([P, P], F32)
+        nc.gpsimd.memset(b2f[:], 0.0)
+
+        w1p = const.tile([P, 2, 4, 2 * P], U8, align_bytes=64)
+        w1s = const.tile([P, 2, 4, P], U8, align_bytes=64)
+
+        def permute_w1(g, t0, t1):
+            nc.vector.tensor_copy(
+                out=w1p[:, g, t0:t1, :].rearrange("p t (m e) -> p t m e", e=2),
+                in_=w1raw[:, g, :].rearrange("p (m t e) -> p t m e", t=4, e=2)[:, t0:t1],
+            )
+
+        def permute_w1_scales(g, t0, t1):
+            nc.vector.tensor_copy(out=w1s[:, g, t0:t1, :], in_=w1sraw[:, g, :].rearrange("p (m t) -> p t m", t=4)[:, t0:t1])
+
+        fwide = const.tile([P, 8, C], BF16, align_bytes=64)
+        fg = const.tile([P, NODES, SETS, 4], BF16, align_bytes=64)
+        fq = const.tile([P, NODES, SETS], I32, align_bytes=64)
+        fs = const.tile([P, NODES, SETS], U8, align_bytes=64)
+        f8q = const.tile([P, NODES, 8, SETS], I32, align_bytes=64)
+        f8s = const.tile([P, NODES, 8, SETS], U8, align_bytes=64)
+
+        def widen(m):
+            nc.scalar.copy(out=fwide[:, m, :], in_=fbytes[:, m * C : (m + 1) * C].bitcast(FP8))
+
+        def transpose_pair(m, tag):
+            xt = ps.tile([P, 2, 2, P], F32, name="xt", tag=tag)
+            for mm in range(2):
+                words = fwide[:, m + mm, :].bitcast(F32)
+                for u in range(2):
+                    nc.tensor.transpose(xt[:, mm, u, :], words[:, u::2], ident[:])
+            return xt
+
+        def scale_out(xt, m):
+            for mm in range(2):
+                src = xt[:, mm, :, :].bitcast(BF16).rearrange("p u (b h e) -> p h b u e", h=2, e=2)
+                sc = fsc[:].rearrange("p (o u e) -> p o u e", o=1, u=2).to_broadcast([P, SETS, 2, 2])
+                for h in range(2):
+                    nc.vector.tensor_tensor(
+                        out=fg[:, 2 * (m + mm) + h, :, :].rearrange("p b (u e) -> p b u e", e=2),
+                        in0=src[:, h],
+                        in1=sc,
+                        op=ALU.mult,
+                    )
+
+        def quantise_f(g):
+            jj = slice(8 * g, 8 * g + 8)
+            nc.vector.quantize_mx(
+                out=fq[:, jj, :].rearrange("p j b -> p (j b)").bitcast(FP8X4),
+                scales=fs[:, jj, :].rearrange("p j b -> p (j b)"),
+                in_=fg[:, jj, :, :].rearrange("p j b t -> p (j b t)"),
+            )
+
+        def repeat_f(j0, j1):
+            n = j1 - j0
+            nc.vector.tensor_copy(
+                out=f8q[:, j0:j1, :, :],
+                in_=fq[:, j0:j1, :].unsqueeze(2).to_broadcast([P, n, 8, SETS]),
+            )
+            nc.vector.tensor_copy(
+                out=f8s[:, j0:j1, :, :].bitcast(I32),
+                in_=fs[:, j0:j1, :].bitcast(I32).unsqueeze(2).to_broadcast([P, n, 8, SETS // 4]),
+            )
+
+        def repeat_f_dma(j0, j1):
+            for j in range(j0, j1):
+                nc.sync.dma_start(out=f8q[:, j, :, :], in_=fq[:, j, :].unsqueeze(1).to_broadcast([P, 8, SETS]))
+                nc.sync.dma_start(
+                    out=f8s[:, j, :, :].bitcast(I32),
+                    in_=fs[:, j, :].bitcast(I32).unsqueeze(1).to_broadcast([P, 8, SETS // 4]),
+                )
+
+        for m in (2, 3):
+            nc.vector.tensor_copy(out=fwide[:, m, :], in_=fbytes[:, m * C : (m + 1) * C].bitcast(FP8))
+        for m in (0, 1):
+            widen(m)
+        for g in range(2):
+            permute_w1(g, 0, 2)
+        xt0 = transpose_pair(0, "l0")
+        xt1 = transpose_pair(2, "l1")
+        scale_out(xt0, 0)
+        scale_out(xt1, 2)
+        permute_w1_scales(0, 0, 2)
+        quantise_f(0)
+        permute_w1_scales(1, 0, 2)
+        repeat_f(0, 1)
+        for m in range(4, 8):
+            widen(m)
+        xt2 = transpose_pair(4, "l2")
+        xt3 = transpose_pair(6, "l3")
+        for g in range(2):
+            permute_w1(g, 2, 4)
+            permute_w1_scales(g, 2, 4)
+        repeat_f(1, 2)
+        repeat_f_dma(2, 4)
+        repeat_f_dma(4, 8)
+        scale_out(xt2, 4)
+        scale_out(xt3, 6)
+        quantise_f(1)
+        repeat_f_dma(8, 16)
+
+        nb2 = const.tile([P, 4], F32)
+        b2x20 = const.tile([P, 4], F32)
+        b2x19 = const.tile([P, 4], F32)
+        b2c = const.tile([P, 4], F32)
+
+        def setup_b2():
+            nc.scalar.copy(out=b2f[0:4, :], in_=b2raw[0:4, :])
+            bt = ps.tile([P, P], F32, name="bt", tag="l0")
+            nc.tensor.transpose(bt[:], b2f[:], ident[:])
+            nc.scalar.activation(out=nb2[:], in_=bt[:, 0:4], func=ACT.Copy, scale=-1.0)
+            nc.scalar.activation(out=b2x20[:], in_=bt[:, 0:4], func=ACT.Copy, scale=20.0)
+            nc.scalar.activation(out=b2x19[:], in_=bt[:, 0:4], func=ACT.Copy, scale=19.0)
+            nc.scalar.copy(out=b2c[:], in_=bt[:, 0:4])
+
+        v_of, h_of, hq_of, pn_of, acc_of, lin_of = {}, {}, {}, {}, {}, {}
+
+        def first_matmul(u, t, tag="z"):
+            g, j = divmod(u, NODES)
+            z = ps.tile([P, UNIT], F32, name="z", tag=tag, bufs=2)
+            jj = slice(8 * g, 8 * g + 8)
+            nc.tensor.matmul_mx(
+                out=z[:],
+                lhsT=w1p[:, 0, t, :].bitcast(FP4X4),
+                lhsT_scale=w1s[:, 0, t, :],
+                rhs=fq[:, jj, :].rearrange("p j b -> p (j b)").bitcast(FP8X4),
+                rhs_scale=fs[:, jj, :].rearrange("p j b -> p (j b)"),
+                start=True,
+                stop=False,
+            )
+            nc.tensor.matmul_mx(
+                out=z[:],
+                lhsT=w1p[:, 1, t, :].bitcast(FP4X4),
+                lhsT_scale=w1s[:, 1, t, :],
+                rhs=f8q[:, j, :, :].rearrange("p r b -> p (r b)").bitcast(FP8X4),
+                rhs_scale=f8s[:, j, :, :].rearrange("p r b -> p (r b)"),
+                start=False,
+                stop=True,
+            )
+            return z
+
+        def leave_first(u, t, z):
+            if t == 0:
+                v = work.tile([P, UNIT // 4, 4, 4], F32, name="v", align_bytes=64)
+                v_of[u] = v
+            nc.scalar.activation(out=v_of[u][:, :, t, :], in_=z[:].rearrange("p (e c) -> p c e", e=4), func=ACT.Identity, bias=b1raw[:, t : t + 1], scale=1.0)
+
+        def scalar_part(u, piece):
+            k = on_scalar(u)
+            if k == 0:
+                return
+            if piece == 0:
+                pos = work.tile([P, 2, BLOCK, 2, 4], BF16, name="pos", bufs=2)
+                neg = work.tile([P, 2, BLOCK, 2, 4], BF16, name="neg", bufs=2)
+                pn_of[u] = (pos, neg)
+            pair, sign = divmod(piece, 2)
+            nc.scalar.activation(
+                out=pn_of[u][sign][:, pair, 0:k].rearrange("p c e t -> p c t e"),
+                in_=v_of[u][:, BLOCK - k :, :, 2 * pair : 2 * pair + 2],
+                func=ACT.Relu,
+                scale=(1.0, -SLOPE)[sign],
+            )
+
+        def leaky_direct(u, pair):
+            if pair == 0:
+                h = work.tile([P, 4, UNIT // 4, 4], BF16, name="h", align_bytes=64)
+                h_of[u] = h
+            d = BLOCK - on_scalar(u)
+            es = slice(2 * pair, 2 * pair + 2)
+            src = v_of[u][:, 0:d, :, es].rearrange("p c t e -> p (c t) e")
+            nc.vector.scalar_tensor_tensor(
+                out=h_of[u][:, es, 0:d, :].rearrange("p e c t -> p (c t) e"), in0=src, scalar=SLOPE, in1=src, op0=ALU.mult, op1=ALU.max
+            )
+
+        def leaky_join(u, pair):
+            k = on_scalar(u)
+            if k == 0:
+                return
+            pos, neg = pn_of[u]
+            nc.vector.tensor_tensor(
+                out=h_of[u][:, 2 * pair : 2 * pair + 2, BLOCK - k :, :].rearrange("p e c t -> p c e t"),
+                in0=pos[:, pair, 0:k],
+                in1=neg[:, pair, 0:k],
+                op=ALU.subtract,
+            )
+
+        def quantise_h(u):
+            hq = work.tile([P, UNIT], I32, name="hq", align_bytes=64)
+            hs = work.tile([P, UNIT], U8, name="hs", align_bytes=64)
+            hq_of[u] = (hq, hs)
+            nc.vector.quantize_mx(out=hq[:].bitcast(FP8X4), scales=hs[:], in_=h_of.pop(u)[:].rearrange("p e c t -> p (e c t)"))
+
+        def second_matmul(u, c, to, start, stop):
+            hq, hs = hq_of[u]
+            nc.tensor.matmul_mx(
+                out=to[:],
+                lhsT=w2[:, 2 * P * c : 2 * P * (c + 1)].bitcast(FP4X4),
+                lhsT_scale=w2s[:, P * c : P * (c + 1)],
+                rhs=hq[:].bitcast(FP8X4),
+                rhs_scale=hs[:],
+                start=start,
+                stop=stop,
+            )
+
+        def message(u, c):
+            r = ps.tile([P, UNIT], F32, name="r", tag="r", bufs=2)
+            second_matmul(u, c, r, True, True)
+            return r
+
+        def linear_sum(u, c):
+            g, j = divmod(u, NODES)
+            if j == 0:
+                lin = ps.tile([P, UNIT], F32, name="lin", tag="l%d" % c)
+                lin_of[g, c] = lin
+            second_matmul(u, c, lin_of[g, c], j == 0, j == NODES - 1)
+
+        last_of = {}
+
+        def by_scalar(u, c):
+            return u == UNITS - 1 and c % 2 == 1
+
+        def accumulate(u, c, r):
+            g, j = divmod(u, NODES)
+            if j == 0 and c == 0:
+                acc = const.tile([P, 4, UNIT], F32, name="acc%d" % g)
+                acc_of[g] = acc
+            a = acc_of[g][:, c, :]
+            if by_scalar(u, c):
+                last = work.tile([P, UNIT], F32, name="last", bufs=2)
+                nc.scalar.activation(out=last[:], in_=r[:], func=ACT.Relu, bias=b2c[:, c : c + 1], scale=1.0)
+                last_of[g, c] = last
+            elif j == 0:
+                start = b2x19 if by_scalar(u + NODES - 1, c) else b2x20
+                nc.vector.tensor_scalar(out=a, in0=r[:], scalar1=nb2[:, c : c + 1], scalar2=start[:, c : c + 1], op0=ALU.max, op1=ALU.add)
+            else:
+                nc.vector.scalar_tensor_tensor(out=a, in0=r[:], scalar=nb2[:, c : c + 1], in1=a, op0=ALU.max, op1=ALU.add)
+
+        quarter_of = {}
+
+        def leave_linear(g, c):
+            quarter = work.tile([P, UNIT], F32, name="quarter", bufs=4)
+            nc.scalar.activation(out=quarter[:], in_=lin_of[g, c][:], func=ACT.Copy, scale=0.25)
+            quarter_of[g, c] = quarter
+
+        out_v = out.rearrange("b (h q s) c -> h q b s c", h=2, q=2)
+
+        def finish(g, c, tag, bufs, on_vector):
+            tr = ps.tile([P, 4, P], F32, name="tr", tag=tag, bufs=bufs)
+            for s in range(4):
+                cols = slice(P * s, P * (s + 1))
+                nc.tensor.matmul(tr[:, s, :], lhsT=quarter_of[g, c][:, cols], rhs=ident[:], is_transpose=True, start=True, stop=False)
+                if (g, c) in last_of:
+                    nc.tensor.matmul(tr[:, s, :], lhsT=acc_of[g][:, c, cols], rhs=ident[:], is_transpose=True, start=False, stop=False)
+                    nc.tensor.matmul(tr[:, s, :], lhsT=last_of[g, c][:, cols], rhs=ident[:], is_transpose=True, start=False, stop=True)
+                else:
+                    nc.tensor.matmul(tr[:, s, :], lhsT=acc_of[g][:, c, cols], rhs=ident[:], is_transpose=True, start=False, stop=True)
+            st = work.tile([P, 4, P], F32, name="st")
+            if on_vector:
+                nc.vector.tensor_scalar(out=st[:], in0=tr[:], scalar1=0.8, scalar2=None, op0=ALU.mult)
+            else:
+                nc.scalar.activation(out=st[:], in_=tr[:], func=ACT.Copy, scale=0.8)
+            for h in range(2):
+                nc.sync.dma_start(out=out_v[h, g][:, :, P * c : P * (c + 1)], in_=st[64 * h : 64 * h + 64, :, :])
+
+        def unit_matmuls(u):
+            for t in range(4):
+                z = first_matmul(u, t, "zr"[t % 2])
+                leave_first(u, t, z)
+
+        setup_b2()
+        unit_matmuls(0)
+        leaky_direct(0, 0)
+        leaky_direct(0, 1)
+        unit_matmuls(1)
+        quantise_h(0)
+        unit_matmuls(2)
+        leaky_direct(1, 0)
+        leaky_direct(1, 1)
+
+        for u in range(UNITS):
+            w = u + AHEAD
+            for c in range(4):
+                if w < UNITS:
+                    z = first_matmul(w, c)
+                r = message(u, c)
+                linear_sum(u, c)
+                if w < UNITS:
+                    leave_first(w, c, z)
+                if w - 1 < UNITS:
+                    scalar_part(w - 1, c)
+                accumulate(u, c, r)
+                if c == 1 and u + 1 < UNITS:
+                    quantise_h(u + 1)
+                if w - 1 < UNITS:
+                    if c == 0:
+                        leaky_direct(w - 1, 0)
+                    if c == 2:
+                        leaky_direct(w - 1, 1)
+                    if c == JA:
+                        leaky_join(w - 1, 0)
+                    if c == 3:
+                        leaky_join(w - 1, 1)
+                if u % NODES == NODES - 1:
+                    leave_linear(u // NODES, c)
+                if NODES <= u < NODES + 4 and c == 3:
+                    finish(0, u - NODES, "r", 2, False)
+        for c in range(4):
+            finish(1, c, ("r", "z")[c % 2], 2, c % 2 == 1)

@@ -18,17 +18,24 @@ SETS, NODES, C = 64, 16, 512
 SLOPE = 0.2
 FLOPS = 2 * SETS * NODES * C * 2 * C + 2 * SETS * NODES * NODES * C * C
 
-UNIT = 512
-GROUPS = 2
-UNITS = GROUPS * NODES
-AHEAD = 3
-JA = 3
-BLOCK = UNIT // 4
-SPLIT = [0, 0, 32] + [64] * 29
+TILES = 8
+SENDERS = 4
+STEPS = NODES // SENDERS
+UNITS = TILES * STEPS
+CHUNKS = C // P
 
 
-def on_scalar(u):
-    return SPLIT[u]
+OWN = 96
+
+
+def scalar_columns(u):
+    if u < 2:
+        return OWN
+    if u == 2:
+        return 72
+    if u == UNITS - 1:
+        return 0
+    return 52
 
 
 def tile_nonlocalmp_pa_t_w4_kernel(tc, F_bytes, F_scale, W1_words, W1_scales, b1, W2_words, W2_scales, b2, out):
@@ -39,14 +46,14 @@ def tile_nonlocalmp_pa_t_w4_kernel(tc, F_bytes, F_scale, W1_words, W1_scales, b1
         work = ctx.enter_context(tc.tile_pool(name="work", bufs=3))
         ps = ctx.enter_context(tc.psum_pool(name="ps", bufs=1))
 
-        fbytes = const.tile([P, 8 * C], U8, align_bytes=64)
         f_src = F_bytes.rearrange("b (h m) k -> (b h) (m k)", h=2)
-        nc.sync.dma_start(out=fbytes[:, 0 : 4 * C], in_=f_src[:, 0 : 4 * C])
+        fbytes0 = const.tile([P, 2 * C], U8, align_bytes=64)
+        fbytes1 = const.tile([P, 6 * C], U8, align_bytes=64)
+        nc.sync.dma_start(out=fbytes0[:], in_=f_src[:, 0 : 2 * C])
         fsc = const.tile([P, 4], F32)
         nc.sync.dma_start(out=fsc[:], in_=F_scale.rearrange("a c (p t) -> p (a c t)", t=4))
         w1raw = const.tile([P, 2, 2 * C], U8, align_bytes=64)
-        for g in range(2):
-            nc.sync.dma_start(out=w1raw[:, g, :].bitcast(I32), in_=W1_words[g].bitcast(I32))
+        nc.sync.dma_start(out=w1raw[:].bitcast(I32), in_=W1_words.rearrange("g p n -> p g n").bitcast(I32))
         w1sraw = const.tile([P, 2, C], U8, align_bytes=64)
         w2s = const.tile([P, C], U8, align_bytes=64)
         nc.vector.memset(w1sraw[:].rearrange("p g n -> p (g n)").bitcast(I32), 0)
@@ -57,7 +64,7 @@ def tile_nonlocalmp_pa_t_w4_kernel(tc, F_bytes, F_scale, W1_words, W1_scales, b1
             nc.sync.dma_start(out=w1sraw[r:P:32, :, :].bitcast(I32), in_=w1s_src[r].bitcast(I32))
         b1raw = const.tile([P, 4], BF16)
         nc.sync.dma_start(out=b1raw[:], in_=b1.rearrange("(p t) -> p t", t=4))
-        nc.sync.dma_start(out=fbytes[:, 4 * C : 8 * C], in_=f_src[:, 4 * C : 8 * C])
+        nc.sync.dma_start(out=fbytes1[:], in_=f_src[:, 2 * C : 8 * C])
         w2 = const.tile([P, 2 * C], U8, align_bytes=64)
         nc.sync.dma_start(out=w2[:].bitcast(I32), in_=W2_words[0].bitcast(I32))
         for r in range(4):
@@ -67,314 +74,293 @@ def tile_nonlocalmp_pa_t_w4_kernel(tc, F_bytes, F_scale, W1_words, W1_scales, b1
 
         ident = const.tile([P, P], F32)
         make_identity(nc, ident[:])
-        warm = const.tile([P, 1], F32)
-        nc.vector.memset(warm[:], 0.0)
-        nc.scalar.activation(out=warm[:], in_=warm[:], func=ACT.Relu)
         b2f = const.tile([P, P], F32)
         nc.gpsimd.memset(b2f[:], 0.0)
 
         w1p = const.tile([P, 2, 4, 2 * P], U8, align_bytes=64)
         w1s = const.tile([P, 2, 4, P], U8, align_bytes=64)
 
-        def permute_w1(g, t0, t1):
+        def permute_w1(g):
             nc.vector.tensor_copy(
-                out=w1p[:, g, t0:t1, :].rearrange("p t (m e) -> p t m e", e=2),
-                in_=w1raw[:, g, :].rearrange("p (m t e) -> p t m e", t=4, e=2)[:, t0:t1],
+                out=w1p[:, g, :, :].rearrange("p t (m e) -> p t m e", e=2),
+                in_=w1raw[:, g, :].rearrange("p (m t e) -> p t m e", t=4, e=2),
             )
 
-        def permute_w1_scales(g, t0, t1):
-            nc.vector.tensor_copy(out=w1s[:, g, t0:t1, :], in_=w1sraw[:, g, :].rearrange("p (m t) -> p t m", t=4)[:, t0:t1])
+        def permute_w1_scales(g):
+            nc.vector.tensor_copy(out=w1s[:, g, :, :], in_=w1sraw[:, g, :].rearrange("p (m t) -> p t m", t=4))
 
-        fwide = const.tile([P, 8, C], BF16, align_bytes=64)
-        fg = const.tile([P, NODES, SETS, 4], BF16, align_bytes=64)
-        fq = const.tile([P, NODES, SETS], I32, align_bytes=64)
-        fs = const.tile([P, NODES, SETS], U8, align_bytes=64)
-        f8q = const.tile([P, NODES, 8, SETS], I32, align_bytes=64)
-        f8s = const.tile([P, NODES, 8, SETS], U8, align_bytes=64)
+        fwide = const.tile([P, TILES, C], BF16, align_bytes=64)
+        fg = const.tile([P, TILES, 2, SETS, 4], BF16, align_bytes=64)
+        fq = const.tile([P, TILES, P], I32, align_bytes=64)
+        fs = const.tile([P, TILES, P], U8, align_bytes=64)
+        bp = const.tile([P, NODES, SETS, 4], F32, align_bytes=64)
 
         def widen(m):
-            nc.scalar.copy(out=fwide[:, m, :], in_=fbytes[:, m * C : (m + 1) * C].bitcast(FP8))
+            src = fbytes0[:, m * C : (m + 1) * C] if m < 2 else fbytes1[:, (m - 2) * C : (m - 1) * C]
+            nc.scalar.copy(out=fwide[:, m, :], in_=src.bitcast(FP8))
 
-        def transpose_pair(m, tag):
-            xt = ps.tile([P, 2, 2, P], F32, name="xt", tag=tag)
+        xt_of = {}
+
+        def turn_f(q):
+            xt = ps.tile([P, 2, 2, P], F32, name="xt", tag="sum", bufs=2)
+            xt_of[q] = xt
             for mm in range(2):
-                words = fwide[:, m + mm, :].bitcast(F32)
+                words = fwide[:, 2 * q + mm, :].bitcast(F32)
                 for u in range(2):
                     nc.tensor.transpose(xt[:, mm, u, :], words[:, u::2], ident[:])
-            return xt
 
-        def scale_out(xt, m):
+        def scale_f(q):
+            sc = fsc[:].rearrange("p (o u e) -> p o u e", o=1, u=2).to_broadcast([P, SETS, 2, 2])
             for mm in range(2):
-                src = xt[:, mm, :, :].bitcast(BF16).rearrange("p u (b h e) -> p h b u e", h=2, e=2)
-                sc = fsc[:].rearrange("p (o u e) -> p o u e", o=1, u=2).to_broadcast([P, SETS, 2, 2])
+                src = xt_of[q][:, mm, :, :].bitcast(BF16).rearrange("p u (b h e) -> p h b u e", h=2, e=2)
                 for h in range(2):
                     nc.vector.tensor_tensor(
-                        out=fg[:, 2 * (m + mm) + h, :, :].rearrange("p b (u e) -> p b u e", e=2),
-                        in0=src[:, h],
-                        in1=sc,
-                        op=ALU.mult,
+                        out=fg[:, 2 * q + mm, h, :, :].rearrange("p b (u e) -> p b u e", e=2), in0=src[:, h], in1=sc, op=ALU.mult
                     )
 
-        def quantise_f(g):
-            jj = slice(8 * g, 8 * g + 8)
+        def quantise_f(q):
+            mm = slice(2 * q, 2 * q + 2)
             nc.vector.quantize_mx(
-                out=fq[:, jj, :].rearrange("p j b -> p (j b)").bitcast(FP8X4),
-                scales=fs[:, jj, :].rearrange("p j b -> p (j b)"),
-                in_=fg[:, jj, :, :].rearrange("p j b t -> p (j b t)"),
+                out=fq[:, mm, :].rearrange("p m r -> p (m r)").bitcast(FP8X4),
+                scales=fs[:, mm, :].rearrange("p m r -> p (m r)"),
+                in_=fg[:, mm].rearrange("p m h b t -> p (m h b t)"),
             )
 
-        def repeat_f(j0, j1):
-            n = j1 - j0
-            nc.vector.tensor_copy(
-                out=f8q[:, j0:j1, :, :],
-                in_=fq[:, j0:j1, :].unsqueeze(2).to_broadcast([P, n, 8, SETS]),
-            )
-            nc.vector.tensor_copy(
-                out=f8s[:, j0:j1, :, :].bitcast(I32),
-                in_=fs[:, j0:j1, :].bitcast(I32).unsqueeze(2).to_broadcast([P, n, 8, SETS // 4]),
-            )
-
-        def repeat_f_dma(j0, j1):
-            for j in range(j0, j1):
-                nc.sync.dma_start(out=f8q[:, j, :, :], in_=fq[:, j, :].unsqueeze(1).to_broadcast([P, 8, SETS]))
-                nc.sync.dma_start(
-                    out=f8s[:, j, :, :].bitcast(I32),
-                    in_=fs[:, j, :].bitcast(I32).unsqueeze(1).to_broadcast([P, 8, SETS // 4]),
+        def first_product(g, m, tag, bufs):
+            bank = ps.tile([P, 4, P], F32, name="first", tag=tag, bufs=bufs)
+            for t in range(4):
+                nc.tensor.matmul_mx(
+                    out=bank[:, t, :],
+                    lhsT=w1p[:, g, t, :].bitcast(FP4X4),
+                    lhsT_scale=w1s[:, g, t, :],
+                    rhs=fq[:, m, :].bitcast(FP8X4),
+                    rhs_scale=fs[:, m, :],
+                    start=True,
+                    stop=True,
                 )
+            return bank
 
-        for m in (2, 3):
-            nc.vector.tensor_copy(out=fwide[:, m, :], in_=fbytes[:, m * C : (m + 1) * C].bitcast(FP8))
-        for m in (0, 1):
-            widen(m)
-        for g in range(2):
-            permute_w1(g, 0, 2)
-        xt0 = transpose_pair(0, "l0")
-        xt1 = transpose_pair(2, "l1")
-        scale_out(xt0, 0)
-        scale_out(xt1, 2)
-        permute_w1_scales(0, 0, 2)
-        quantise_f(0)
-        permute_w1_scales(1, 0, 2)
-        repeat_f(0, 1)
-        for m in range(4, 8):
-            widen(m)
-        xt2 = transpose_pair(4, "l2")
-        xt3 = transpose_pair(6, "l3")
-        for g in range(2):
-            permute_w1(g, 2, 4)
-            permute_w1_scales(g, 2, 4)
-        repeat_f(1, 2)
-        repeat_f_dma(2, 4)
-        repeat_f_dma(4, 8)
-        scale_out(xt2, 4)
-        scale_out(xt3, 6)
-        quantise_f(1)
-        repeat_f_dma(8, 16)
+        def leave_b(m, bank):
+            nc.vector.tensor_tensor(
+                out=bp[:, 2 * m : 2 * m + 2, :, :].rearrange("p h b t -> p (h b) t"),
+                in0=bank[:].rearrange("p t r -> p r t"),
+                in1=b1raw[:].unsqueeze(1).to_broadcast([P, P, 4]),
+                op=ALU.add,
+            )
 
-        nb2 = const.tile([P, 4], F32)
-        b2x20 = const.tile([P, 4], F32)
-        b2x19 = const.tile([P, 4], F32)
-        b2c = const.tile([P, 4], F32)
+        b2c = const.tile([P, CHUNKS], F32)
+        b2x4 = const.tile([P, CHUNKS], F32)
 
         def setup_b2():
             nc.scalar.copy(out=b2f[0:4, :], in_=b2raw[0:4, :])
-            bt = ps.tile([P, P], F32, name="bt", tag="l0")
+            bt = ps.tile([P, P], F32, name="bt", tag="lin")
             nc.tensor.transpose(bt[:], b2f[:], ident[:])
-            nc.scalar.activation(out=nb2[:], in_=bt[:, 0:4], func=ACT.Copy, scale=-1.0)
-            nc.scalar.activation(out=b2x20[:], in_=bt[:, 0:4], func=ACT.Copy, scale=20.0)
-            nc.scalar.activation(out=b2x19[:], in_=bt[:, 0:4], func=ACT.Copy, scale=19.0)
-            nc.scalar.copy(out=b2c[:], in_=bt[:, 0:4])
+            nc.scalar.copy(out=b2c[:], in_=bt[:, 0:CHUNKS])
+            nc.scalar.activation(out=b2x4[:], in_=bt[:, 0:CHUNKS], func=ACT.Copy, scale=4.0)
 
-        v_of, h_of, hq_of, pn_of, acc_of, lin_of = {}, {}, {}, {}, {}, {}
+        rest_of, w_of = {}, {}
+        a_of, v_of, h_of, part_of, hq_of, relu_of, lin_of, sum_of, fifth_of = {}, {}, {}, {}, {}, {}, {}, {}, {}
 
-        def first_matmul(u, t, tag="z"):
-            g, j = divmod(u, NODES)
-            z = ps.tile([P, UNIT], F32, name="z", tag=tag, bufs=2)
-            jj = slice(8 * g, 8 * g + 8)
-            nc.tensor.matmul_mx(
-                out=z[:],
-                lhsT=w1p[:, 0, t, :].bitcast(FP4X4),
-                lhsT_scale=w1s[:, 0, t, :],
-                rhs=fq[:, jj, :].rearrange("p j b -> p (j b)").bitcast(FP8X4),
-                rhs_scale=fs[:, jj, :].rearrange("p j b -> p (j b)"),
-                start=True,
-                stop=False,
-            )
-            nc.tensor.matmul_mx(
-                out=z[:],
-                lhsT=w1p[:, 1, t, :].bitcast(FP4X4),
-                lhsT_scale=w1s[:, 1, t, :],
-                rhs=f8q[:, j, :, :].rearrange("p r b -> p (r b)").bitcast(FP8X4),
-                rhs_scale=f8s[:, j, :, :].rearrange("p r b -> p (r b)"),
-                start=False,
-                stop=True,
-            )
-            return z
+        def receivers(m):
+            a_of[m] = first_product(0, m, "a", 2)
+            rest = work.tile([P, P - OWN, 4], F32, name="rest", bufs=2, align_bytes=64)
+            rest_of[m] = rest
+            nc.scalar.copy(out=rest[:], in_=a_of[m][:].rearrange("p t r -> p r t")[:, OWN:, :])
 
-        def leave_first(u, t, z):
-            if t == 0:
-                v = work.tile([P, UNIT // 4, 4, 4], F32, name="v", align_bytes=64)
+        def add(u, h):
+            m, q = divmod(u, STEPS)
+            if u not in v_of:
+                v = work.tile([P, SENDERS, OWN, 4], F32, name="v", align_bytes=64)
                 v_of[u] = v
-            nc.scalar.activation(out=v_of[u][:, :, t, :], in_=z[:].rearrange("p (e c) -> p c e", e=4), func=ACT.Identity, bias=b1raw[:, t : t + 1], scale=1.0)
-
-        def scalar_part(u, piece):
-            k = on_scalar(u)
-            if k == 0:
-                return
-            if piece == 0:
-                pos = work.tile([P, 2, BLOCK, 2, 4], BF16, name="pos", bufs=2)
-                neg = work.tile([P, 2, BLOCK, 2, 4], BF16, name="neg", bufs=2)
-                pn_of[u] = (pos, neg)
-            pair, sign = divmod(piece, 2)
-            nc.scalar.activation(
-                out=pn_of[u][sign][:, pair, 0:k].rearrange("p c e t -> p c t e"),
-                in_=v_of[u][:, BLOCK - k :, :, 2 * pair : 2 * pair + 2],
-                func=ACT.Relu,
-                scale=(1.0, -SLOPE)[sign],
-            )
-
-        def leaky_direct(u, pair):
-            if pair == 0:
-                h = work.tile([P, 4, UNIT // 4, 4], BF16, name="h", align_bytes=64)
-                h_of[u] = h
-            d = BLOCK - on_scalar(u)
-            es = slice(2 * pair, 2 * pair + 2)
-            src = v_of[u][:, 0:d, :, es].rearrange("p c t e -> p (c t) e")
-            nc.vector.scalar_tensor_tensor(
-                out=h_of[u][:, es, 0:d, :].rearrange("p e c t -> p (c t) e"), in0=src, scalar=SLOPE, in1=src, op0=ALU.mult, op1=ALU.max
-            )
-
-        def leaky_join(u, pair):
-            k = on_scalar(u)
-            if k == 0:
-                return
-            pos, neg = pn_of[u]
+            cols = slice(SETS * h, min(SETS * (h + 1), OWN))
+            n = cols.stop - cols.start
             nc.vector.tensor_tensor(
-                out=h_of[u][:, 2 * pair : 2 * pair + 2, BLOCK - k :, :].rearrange("p e c t -> p c e t"),
-                in0=pos[:, pair, 0:k],
-                in1=neg[:, pair, 0:k],
-                op=ALU.subtract,
+                out=v_of[u][:, :, cols, :],
+                in0=a_of[m][:].rearrange("p t r -> p r t")[:, cols, :].unsqueeze(1).to_broadcast([P, SENDERS, n, 4]),
+                in1=bp[:, SENDERS * q : SENDERS * (q + 1), 0:n, :],
+                op=ALU.add,
             )
+
+        def add_rest(u):
+            m, q = divmod(u, STEPS)
+            w = work.tile([P, SENDERS, P - OWN, 4], F32, name="w", bufs=1, align_bytes=64)
+            w_of[u] = w
+            nc.gpsimd.tensor_tensor(
+                out=w[:],
+                in0=rest_of[m][:].unsqueeze(1).to_broadcast([P, SENDERS, P - OWN, 4]),
+                in1=bp[:, SENDERS * q : SENDERS * (q + 1), OWN - SETS :, :],
+                op=ALU.add,
+            )
+
+        def scalar_part(u, sign):
+            x = scalar_columns(u)
+            if x == 0:
+                return
+            part = work.tile([P, SENDERS, x, 4], BF16, name="part", bufs=4, align_bytes=64)
+            part_of[u, sign] = part
+            nc.scalar.activation(out=part[:], in_=v_of[u][:, :, 0:x, :], func=ACT.Relu, scale=(1.0, -SLOPE)[sign])
+
+        def h_tile(u):
+            if u not in h_of:
+                h = work.tile([P, SENDERS, P, 4], BF16, name="h", align_bytes=64)
+                h_of[u] = h
+            return h_of[u]
+
+        def leaky(to, src):
+            src = src.rearrange("p j r t -> p j (r t)")
+            nc.vector.scalar_tensor_tensor(out=to.rearrange("p j r t -> p j (r t)"), in0=src, scalar=SLOPE, in1=src, op0=ALU.mult, op1=ALU.max)
+
+        def leaky_own(u):
+            x = scalar_columns(u)
+            if x < OWN:
+                leaky(h_tile(u)[:, :, x:OWN, :], v_of[u][:, :, x:, :])
+
+        def leaky_rest(u):
+            leaky(h_tile(u)[:, :, OWN:, :], w_of[u][:])
+
+        def join(u):
+            x = scalar_columns(u)
+            if x > 0:
+                nc.vector.tensor_tensor(out=h_tile(u)[:, :, 0:x, :], in0=part_of[u, 0][:], in1=part_of[u, 1][:], op=ALU.subtract)
 
         def quantise_h(u):
-            hq = work.tile([P, UNIT], I32, name="hq", align_bytes=64)
-            hs = work.tile([P, UNIT], U8, name="hs", align_bytes=64)
+            hq = work.tile([P, SENDERS * P], I32, name="hq", align_bytes=64)
+            hs = work.tile([P, SENDERS * P], U8, name="hs", align_bytes=64)
             hq_of[u] = (hq, hs)
-            nc.vector.quantize_mx(out=hq[:].bitcast(FP8X4), scales=hs[:], in_=h_of.pop(u)[:].rearrange("p e c t -> p (e c t)"))
+            nc.vector.quantize_mx(out=hq[:].bitcast(FP8X4), scales=hs[:], in_=h_of[u][:].rearrange("p j r t -> p (j r t)"))
 
-        def second_matmul(u, c, to, start, stop):
+        def message(u, c):
             hq, hs = hq_of[u]
+            bank = ps.tile([P, SENDERS * P], F32, name="bank", tag="message", bufs=3)
             nc.tensor.matmul_mx(
-                out=to[:],
+                out=bank[:],
                 lhsT=w2[:, 2 * P * c : 2 * P * (c + 1)].bitcast(FP4X4),
                 lhsT_scale=w2s[:, P * c : P * (c + 1)],
                 rhs=hq[:].bitcast(FP8X4),
                 rhs_scale=hs[:],
-                start=start,
-                stop=stop,
+                start=True,
+                stop=True,
+            )
+            return bank
+
+        def linear(u, j):
+            m, q = divmod(u, STEPS)
+            hq, hs = hq_of[u]
+            if q == 0 and j == 0:
+                lin = ps.tile([P, C], F32, name="lin", tag="lin")
+                lin_of[m] = lin
+            nc.tensor.matmul_mx(
+                out=lin_of[m][:],
+                lhsT=hq[:, P * j : P * (j + 1)].bitcast(FP8X4),
+                lhsT_scale=hs[:, P * j : P * (j + 1)],
+                rhs=w2[:].bitcast(FP4X4),
+                rhs_scale=w2s[:],
+                start=(q == 0 and j == 0),
+                stop=(q == STEPS - 1 and j == SENDERS - 1),
             )
 
-        def message(u, c):
-            r = ps.tile([P, UNIT], F32, name="r", tag="r", bufs=2)
-            second_matmul(u, c, r, True, True)
-            return r
-
-        def linear_sum(u, c):
-            g, j = divmod(u, NODES)
-            if j == 0:
-                lin = ps.tile([P, UNIT], F32, name="lin", tag="l%d" % c)
-                lin_of[g, c] = lin
-            second_matmul(u, c, lin_of[g, c], j == 0, j == NODES - 1)
-
-        last_of = {}
-
-        def by_scalar(u, c):
-            return u == UNITS - 1 and c % 2 == 1
-
-        def accumulate(u, c, r):
-            g, j = divmod(u, NODES)
-            if j == 0 and c == 0:
-                acc = const.tile([P, 4, UNIT], F32, name="acc%d" % g)
-                acc_of[g] = acc
-            a = acc_of[g][:, c, :]
-            if by_scalar(u, c):
-                last = work.tile([P, UNIT], F32, name="last", bufs=2)
-                nc.scalar.activation(out=last[:], in_=r[:], func=ACT.Relu, bias=b2c[:, c : c + 1], scale=1.0)
-                last_of[g, c] = last
-            elif j == 0:
-                start = b2x19 if by_scalar(u + NODES - 1, c) else b2x20
-                nc.vector.tensor_scalar(out=a, in0=r[:], scalar1=nb2[:, c : c + 1], scalar2=start[:, c : c + 1], op0=ALU.max, op1=ALU.add)
+        def rectify(u, c, bank):
+            relu = work.tile([P, SENDERS, P], F32, name="relu", bufs=6, align_bytes=64)
+            relu_of[u, c] = relu
+            flat = relu[:].rearrange("p j r -> p (j r)")
+            if u >= UNITS - 2 and c % 2 == 1:
+                nc.vector.tensor_scalar(out=flat, in0=bank[:], scalar1=b2c[:, c : c + 1], scalar2=0.0, op0=ALU.add, op1=ALU.max)
             else:
-                nc.vector.scalar_tensor_tensor(out=a, in0=r[:], scalar=nb2[:, c : c + 1], in1=a, op0=ALU.max, op1=ALU.add)
+                nc.scalar.activation(out=flat, in_=bank[:], func=ACT.Relu, bias=b2c[:, c : c + 1], scale=1.0)
 
-        quarter_of = {}
+        def add_up(u, c):
+            m, q = divmod(u, STEPS)
+            if q == 0 and c == 0:
+                total = ps.tile([P, CHUNKS, P], F32, name="total", tag="sum", bufs=2)
+                sum_of[m] = total
+                for cc in range(CHUNKS):
+                    nc.tensor.matmul(
+                        total[:, cc, :], lhsT=b2x4[:, cc : cc + 1].to_broadcast([P, P]), rhs=ident[:], is_transpose=True, start=(cc == 0), stop=False
+                    )
+            for j in range(SENDERS):
+                last = q == STEPS - 1 and c == CHUNKS - 1 and j == SENDERS - 1
+                nc.tensor.matmul(sum_of[m][:, c, :], lhsT=relu_of[u, c][:, j, :], rhs=ident[:], is_transpose=True, start=False, stop=last)
 
-        def leave_linear(g, c):
-            quarter = work.tile([P, UNIT], F32, name="quarter", bufs=4)
-            nc.scalar.activation(out=quarter[:], in_=lin_of[g, c][:], func=ACT.Copy, scale=0.25)
-            quarter_of[g, c] = quarter
+        def leave_linear(m):
+            fifth = work.tile([P, C], F32, name="fifth", bufs=2)
+            fifth_of[m] = fifth
+            nc.scalar.activation(out=fifth[:], in_=lin_of[m][:], func=ACT.Copy, scale=SLOPE)
 
-        out_v = out.rearrange("b (h q s) c -> h q b s c", h=2, q=2)
+        out_v = out.rearrange("b (h m) c -> m h b c", h=2)
 
-        def finish(g, c, tag, bufs, on_vector):
-            tr = ps.tile([P, 4, P], F32, name="tr", tag=tag, bufs=bufs)
-            for s in range(4):
-                cols = slice(P * s, P * (s + 1))
-                nc.tensor.matmul(tr[:, s, :], lhsT=quarter_of[g, c][:, cols], rhs=ident[:], is_transpose=True, start=True, stop=False)
-                if (g, c) in last_of:
-                    nc.tensor.matmul(tr[:, s, :], lhsT=acc_of[g][:, c, cols], rhs=ident[:], is_transpose=True, start=False, stop=False)
-                    nc.tensor.matmul(tr[:, s, :], lhsT=last_of[g, c][:, cols], rhs=ident[:], is_transpose=True, start=False, stop=True)
-                else:
-                    nc.tensor.matmul(tr[:, s, :], lhsT=acc_of[g][:, c, cols], rhs=ident[:], is_transpose=True, start=False, stop=True)
-            st = work.tile([P, 4, P], F32, name="st")
-            if on_vector:
-                nc.vector.tensor_scalar(out=st[:], in0=tr[:], scalar1=0.8, scalar2=None, op0=ALU.mult)
-            else:
-                nc.scalar.activation(out=st[:], in_=tr[:], func=ACT.Copy, scale=0.8)
+        def finish(m):
+            st = work.tile([P, C], F32, name="st", bufs=2)
+            nc.vector.scalar_tensor_tensor(
+                out=st[:], in0=sum_of[m][:].rearrange("p c r -> p (c r)"), scalar=1.0 - SLOPE, in1=fifth_of[m][:], op0=ALU.mult, op1=ALU.add
+            )
             for h in range(2):
-                nc.sync.dma_start(out=out_v[h, g][:, :, P * c : P * (c + 1)], in_=st[64 * h : 64 * h + 64, :, :])
+                nc.sync.dma_start(out=out_v[m, h], in_=st[SETS * h : SETS * (h + 1), :])
 
-        def unit_matmuls(u):
-            for t in range(4):
-                z = first_matmul(u, t, "zr"[t % 2])
-                leave_first(u, t, z)
+        def second_half(u, half):
+            for c in (2 * half, 2 * half + 1):
+                bank = message(u, c)
+                linear(u, c)
+                rectify(u, c, bank)
 
+        widen(0)
+        widen(1)
+        permute_w1(1)
+        turn_f(0)
+        scale_f(0)
+        permute_w1_scales(1)
+        quantise_f(0)
+        permute_w1(0)
+        permute_w1_scales(0)
+        banks = [first_product(1, m, "message", 3) for m in range(2)]
+        receivers(0)
+        for m in range(2):
+            leave_b(m, banks[m])
+        for m in range(2, TILES):
+            widen(m)
+        turn_f(1)
         setup_b2()
-        unit_matmuls(0)
-        leaky_direct(0, 0)
-        leaky_direct(0, 1)
-        unit_matmuls(1)
-        quantise_h(0)
-        unit_matmuls(2)
-        leaky_direct(1, 0)
-        leaky_direct(1, 1)
 
-        for u in range(UNITS):
-            w = u + AHEAD
-            for c in range(4):
-                if w < UNITS:
-                    z = first_matmul(w, c)
-                r = message(u, c)
-                linear_sum(u, c)
-                if w < UNITS:
-                    leave_first(w, c, z)
-                if w - 1 < UNITS:
-                    scalar_part(w - 1, c)
-                accumulate(u, c, r)
-                if c == 1 and u + 1 < UNITS:
-                    quantise_h(u + 1)
-                if w - 1 < UNITS:
-                    if c == 0:
-                        leaky_direct(w - 1, 0)
-                    if c == 2:
-                        leaky_direct(w - 1, 1)
-                    if c == JA:
-                        leaky_join(w - 1, 0)
-                    if c == 3:
-                        leaky_join(w - 1, 1)
-                if u % NODES == NODES - 1:
-                    leave_linear(u // NODES, c)
-                if NODES <= u < NODES + 4 and c == 3:
-                    finish(0, u - NODES, "r", 2, False)
-        for c in range(4):
-            finish(1, c, ("r", "z")[c % 2], 2, c % 2 == 1)
+        for p in range(UNITS + 4):
+            s = p - 2
+            if p < UNITS:
+                add_rest(p)
+                add(p, 0)
+                add(p, 1)
+            if 0 <= s - 2 and (s - 2) % STEPS == STEPS - 1:
+                finish((s - 2) // STEPS)
+            if p + 1 < STEPS:
+                scale_f(p + 1)
+                if p + 2 < STEPS:
+                    turn_f(p + 2)
+            if 0 <= s < UNITS:
+                second_half(s, 0)
+            if p < UNITS:
+                scalar_part(p, 0)
+            if 0 <= s - 1 < UNITS:
+                add_up(s - 1, 2)
+                add_up(s - 1, 3)
+            if 0 <= p - 1 < UNITS:
+                join(p - 1)
+            if p + 1 < STEPS:
+                quantise_f(p + 1)
+                banks = [first_product(1, m, "message", 3) for m in (2 * p + 2, 2 * p + 3)]
+            if p < UNITS:
+                leaky_own(p)
+            if 0 <= p - 1 < UNITS:
+                quantise_h(p - 1)
+            if p < UNITS:
+                leaky_rest(p)
+            if p + 1 < STEPS:
+                for mm in range(2):
+                    leave_b(2 * p + 2 + mm, banks[mm])
+            if p % STEPS == STEPS - 2 and p // STEPS + 1 < TILES:
+                receivers(p // STEPS + 1)
+            if 0 <= s < UNITS:
+                second_half(s, 1)
+                if s % STEPS == STEPS - 1:
+                    leave_linear(s // STEPS)
+            if p < UNITS:
+                scalar_part(p, 1)
+            if 0 <= s < UNITS:
+                add_up(s, 0)
+                add_up(s, 1)

@@ -47,9 +47,9 @@ def tile_nonlocalmp_pa_t_w4_kernel(tc, F_bytes, F_scale, W1_words, W1_scales, b1
         ps = ctx.enter_context(tc.psum_pool(name="ps", bufs=1))
 
         f_src = F_bytes.rearrange("b (h m) k -> (b h) (m k)", h=2)
-        fbytes0 = const.tile([P, 2 * C], U8, align_bytes=64)
-        fbytes1 = const.tile([P, 6 * C], U8, align_bytes=64)
-        nc.sync.dma_start(out=fbytes0[:], in_=f_src[:, 0 : 2 * C])
+        fbytes0 = const.tile([P, 4 * C], U8, align_bytes=64)
+        fbytes1 = const.tile([P, 4 * C], U8, align_bytes=64)
+        nc.sync.dma_start(out=fbytes0[:], in_=f_src[:, 0 : 4 * C])
         fsc = const.tile([P, 4], F32)
         nc.sync.dma_start(out=fsc[:], in_=F_scale.rearrange("a c (p t) -> p (a c t)", t=4))
         w1raw = const.tile([P, 2, 2 * C], U8, align_bytes=64)
@@ -64,7 +64,7 @@ def tile_nonlocalmp_pa_t_w4_kernel(tc, F_bytes, F_scale, W1_words, W1_scales, b1
             nc.sync.dma_start(out=w1sraw[r:P:32, :, :].bitcast(I32), in_=w1s_src[r].bitcast(I32))
         b1raw = const.tile([P, 4], BF16)
         nc.sync.dma_start(out=b1raw[:], in_=b1.rearrange("(p t) -> p t", t=4))
-        nc.sync.dma_start(out=fbytes1[:], in_=f_src[:, 2 * C : 8 * C])
+        nc.sync.dma_start(out=fbytes1[:], in_=f_src[:, 4 * C : 8 * C])
         w2 = const.tile([P, 2 * C], U8, align_bytes=64)
         nc.sync.dma_start(out=w2[:].bitcast(I32), in_=W2_words[0].bitcast(I32))
         for r in range(4):
@@ -96,27 +96,24 @@ def tile_nonlocalmp_pa_t_w4_kernel(tc, F_bytes, F_scale, W1_words, W1_scales, b1
         bp = const.tile([P, NODES, SETS, 4], F32, align_bytes=64)
 
         def widen(m):
-            src = fbytes0[:, m * C : (m + 1) * C] if m < 2 else fbytes1[:, (m - 2) * C : (m - 1) * C]
+            src = fbytes0[:, m * C : (m + 1) * C] if m < 4 else fbytes1[:, (m - 4) * C : (m - 3) * C]
             nc.scalar.copy(out=fwide[:, m, :], in_=src.bitcast(FP8))
 
         xt_of = {}
 
-        def turn_f(q):
-            xt = ps.tile([P, 2, 2, P], F32, name="xt", tag="sum", bufs=2)
-            xt_of[q] = xt
-            for mm in range(2):
-                words = fwide[:, 2 * q + mm, :].bitcast(F32)
+        def turn_f(tiles, tag, bufs):
+            xt = ps.tile([P, len(tiles), 2, P], F32, name="xt", tag=tag, bufs=bufs)
+            for i, m in enumerate(tiles):
+                xt_of[m] = xt[:, i]
+                words = fwide[:, m, :].bitcast(F32)
                 for u in range(2):
-                    nc.tensor.transpose(xt[:, mm, u, :], words[:, u::2], ident[:])
+                    nc.tensor.transpose(xt[:, i, u, :], words[:, u::2], ident[:])
 
-        def scale_f(q):
+        def scale_f(m):
             sc = fsc[:].rearrange("p (o u e) -> p o u e", o=1, u=2).to_broadcast([P, SETS, 2, 2])
-            for mm in range(2):
-                src = xt_of[q][:, mm, :, :].bitcast(BF16).rearrange("p u (b h e) -> p h b u e", h=2, e=2)
-                for h in range(2):
-                    nc.vector.tensor_tensor(
-                        out=fg[:, 2 * q + mm, h, :, :].rearrange("p b (u e) -> p b u e", e=2), in0=src[:, h], in1=sc, op=ALU.mult
-                    )
+            src = xt_of[m].bitcast(BF16).rearrange("p u (b h e) -> p h b u e", h=2, e=2)
+            for h in range(2):
+                nc.vector.tensor_tensor(out=fg[:, m, h, :, :].rearrange("p b (u e) -> p b u e", e=2), in0=src[:, h], in1=sc, op=ALU.mult)
 
         def quantise_f(q):
             mm = slice(2 * q, 2 * q + 2)
@@ -150,6 +147,8 @@ def tile_nonlocalmp_pa_t_w4_kernel(tc, F_bytes, F_scale, W1_words, W1_scales, b1
 
         b2c = const.tile([P, CHUNKS], F32)
         b2x4 = const.tile([P, CHUNKS], F32)
+        b2x8 = const.tile([P, CHUNKS], F32)
+        b2neg = const.tile([P, CHUNKS], F32)
 
         def setup_b2():
             nc.scalar.copy(out=b2f[0:4, :], in_=b2raw[0:4, :])
@@ -157,6 +156,8 @@ def tile_nonlocalmp_pa_t_w4_kernel(tc, F_bytes, F_scale, W1_words, W1_scales, b1
             nc.tensor.transpose(bt[:], b2f[:], ident[:])
             nc.scalar.copy(out=b2c[:], in_=bt[:, 0:CHUNKS])
             nc.scalar.activation(out=b2x4[:], in_=bt[:, 0:CHUNKS], func=ACT.Copy, scale=4.0)
+            nc.scalar.activation(out=b2x8[:], in_=bt[:, 0:CHUNKS], func=ACT.Copy, scale=8.0)
+            nc.scalar.activation(out=b2neg[:], in_=bt[:, 0:CHUNKS], func=ACT.Copy, scale=-1.0)
 
         rest_of, w_of = {}, {}
         a_of, v_of, h_of, part_of, hq_of, relu_of, lin_of, sum_of, fifth_of = {}, {}, {}, {}, {}, {}, {}, {}, {}
@@ -260,11 +261,12 @@ def tile_nonlocalmp_pa_t_w4_kernel(tc, F_bytes, F_scale, W1_words, W1_scales, b1
             )
 
         def rectify(u, c, bank):
-            relu = work.tile([P, SENDERS, P], F32, name="relu", bufs=6, align_bytes=64)
+            relu = work.tile([P, SENDERS, P], F32, name="relu", bufs=10, align_bytes=64)
             relu_of[u, c] = relu
             flat = relu[:].rearrange("p j r -> p (j r)")
-            if u >= UNITS - 2 and c % 2 == 1:
-                nc.vector.tensor_scalar(out=flat, in0=bank[:], scalar1=b2c[:, c : c + 1], scalar2=0.0, op0=ALU.add, op1=ALU.max)
+            if u == UNITS - 1:
+                before = relu_of[u - 1, c][:].rearrange("p j r -> p (j r)")
+                nc.vector.scalar_tensor_tensor(out=flat, in0=bank[:], scalar=b2neg[:, c : c + 1], in1=before, op0=ALU.max, op1=ALU.add)
             else:
                 nc.scalar.activation(out=flat, in_=bank[:], func=ACT.Relu, bias=b2c[:, c : c + 1], scale=1.0)
 
@@ -273,9 +275,10 @@ def tile_nonlocalmp_pa_t_w4_kernel(tc, F_bytes, F_scale, W1_words, W1_scales, b1
             if q == 0 and c == 0:
                 total = ps.tile([P, CHUNKS, P], F32, name="total", tag="sum", bufs=2)
                 sum_of[m] = total
+                start = b2x8 if m == TILES - 1 else b2x4
                 for cc in range(CHUNKS):
                     nc.tensor.matmul(
-                        total[:, cc, :], lhsT=b2x4[:, cc : cc + 1].to_broadcast([P, P]), rhs=ident[:], is_transpose=True, start=(cc == 0), stop=False
+                        total[:, cc, :], lhsT=start[:, cc : cc + 1].to_broadcast([P, P]), rhs=ident[:], is_transpose=True, start=(cc == 0), stop=False
                     )
             for j in range(SENDERS):
                 last = q == STEPS - 1 and c == CHUNKS - 1 and j == SENDERS - 1
@@ -293,74 +296,86 @@ def tile_nonlocalmp_pa_t_w4_kernel(tc, F_bytes, F_scale, W1_words, W1_scales, b1
             nc.vector.scalar_tensor_tensor(
                 out=st[:], in0=sum_of[m][:].rearrange("p c r -> p (c r)"), scalar=1.0 - SLOPE, in1=fifth_of[m][:], op0=ALU.mult, op1=ALU.add
             )
-            for h in range(2):
-                nc.sync.dma_start(out=out_v[m, h], in_=st[SETS * h : SETS * (h + 1), :])
+            nc.sync.dma_start(out=out_v[m], in_=st[:])
 
-        def second_half(u, half):
-            for c in (2 * half, 2 * half + 1):
+        def second_product(u):
+            for c in range(CHUNKS):
                 bank = message(u, c)
                 linear(u, c)
                 rectify(u, c, bank)
 
-        widen(0)
-        widen(1)
+        nc.vector.tensor_copy(out=fwide[:, 0, :], in_=fbytes0[:, 0:C].bitcast(FP8))
+        for m in (1, 2, 3):
+            widen(m)
         permute_w1(1)
-        turn_f(0)
+        turn_f([0], "sum", 2)
+        turn_f([1], "lin", 1)
+        turn_f([2, 3], "sum", 2)
         scale_f(0)
+        scale_f(1)
         permute_w1_scales(1)
         quantise_f(0)
         permute_w1(0)
         permute_w1_scales(0)
         banks = [first_product(1, m, "message", 3) for m in range(2)]
-        receivers(0)
         for m in range(2):
             leave_b(m, banks[m])
-        for m in range(2, TILES):
+        receivers(0)
+        for m in range(4, TILES):
             widen(m)
-        turn_f(1)
         setup_b2()
 
-        for p in range(UNITS + 4):
+        last = UNITS - 1
+        for p in range(UNITS):
             s = p - 2
-            if p < UNITS:
-                add_rest(p)
-                add(p, 0)
-                add(p, 1)
-            if 0 <= s - 2 and (s - 2) % STEPS == STEPS - 1:
+            nxt = (2 * p + 2, 2 * p + 3)
+            add_rest(p)
+            add(p, 0)
+            add(p, 1)
+            if s >= 2 and (s - 2) % STEPS == STEPS - 1:
                 finish((s - 2) // STEPS)
             if p + 1 < STEPS:
-                scale_f(p + 1)
-                if p + 2 < STEPS:
-                    turn_f(p + 2)
-            if 0 <= s < UNITS:
-                second_half(s, 0)
-            if p < UNITS:
-                scalar_part(p, 0)
-            if 0 <= s - 1 < UNITS:
+                for m in nxt:
+                    scale_f(m)
+            if p + 2 < STEPS:
+                turn_f([m + 2 for m in nxt], "sum", 2)
+            if s >= 0:
+                second_product(s)
+                if s % STEPS == STEPS - 1:
+                    leave_linear(s // STEPS)
+            if p % STEPS == STEPS - 2 and p // STEPS + 1 < TILES:
+                receivers(p // STEPS + 1)
+            scalar_part(p, 0)
+            scalar_part(p, 1)
+            if s >= 1:
                 add_up(s - 1, 2)
                 add_up(s - 1, 3)
-            if 0 <= p - 1 < UNITS:
+            if s >= 0:
+                add_up(s, 0)
+                add_up(s, 1)
+            if p >= 1:
                 join(p - 1)
             if p + 1 < STEPS:
                 quantise_f(p + 1)
-                banks = [first_product(1, m, "message", 3) for m in (2 * p + 2, 2 * p + 3)]
-            if p < UNITS:
+                banks = [first_product(1, m, "message", 3) for m in nxt]
+            if p < last:
                 leaky_own(p)
-            if 0 <= p - 1 < UNITS:
+            leaky_rest(p)
+            if p >= 1:
                 quantise_h(p - 1)
-            if p < UNITS:
-                leaky_rest(p)
             if p + 1 < STEPS:
-                for mm in range(2):
-                    leave_b(2 * p + 2 + mm, banks[mm])
-            if p % STEPS == STEPS - 2 and p // STEPS + 1 < TILES:
-                receivers(p // STEPS + 1)
-            if 0 <= s < UNITS:
-                second_half(s, 1)
-                if s % STEPS == STEPS - 1:
-                    leave_linear(s // STEPS)
-            if p < UNITS:
-                scalar_part(p, 1)
-            if 0 <= s < UNITS:
-                add_up(s, 0)
-                add_up(s, 1)
+                for m, bank in zip(nxt, banks):
+                    leave_b(m, bank)
+        leaky_own(last)
+        quantise_h(last)
+        second_product(last - 1)
+        add_up(last - 2, 2)
+        add_up(last - 2, 3)
+        for c in range(CHUNKS):
+            rectify(last, c, message(last, c))
+        for j in range(SENDERS):
+            linear(last, j)
+        leave_linear(TILES - 1)
+        for c in range(CHUNKS):
+            add_up(last, c)
+        finish(TILES - 1)

@@ -35,7 +35,7 @@ def scalar_columns(u):
         return 72
     if u == UNITS - 1:
         return 0
-    return 52
+    return 44
 
 
 def tile_nonlocalmp_pa_t_w4_kernel(tc, F_bytes, F_scale, W1_words, W1_scales, b1, W2_words, W2_scales, b2, out):

@@ -29,13 +29,11 @@ OWN = 96
 
 
 def scalar_columns(u):
-    if u < 2:
-        return OWN
-    if u == 2:
-        return 72
-    if u == UNITS - 1:
+    if u < 3:
+        return 36
+    if u >= UNITS - 2:
         return 0
-    return 44
+    return 46
 
 
 def tile_nonlocalmp_pa_t_w4_kernel(tc, F_bytes, F_scale, W1_words, W1_scales, b1, W2_words, W2_scales, b2, out):
@@ -46,10 +44,10 @@ def tile_nonlocalmp_pa_t_w4_kernel(tc, F_bytes, F_scale, W1_words, W1_scales, b1
         work = ctx.enter_context(tc.tile_pool(name="work", bufs=3))
         ps = ctx.enter_context(tc.psum_pool(name="ps", bufs=1))
 
-        f_src = F_bytes.rearrange("b (h m) k -> (b h) (m k)", h=2)
+        f_src = F_bytes.rearrange("b (h m) k -> h b (m k)", h=2)
         fbytes0 = const.tile([P, 4 * C], U8, align_bytes=64)
         fbytes1 = const.tile([P, 4 * C], U8, align_bytes=64)
-        nc.sync.dma_start(out=fbytes0[:], in_=f_src[:, 0 : 4 * C])
+        nc.sync.dma_start(out=fbytes0[:], in_=f_src[:, :, 0 : 4 * C])
         fsc = const.tile([P, 4], F32)
         nc.sync.dma_start(out=fsc[:], in_=F_scale.rearrange("a c (p t) -> p (a c t)", t=4))
         w1raw = const.tile([P, 2, 2 * C], U8, align_bytes=64)
@@ -58,46 +56,55 @@ def tile_nonlocalmp_pa_t_w4_kernel(tc, F_bytes, F_scale, W1_words, W1_scales, b1
         w2s = const.tile([P, C], U8, align_bytes=64)
         nc.vector.memset(w1sraw[:].rearrange("p g n -> p (g n)").bitcast(I32), 0)
         nc.vector.memset(w2s[:].bitcast(I32), 0)
+        b2row = const.tile([P, C], BF16)
+        nc.vector.memset(b2row[:], 0.0)
         w1s_src = W1_scales.rearrange("g (q r) n -> r q g n", r=4)
         w2s_src = W2_scales.rearrange("g (q r) n -> r q (g n)", r=4)
         for r in range(4):
             nc.sync.dma_start(out=w1sraw[r:P:32, :, :].bitcast(I32), in_=w1s_src[r].bitcast(I32))
+        nc.sync.dma_start(out=fbytes1[:], in_=f_src[:, :, 4 * C : 8 * C])
         b1raw = const.tile([P, 4], BF16)
         nc.sync.dma_start(out=b1raw[:], in_=b1.rearrange("(p t) -> p t", t=4))
-        nc.sync.dma_start(out=fbytes1[:], in_=f_src[:, 4 * C : 8 * C])
         w2 = const.tile([P, 2 * C], U8, align_bytes=64)
         nc.sync.dma_start(out=w2[:].bitcast(I32), in_=W2_words[0].bitcast(I32))
         for r in range(4):
             nc.sync.dma_start(out=w2s[r:P:32, :].bitcast(I32), in_=w2s_src[r].bitcast(I32))
         b2raw = const.tile([P, P], BF16)
         nc.sync.dma_start(out=b2raw[0:4, :], in_=b2.rearrange("(c p) -> c p", p=P))
+        nc.sync.dma_start(out=b2row[0:1, :], in_=b2.rearrange("(o c) -> o c", o=1))
 
         ident = const.tile([P, P], F32)
         make_identity(nc, ident[:])
         b2f = const.tile([P, P], F32)
-        nc.gpsimd.memset(b2f[:], 0.0)
+        nc.vector.memset(b2f[:], 0.0)
+        fours = const.tile([P, P], BF16)
+        eights = const.tile([P, P], BF16)
+        nc.vector.memset(fours[:], 4.0)
+        nc.vector.memset(eights[:], 8.0)
+        ident16 = const.tile([P, P], BF16)
+        nc.scalar.copy(out=ident16[:], in_=ident[:])
+        b1wide = const.tile([P, 4, P], BF16)
 
-        w1p = const.tile([P, 2, 4, 2 * P], U8, align_bytes=64)
-        w1s = const.tile([P, 2, 4, P], U8, align_bytes=64)
+        w1p = const.tile([P, 4, 2 * P], U8, align_bytes=64)
+        w1s = const.tile([P, 4, P], U8, align_bytes=64)
 
-        def permute_w1(g):
+        def permute_w1a():
             nc.vector.tensor_copy(
-                out=w1p[:, g, :, :].rearrange("p t (m e) -> p t m e", e=2),
-                in_=w1raw[:, g, :].rearrange("p (m t e) -> p t m e", t=4, e=2),
+                out=w1p[:].rearrange("p t (m e) -> p t m e", e=2), in_=w1raw[:, 0, :].rearrange("p (m t e) -> p t m e", t=4, e=2)
             )
 
-        def permute_w1_scales(g):
-            nc.vector.tensor_copy(out=w1s[:, g, :, :], in_=w1sraw[:, g, :].rearrange("p (m t) -> p t m", t=4))
+        def permute_w1a_scales():
+            nc.vector.tensor_copy(out=w1s[:], in_=w1sraw[:, 0, :].rearrange("p (m t) -> p t m", t=4))
 
         fwide = const.tile([P, TILES, C], BF16, align_bytes=64)
-        fg = const.tile([P, TILES, 2, SETS, 4], BF16, align_bytes=64)
+        fg = const.tile([P, TILES, P, 4], BF16, align_bytes=64)
         fq = const.tile([P, TILES, P], I32, align_bytes=64)
         fs = const.tile([P, TILES, P], U8, align_bytes=64)
         bp = const.tile([P, NODES, SETS, 4], F32, align_bytes=64)
 
-        def widen(m):
+        def widen(m, copy):
             src = fbytes0[:, m * C : (m + 1) * C] if m < 4 else fbytes1[:, (m - 4) * C : (m - 3) * C]
-            nc.scalar.copy(out=fwide[:, m, :], in_=src.bitcast(FP8))
+            copy(out=fwide[:, m, :], in_=src.bitcast(FP8))
 
         xt_of = {}
 
@@ -110,60 +117,76 @@ def tile_nonlocalmp_pa_t_w4_kernel(tc, F_bytes, F_scale, W1_words, W1_scales, b1
                     nc.tensor.transpose(xt[:, i, u, :], words[:, u::2], ident[:])
 
         def scale_f(m):
-            sc = fsc[:].rearrange("p (o u e) -> p o u e", o=1, u=2).to_broadcast([P, SETS, 2, 2])
-            src = xt_of[m].bitcast(BF16).rearrange("p u (b h e) -> p h b u e", h=2, e=2)
-            for h in range(2):
-                nc.vector.tensor_tensor(out=fg[:, m, h, :, :].rearrange("p b (u e) -> p b u e", e=2), in0=src[:, h], in1=sc, op=ALU.mult)
+            nc.vector.tensor_tensor(
+                out=fg[:, m, :, :].rearrange("p r (u e) -> p r u e", e=2),
+                in0=xt_of[m].bitcast(BF16).rearrange("p u (r e) -> p r u e", e=2),
+                in1=fsc[:].rearrange("p (o u e) -> p o u e", o=1, u=2).to_broadcast([P, P, 2, 2]),
+                op=ALU.mult,
+            )
 
-        def quantise_f(q):
-            mm = slice(2 * q, 2 * q + 2)
+        def quantise_f(first, end):
+            mm = slice(first, end)
             nc.vector.quantize_mx(
                 out=fq[:, mm, :].rearrange("p m r -> p (m r)").bitcast(FP8X4),
                 scales=fs[:, mm, :].rearrange("p m r -> p (m r)"),
-                in_=fg[:, mm].rearrange("p m h b t -> p (m h b t)"),
+                in_=fg[:, mm].rearrange("p m r t -> p (m r t)"),
             )
 
-        def first_product(g, m, tag, bufs):
-            bank = ps.tile([P, 4, P], F32, name="first", tag=tag, bufs=bufs)
-            for t in range(4):
+        rows_of = {}
+
+        def sender_rows(q):
+            for m in (2 * q, 2 * q + 1):
+                bank = ps.tile([P, C], F32, name="bank", tag="message", bufs=3)
                 nc.tensor.matmul_mx(
-                    out=bank[:, t, :],
-                    lhsT=w1p[:, g, t, :].bitcast(FP4X4),
-                    lhsT_scale=w1s[:, g, t, :],
-                    rhs=fq[:, m, :].bitcast(FP8X4),
-                    rhs_scale=fs[:, m, :],
+                    out=bank[:],
+                    lhsT=fq[:, m, :].bitcast(FP8X4),
+                    lhsT_scale=fs[:, m, :],
+                    rhs=w1raw[:, 1, :].bitcast(FP4X4),
+                    rhs_scale=w1sraw[:, 1, :],
                     start=True,
                     stop=True,
                 )
-            return bank
+                rows = work.tile([P, 4, P], F32, name="rows", bufs=2, align_bytes=64)
+                rows_of[m] = rows
+                nc.scalar.copy(out=rows[:], in_=bank[:].rearrange("r (p t) -> r t p", t=4))
 
-        def leave_b(m, bank):
-            nc.vector.tensor_tensor(
-                out=bp[:, 2 * m : 2 * m + 2, :, :].rearrange("p h b t -> p (h b) t"),
-                in0=bank[:].rearrange("p t r -> p r t"),
-                in1=b1raw[:].unsqueeze(1).to_broadcast([P, P, 4]),
-                op=ALU.add,
-            )
+        def sender_columns(q):
+            for m in (2 * q, 2 * q + 1):
+                bank = ps.tile([P, 4, P], F32, name="bank", tag="message", bufs=3)
+                flat = bank[:].rearrange("p t r -> p (t r)")
+                nc.tensor.matmul(flat, lhsT=ident16[:], rhs=b1wide[:].rearrange("p t r -> p (t r)"), start=True, stop=False)
+                for t in range(4):
+                    nc.tensor.matmul(bank[:, t, :], lhsT=rows_of[m][:, t, :], rhs=ident[:], is_transpose=True, start=False, stop=(t == 3))
+                nc.scalar.copy(out=bp[:, 2 * m : 2 * m + 2, :, :].rearrange("p h b t -> p (h b) t"), in_=bank[:].rearrange("p t r -> p r t"))
 
         b2c = const.tile([P, CHUNKS], F32)
-        b2x4 = const.tile([P, CHUNKS], F32)
-        b2x8 = const.tile([P, CHUNKS], F32)
         b2neg = const.tile([P, CHUNKS], F32)
 
         def setup_b2():
             nc.scalar.copy(out=b2f[0:4, :], in_=b2raw[0:4, :])
-            bt = ps.tile([P, P], F32, name="bt", tag="lin")
+            bt = ps.tile([P, P], F32, name="bt", tag="lin", bufs=2)
             nc.tensor.transpose(bt[:], b2f[:], ident[:])
             nc.scalar.copy(out=b2c[:], in_=bt[:, 0:CHUNKS])
-            nc.scalar.activation(out=b2x4[:], in_=bt[:, 0:CHUNKS], func=ACT.Copy, scale=4.0)
-            nc.scalar.activation(out=b2x8[:], in_=bt[:, 0:CHUNKS], func=ACT.Copy, scale=8.0)
             nc.scalar.activation(out=b2neg[:], in_=bt[:, 0:CHUNKS], func=ACT.Copy, scale=-1.0)
 
         rest_of, w_of = {}, {}
         a_of, v_of, h_of, part_of, hq_of, relu_of, lin_of, sum_of, fifth_of = {}, {}, {}, {}, {}, {}, {}, {}, {}
 
         def receivers(m):
-            a_of[m] = first_product(0, m, "a", 2)
+            bank = ps.tile([P, 4, P], F32, name="bank", tag="a", bufs=1)
+            a_of[m] = bank
+            for t in range(4):
+                nc.tensor.matmul_mx(
+                    out=bank[:, t, :],
+                    lhsT=w1p[:, t, :].bitcast(FP4X4),
+                    lhsT_scale=w1s[:, t, :],
+                    rhs=fq[:, m, :].bitcast(FP8X4),
+                    rhs_scale=fs[:, m, :],
+                    start=True,
+                    stop=True,
+                )
+
+        def receivers_rest(m):
             rest = work.tile([P, P - OWN, 4], F32, name="rest", bufs=2, align_bytes=64)
             rest_of[m] = rest
             nc.scalar.copy(out=rest[:], in_=a_of[m][:].rearrange("p t r -> p r t")[:, OWN:, :])
@@ -248,7 +271,7 @@ def tile_nonlocalmp_pa_t_w4_kernel(tc, F_bytes, F_scale, W1_words, W1_scales, b1
             m, q = divmod(u, STEPS)
             hq, hs = hq_of[u]
             if q == 0 and j == 0:
-                lin = ps.tile([P, C], F32, name="lin", tag="lin")
+                lin = ps.tile([P, C], F32, name="lin", tag="lin", bufs=2)
                 lin_of[m] = lin
             nc.tensor.matmul_mx(
                 out=lin_of[m][:],
@@ -275,11 +298,8 @@ def tile_nonlocalmp_pa_t_w4_kernel(tc, F_bytes, F_scale, W1_words, W1_scales, b1
             if q == 0 and c == 0:
                 total = ps.tile([P, CHUNKS, P], F32, name="total", tag="sum", bufs=2)
                 sum_of[m] = total
-                start = b2x8 if m == TILES - 1 else b2x4
-                for cc in range(CHUNKS):
-                    nc.tensor.matmul(
-                        total[:, cc, :], lhsT=start[:, cc : cc + 1].to_broadcast([P, P]), rhs=ident[:], is_transpose=True, start=(cc == 0), stop=False
-                    )
+                times = eights if m == TILES - 1 else fours
+                nc.tensor.matmul(total[:].rearrange("p c r -> p (c r)"), lhsT=times[:], rhs=b2row[:], start=True, stop=False)
             for j in range(SENDERS):
                 last = q == STEPS - 1 and c == CHUNKS - 1 and j == SENDERS - 1
                 nc.tensor.matmul(sum_of[m][:, c, :], lhsT=relu_of[u, c][:, j, :], rhs=ident[:], is_transpose=True, start=False, stop=last)
@@ -299,78 +319,86 @@ def tile_nonlocalmp_pa_t_w4_kernel(tc, F_bytes, F_scale, W1_words, W1_scales, b1
             nc.sync.dma_start(out=out_v[m], in_=st[:])
 
         def second_product(u):
-            for c in range(CHUNKS):
-                bank = message(u, c)
-                linear(u, c)
-                rectify(u, c, bank)
+            rectify(u, 0, message(u, 0))
+            linear(u, 0)
+            rectify(u, 1, message(u, 1))
+            rectify(u, 2, message(u, 2))
+            linear(u, 1)
+            rectify(u, 3, message(u, 3))
 
-        nc.vector.tensor_copy(out=fwide[:, 0, :], in_=fbytes0[:, 0:C].bitcast(FP8))
-        for m in (1, 2, 3):
-            widen(m)
-        permute_w1(1)
+        widen(0, nc.vector.tensor_copy)
+        for m in range(1, TILES - 1):
+            widen(m, nc.scalar.copy)
+        nc.scalar.copy(out=b1wide[:], in_=b1raw[:].unsqueeze(2).to_broadcast([P, 4, P]))
         turn_f([0], "sum", 2)
-        turn_f([1], "lin", 1)
+        turn_f([1], "lin", 2)
         turn_f([2, 3], "sum", 2)
+        permute_w1a()
         scale_f(0)
         scale_f(1)
-        permute_w1_scales(1)
-        quantise_f(0)
-        permute_w1(0)
-        permute_w1_scales(0)
-        banks = [first_product(1, m, "message", 3) for m in range(2)]
-        for m in range(2):
-            leave_b(m, banks[m])
+        permute_w1a_scales()
+        quantise_f(0, 2)
+        scale_f(2)
+        scale_f(3)
+        turn_f([4, 5], "sum", 2)
+        sender_rows(0)
         receivers(0)
+        widen(TILES - 1, nc.vector.tensor_copy)
+        quantise_f(2, 4)
+        sender_columns(0)
+        receivers_rest(0)
+        turn_f([6, 7], "lin", 2)
+        sender_rows(1)
+        sender_columns(1)
         for m in range(4, TILES):
-            widen(m)
+            scale_f(m)
         setup_b2()
 
         last = UNITS - 1
         for p in range(UNITS):
             s = p - 2
-            nxt = (2 * p + 2, 2 * p + 3)
             add_rest(p)
             add(p, 0)
             add(p, 1)
-            if s >= 2 and (s - 2) % STEPS == STEPS - 1:
+            if s >= 2 and (s - 2) % STEPS == STEPS - 1 and p < last:
                 finish((s - 2) // STEPS)
-            if p + 1 < STEPS:
-                for m in nxt:
-                    scale_f(m)
-            if p + 2 < STEPS:
-                turn_f([m + 2 for m in nxt], "sum", 2)
+            if p == 0:
+                quantise_f(4, TILES)
             if s >= 0:
                 second_product(s)
-                if s % STEPS == STEPS - 1:
-                    leave_linear(s // STEPS)
-            if p % STEPS == STEPS - 2 and p // STEPS + 1 < TILES:
+            if s > 0 and s % STEPS == 0:
+                leave_linear(s // STEPS - 1)
+            if p % STEPS == STEPS - 1 and p // STEPS + 1 < TILES:
                 receivers(p // STEPS + 1)
+                receivers_rest(p // STEPS + 1)
             scalar_part(p, 0)
             scalar_part(p, 1)
+            if p + 2 < STEPS:
+                sender_rows(p + 2)
+                sender_columns(p + 2)
             if s >= 1:
                 add_up(s - 1, 2)
                 add_up(s - 1, 3)
             if s >= 0:
                 add_up(s, 0)
                 add_up(s, 1)
+                linear(s, 2)
+                linear(s, 3)
             if p >= 1:
                 join(p - 1)
-            if p + 1 < STEPS:
-                quantise_f(p + 1)
-                banks = [first_product(1, m, "message", 3) for m in nxt]
-            if p < last:
-                leaky_own(p)
-            leaky_rest(p)
-            if p >= 1:
+            if p == last:
                 quantise_h(p - 1)
-            if p + 1 < STEPS:
-                for m, bank in zip(nxt, banks):
-                    leave_b(m, bank)
-        leaky_own(last)
+            leaky_own(p)
+            leaky_rest(p)
+            if 1 <= p < last:
+                quantise_h(p - 1)
+        finish(TILES - 2)
         quantise_h(last)
         second_product(last - 1)
         add_up(last - 2, 2)
         add_up(last - 2, 3)
+        linear(last - 1, 2)
+        linear(last - 1, 3)
         for c in range(CHUNKS):
             rectify(last, c, message(last, c))
         for j in range(SENDERS):

@@ -44,10 +44,10 @@ def tile_nonlocalmp_pa_t_w4_kernel(tc, F_bytes, F_scale, W1_words, W1_scales, b1
         work = ctx.enter_context(tc.tile_pool(name="work", bufs=3))
         ps = ctx.enter_context(tc.psum_pool(name="ps", bufs=1))
 
-        f_src = F_bytes.rearrange("b (h m) k -> h b (m k)", h=2)
+        f_src = F_bytes.rearrange("b (h m) k -> (b h) (m k)", h=2)
         fbytes0 = const.tile([P, 4 * C], U8, align_bytes=64)
         fbytes1 = const.tile([P, 4 * C], U8, align_bytes=64)
-        nc.sync.dma_start(out=fbytes0[:], in_=f_src[:, :, 0 : 4 * C])
+        nc.sync.dma_start(out=fbytes0[:], in_=f_src[:, 0 : 4 * C])
         fsc = const.tile([P, 4], F32)
         nc.sync.dma_start(out=fsc[:], in_=F_scale.rearrange("a c (p t) -> p (a c t)", t=4))
         w1raw = const.tile([P, 2, 2 * C], U8, align_bytes=64)
@@ -62,7 +62,7 @@ def tile_nonlocalmp_pa_t_w4_kernel(tc, F_bytes, F_scale, W1_words, W1_scales, b1
         w2s_src = W2_scales.rearrange("g (q r) n -> r q (g n)", r=4)
         for r in range(4):
             nc.sync.dma_start(out=w1sraw[r:P:32, :, :].bitcast(I32), in_=w1s_src[r].bitcast(I32))
-        nc.sync.dma_start(out=fbytes1[:], in_=f_src[:, :, 4 * C : 8 * C])
+        nc.sync.dma_start(out=fbytes1[:], in_=f_src[:, 4 * C : 8 * C])
         b1raw = const.tile([P, 4], BF16)
         nc.sync.dma_start(out=b1raw[:], in_=b1.rearrange("(p t) -> p t", t=4))
         w2 = const.tile([P, 2 * C], U8, align_bytes=64)
@@ -117,12 +117,11 @@ def tile_nonlocalmp_pa_t_w4_kernel(tc, F_bytes, F_scale, W1_words, W1_scales, b1
                     nc.tensor.transpose(xt[:, i, u, :], words[:, u::2], ident[:])
 
         def scale_f(m):
-            nc.vector.tensor_tensor(
-                out=fg[:, m, :, :].rearrange("p r (u e) -> p r u e", e=2),
-                in0=xt_of[m].bitcast(BF16).rearrange("p u (r e) -> p r u e", e=2),
-                in1=fsc[:].rearrange("p (o u e) -> p o u e", o=1, u=2).to_broadcast([P, P, 2, 2]),
-                op=ALU.mult,
-            )
+            sc = fsc[:].rearrange("p (o u e) -> p o u e", o=1, u=2).to_broadcast([P, SETS, 2, 2])
+            src = xt_of[m].bitcast(BF16).rearrange("p u (b h e) -> p h b u e", h=2, e=2)
+            for h in range(2):
+                to = fg[:, m, SETS * h : SETS * (h + 1), :].rearrange("p b (u e) -> p b u e", e=2)
+                nc.vector.tensor_tensor(out=to, in0=src[:, h], in1=sc, op=ALU.mult)
 
         def quantise_f(first, end):
             mm = slice(first, end)
@@ -316,7 +315,8 @@ def tile_nonlocalmp_pa_t_w4_kernel(tc, F_bytes, F_scale, W1_words, W1_scales, b1
             nc.vector.scalar_tensor_tensor(
                 out=st[:], in0=sum_of[m][:].rearrange("p c r -> p (c r)"), scalar=1.0 - SLOPE, in1=fifth_of[m][:], op0=ALU.mult, op1=ALU.add
             )
-            nc.sync.dma_start(out=out_v[m], in_=st[:])
+            for h in range(2):
+                nc.sync.dma_start(out=out_v[m, h], in_=st[SETS * h : SETS * (h + 1), :])
 
         def second_product(u):
             rectify(u, 0, message(u, 0))

@@ -25,7 +25,8 @@ UNITS = TILES * STEPS
 CHUNKS = C // P
 
 
-OWN = 96
+SHARE = 38
+MOST = 44
 
 
 def scalar_columns(u):
@@ -33,7 +34,7 @@ def scalar_columns(u):
         return 36
     if u >= UNITS - 2:
         return 0
-    return 46
+    return MOST
 
 
 def tile_nonlocalmp_pa_t_w4_kernel(tc, F_bytes, F_scale, W1_words, W1_scales, b1, W2_words, W2_scales, b2, out):
@@ -168,8 +169,7 @@ def tile_nonlocalmp_pa_t_w4_kernel(tc, F_bytes, F_scale, W1_words, W1_scales, b1
             nc.scalar.copy(out=b2c[:], in_=bt[:, 0:CHUNKS])
             nc.scalar.activation(out=b2neg[:], in_=bt[:, 0:CHUNKS], func=ACT.Copy, scale=-1.0)
 
-        rest_of, w_of = {}, {}
-        a_of, v_of, h_of, part_of, hq_of, relu_of, lin_of, sum_of, fifth_of = {}, {}, {}, {}, {}, {}, {}, {}, {}
+        a_of, rest_of, h_of, part_of, hq_of, relu_of, lin_of, sum_of, fifth_of = {}, {}, {}, {}, {}, {}, {}, {}, {}
 
         def receivers(m):
             bank = ps.tile([P, 4, P], F32, name="bank", tag="a", bufs=1)
@@ -186,32 +186,40 @@ def tile_nonlocalmp_pa_t_w4_kernel(tc, F_bytes, F_scale, W1_words, W1_scales, b1
                 )
 
         def receivers_rest(m):
-            rest = work.tile([P, P - OWN, 4], F32, name="rest", bufs=2, align_bytes=64)
+            rest = work.tile([P, 2, SHARE, 4], F32, name="rest", bufs=2, align_bytes=64)
             rest_of[m] = rest
-            nc.scalar.copy(out=rest[:], in_=a_of[m][:].rearrange("p t r -> p r t")[:, OWN:, :])
+            nc.scalar.copy(out=rest[:], in_=a_of[m][:].rearrange("p t (h b) -> p h b t", h=2)[:, :, SETS - SHARE :, :])
 
-        def add(u, h):
+        v_all = const.tile([P, SENDERS, P + MOST, 4], F32, align_bytes=64)
+
+        def v_of(u):
+            first = MOST * (u % 2)
+            return v_all[:, :, first : first + P, :]
+
+        def by_scalar(u):
+            x = scalar_columns(u)
+            return slice(0, x) if u % 2 == 0 else slice(P - x, P)
+
+        def by_vector(u):
+            x = scalar_columns(u)
+            return slice(x, P) if u % 2 == 0 else slice(0, P - x)
+
+        def add(u, h, n):
             m, q = divmod(u, STEPS)
-            if u not in v_of:
-                v = work.tile([P, SENDERS, OWN, 4], F32, name="v", align_bytes=64)
-                v_of[u] = v
-            cols = slice(SETS * h, min(SETS * (h + 1), OWN))
-            n = cols.stop - cols.start
+            cols = slice(SETS * h, SETS * h + n)
             nc.vector.tensor_tensor(
-                out=v_of[u][:, :, cols, :],
+                out=v_of(u)[:, :, cols, :],
                 in0=a_of[m][:].rearrange("p t r -> p r t")[:, cols, :].unsqueeze(1).to_broadcast([P, SENDERS, n, 4]),
                 in1=bp[:, SENDERS * q : SENDERS * (q + 1), 0:n, :],
                 op=ALU.add,
             )
 
-        def add_rest(u):
+        def add_rest(u, h):
             m, q = divmod(u, STEPS)
-            w = work.tile([P, SENDERS, P - OWN, 4], F32, name="w", bufs=1, align_bytes=64)
-            w_of[u] = w
             nc.gpsimd.tensor_tensor(
-                out=w[:],
-                in0=rest_of[m][:].unsqueeze(1).to_broadcast([P, SENDERS, P - OWN, 4]),
-                in1=bp[:, SENDERS * q : SENDERS * (q + 1), OWN - SETS :, :],
+                out=v_of(u)[:, :, SETS * (h + 1) - SHARE : SETS * (h + 1), :],
+                in0=rest_of[m][:, h].unsqueeze(1).to_broadcast([P, SENDERS, SHARE, 4]),
+                in1=bp[:, SENDERS * q : SENDERS * (q + 1), SETS - SHARE :, :],
                 op=ALU.add,
             )
 
@@ -221,7 +229,7 @@ def tile_nonlocalmp_pa_t_w4_kernel(tc, F_bytes, F_scale, W1_words, W1_scales, b1
                 return
             part = work.tile([P, SENDERS, x, 4], BF16, name="part", bufs=4, align_bytes=64)
             part_of[u, sign] = part
-            nc.scalar.activation(out=part[:], in_=v_of[u][:, :, 0:x, :], func=ACT.Relu, scale=(1.0, -SLOPE)[sign])
+            nc.scalar.activation(out=part[:], in_=v_of(u)[:, :, by_scalar(u), :], func=ACT.Relu, scale=(1.0, -SLOPE)[sign])
 
         def h_tile(u):
             if u not in h_of:
@@ -229,22 +237,14 @@ def tile_nonlocalmp_pa_t_w4_kernel(tc, F_bytes, F_scale, W1_words, W1_scales, b1
                 h_of[u] = h
             return h_of[u]
 
-        def leaky(to, src):
-            src = src.rearrange("p j r t -> p j (r t)")
-            nc.vector.scalar_tensor_tensor(out=to.rearrange("p j r t -> p j (r t)"), in0=src, scalar=SLOPE, in1=src, op0=ALU.mult, op1=ALU.max)
-
-        def leaky_own(u):
-            x = scalar_columns(u)
-            if x < OWN:
-                leaky(h_tile(u)[:, :, x:OWN, :], v_of[u][:, :, x:, :])
-
-        def leaky_rest(u):
-            leaky(h_tile(u)[:, :, OWN:, :], w_of[u][:])
+        def leaky(u):
+            src = v_of(u)[:, :, by_vector(u), :].rearrange("p j r t -> p j (r t)")
+            to = h_tile(u)[:, :, by_vector(u), :].rearrange("p j r t -> p j (r t)")
+            nc.vector.scalar_tensor_tensor(out=to, in0=src, scalar=SLOPE, in1=src, op0=ALU.mult, op1=ALU.max)
 
         def join(u):
-            x = scalar_columns(u)
-            if x > 0:
-                nc.vector.tensor_tensor(out=h_tile(u)[:, :, 0:x, :], in0=part_of[u, 0][:], in1=part_of[u, 1][:], op=ALU.subtract)
+            if scalar_columns(u) > 0:
+                nc.vector.tensor_tensor(out=h_tile(u)[:, :, by_scalar(u), :], in0=part_of[u, 0][:], in1=part_of[u, 1][:], op=ALU.subtract)
 
         def quantise_h(u):
             hq = work.tile([P, SENDERS * P], I32, name="hq", align_bytes=64)
@@ -357,9 +357,9 @@ def tile_nonlocalmp_pa_t_w4_kernel(tc, F_bytes, F_scale, W1_words, W1_scales, b1
         last = UNITS - 1
         for p in range(UNITS):
             s = p - 2
-            add_rest(p)
-            add(p, 0)
-            add(p, 1)
+            add_rest(p, 1 - p % 2)
+            add(p, p % 2, SETS)
+            add(p, 1 - p % 2, SETS - SHARE)
             if s >= 2 and (s - 2) % STEPS == STEPS - 1 and p < last:
                 finish((s - 2) // STEPS)
             if p == 0:
@@ -388,8 +388,7 @@ def tile_nonlocalmp_pa_t_w4_kernel(tc, F_bytes, F_scale, W1_words, W1_scales, b1
                 join(p - 1)
             if p == last:
                 quantise_h(p - 1)
-            leaky_own(p)
-            leaky_rest(p)
+            leaky(p)
             if 1 <= p < last:
                 quantise_h(p - 1)
         finish(TILES - 2)

@@ -25,13 +25,13 @@ UNITS = TILES * STEPS
 CHUNKS = C // P
 
 
-SHARE = 38
-MOST = 44
+SHARE = 36
+MOST = 46
 
 
 def scalar_columns(u):
     if u < 3:
-        return 36
+        return 30
     if u >= UNITS - 2:
         return 0
     return MOST
@@ -79,9 +79,9 @@ def tile_nonlocalmp_pa_t_w4_kernel(tc, F_bytes, F_scale, W1_words, W1_scales, b1
         b2f = const.tile([P, P], F32)
         nc.vector.memset(b2f[:], 0.0)
         fours = const.tile([P, P], BF16)
-        eights = const.tile([P, P], BF16)
         nc.vector.memset(fours[:], 4.0)
-        nc.vector.memset(eights[:], 8.0)
+        twelves = const.tile([P, P], BF16)
+        nc.vector.memset(twelves[:], 12.0)
         ident16 = const.tile([P, P], BF16)
         nc.scalar.copy(out=ident16[:], in_=ident[:])
         b1wide = const.tile([P, 4, P], BF16)
@@ -162,14 +162,20 @@ def tile_nonlocalmp_pa_t_w4_kernel(tc, F_bytes, F_scale, W1_words, W1_scales, b1
         b2c = const.tile([P, CHUNKS], F32)
         b2neg = const.tile([P, CHUNKS], F32)
 
-        def setup_b2():
+        b2_bank = []
+
+        def turn_b2():
             nc.scalar.copy(out=b2f[0:4, :], in_=b2raw[0:4, :])
             bt = ps.tile([P, P], F32, name="bt", tag="lin", bufs=2)
             nc.tensor.transpose(bt[:], b2f[:], ident[:])
+            b2_bank.append(bt)
+
+        def leave_b2():
+            bt = b2_bank[0]
             nc.scalar.copy(out=b2c[:], in_=bt[:, 0:CHUNKS])
             nc.scalar.activation(out=b2neg[:], in_=bt[:, 0:CHUNKS], func=ACT.Copy, scale=-1.0)
 
-        a_of, rest_of, h_of, part_of, hq_of, relu_of, lin_of, sum_of, fifth_of = {}, {}, {}, {}, {}, {}, {}, {}, {}
+        a_of, rest_of, h_of, part_of, hq_of, relu_of, lin_of, sum_of, bank_of, fifth_of = {}, {}, {}, {}, {}, {}, {}, {}, {}, {}
 
         def receivers(m):
             bank = ps.tile([P, 4, P], F32, name="bank", tag="a", bufs=1)
@@ -252,9 +258,9 @@ def tile_nonlocalmp_pa_t_w4_kernel(tc, F_bytes, F_scale, W1_words, W1_scales, b1
             hq_of[u] = (hq, hs)
             nc.vector.quantize_mx(out=hq[:].bitcast(FP8X4), scales=hs[:], in_=h_of[u][:].rearrange("p j r t -> p (j r t)"))
 
-        def message(u, c):
+        def message(u, c, tag="message", bufs=3):
             hq, hs = hq_of[u]
-            bank = ps.tile([P, SENDERS * P], F32, name="bank", tag="message", bufs=3)
+            bank = ps.tile([P, SENDERS * P], F32, name="bank", tag=tag, bufs=bufs)
             nc.tensor.matmul_mx(
                 out=bank[:],
                 lhsT=w2[:, 2 * P * c : 2 * P * (c + 1)].bitcast(FP4X4),
@@ -286,22 +292,31 @@ def tile_nonlocalmp_pa_t_w4_kernel(tc, F_bytes, F_scale, W1_words, W1_scales, b1
             relu = work.tile([P, SENDERS, P], F32, name="relu", bufs=10, align_bytes=64)
             relu_of[u, c] = relu
             flat = relu[:].rearrange("p j r -> p (j r)")
-            if u == UNITS - 1:
+            if u >= UNITS - 2:
                 before = relu_of[u - 1, c][:].rearrange("p j r -> p (j r)")
                 nc.vector.scalar_tensor_tensor(out=flat, in0=bank[:], scalar=b2neg[:, c : c + 1], in1=before, op0=ALU.max, op1=ALU.add)
             else:
                 nc.scalar.activation(out=flat, in_=bank[:], func=ACT.Relu, bias=b2c[:, c : c + 1], scale=1.0)
 
+        def open_sum(m, chunks, tag):
+            total = ps.tile([P, len(chunks), P], F32, name="total", tag=tag, bufs=2)
+            for i, c in enumerate(chunks):
+                sum_of[m, c] = total[:, i, :]
+            bank_of[m, chunks[0]] = total
+            times = fours if m < TILES - 1 else twelves
+            row = b2row[:, P * chunks[0] : P * (chunks[-1] + 1)]
+            nc.tensor.matmul(total[:].rearrange("p c r -> p (c r)"), lhsT=times[:], rhs=row, start=True, stop=False)
+
         def add_up(u, c):
             m, q = divmod(u, STEPS)
+            halves = m == TILES - 1
             if q == 0 and c == 0:
-                total = ps.tile([P, CHUNKS, P], F32, name="total", tag="sum", bufs=2)
-                sum_of[m] = total
-                times = eights if m == TILES - 1 else fours
-                nc.tensor.matmul(total[:].rearrange("p c r -> p (c r)"), lhsT=times[:], rhs=b2row[:], start=True, stop=False)
+                open_sum(m, (0, 1) if halves else (0, 1, 2, 3), "sum")
+            if q == 0 and c == 2 and halves:
+                open_sum(m, (2, 3), "lin")
             for j in range(SENDERS):
-                last = q == STEPS - 1 and c == CHUNKS - 1 and j == SENDERS - 1
-                nc.tensor.matmul(sum_of[m][:, c, :], lhsT=relu_of[u, c][:, j, :], rhs=ident[:], is_transpose=True, start=False, stop=last)
+                last = q == STEPS - 1 and j == SENDERS - 1 and (c == 3 or (c == 1 and halves))
+                nc.tensor.matmul(sum_of[m, c], lhsT=relu_of[u, c][:, j, :], rhs=ident[:], is_transpose=True, start=False, stop=last)
 
         def leave_linear(m):
             fifth = work.tile([P, C], F32, name="fifth", bufs=2)
@@ -310,13 +325,19 @@ def tile_nonlocalmp_pa_t_w4_kernel(tc, F_bytes, F_scale, W1_words, W1_scales, b1
 
         out_v = out.rearrange("b (h m) c -> m h b c", h=2)
 
-        def finish(m):
-            st = work.tile([P, C], F32, name="st", bufs=2)
+        def finish(m, first, end, queues):
+            cols = slice(P * first, P * end)
+            st = work.tile([P, P * (end - first)], F32, name="st", bufs=2)
             nc.vector.scalar_tensor_tensor(
-                out=st[:], in0=sum_of[m][:].rearrange("p c r -> p (c r)"), scalar=1.0 - SLOPE, in1=fifth_of[m][:], op0=ALU.mult, op1=ALU.add
+                out=st[:],
+                in0=bank_of[m, first][:].rearrange("p c r -> p (c r)"),
+                scalar=1.0 - SLOPE,
+                in1=fifth_of[m][:, cols],
+                op0=ALU.mult,
+                op1=ALU.add,
             )
             for h in range(2):
-                nc.sync.dma_start(out=out_v[m, h], in_=st[SETS * h : SETS * (h + 1), :])
+                queues[h].dma_start(out=out_v[m, h][:, cols], in_=st[SETS * h : SETS * (h + 1), :])
 
         def second_product(u):
             rectify(u, 0, message(u, 0))
@@ -345,14 +366,14 @@ def tile_nonlocalmp_pa_t_w4_kernel(tc, F_bytes, F_scale, W1_words, W1_scales, b1
         receivers(0)
         widen(TILES - 1, nc.vector.tensor_copy)
         quantise_f(2, 4)
-        sender_columns(0)
         receivers_rest(0)
+        sender_columns(0)
         turn_f([6, 7], "lin", 2)
         sender_rows(1)
         sender_columns(1)
-        for m in range(4, TILES):
-            scale_f(m)
-        setup_b2()
+        scale_f(4)
+        scale_f(5)
+        quantise_f(4, 6)
 
         last = UNITS - 1
         for p in range(UNITS):
@@ -361,9 +382,10 @@ def tile_nonlocalmp_pa_t_w4_kernel(tc, F_bytes, F_scale, W1_words, W1_scales, b1
             add(p, p % 2, SETS)
             add(p, 1 - p % 2, SETS - SHARE)
             if s >= 2 and (s - 2) % STEPS == STEPS - 1 and p < last:
-                finish((s - 2) // STEPS)
+                finish((s - 2) // STEPS, 0, CHUNKS, (nc.sync, nc.sync))
             if p == 0:
-                quantise_f(4, TILES)
+                scale_f(6)
+                scale_f(7)
             if s >= 0:
                 second_product(s)
             if s > 0 and s % STEPS == 0:
@@ -371,17 +393,23 @@ def tile_nonlocalmp_pa_t_w4_kernel(tc, F_bytes, F_scale, W1_words, W1_scales, b1
             if p % STEPS == STEPS - 1 and p // STEPS + 1 < TILES:
                 receivers(p // STEPS + 1)
                 receivers_rest(p // STEPS + 1)
-            scalar_part(p, 0)
-            scalar_part(p, 1)
             if p + 2 < STEPS:
                 sender_rows(p + 2)
+            scalar_part(p, 0)
+            if p + 2 < STEPS:
                 sender_columns(p + 2)
+            if p == 0:
+                turn_b2()
+            scalar_part(p, 1)
+            if p == 0:
+                leave_b2()
             if s >= 1:
                 add_up(s - 1, 2)
                 add_up(s - 1, 3)
             if s >= 0:
-                add_up(s, 0)
-                add_up(s, 1)
+                if p < last:
+                    add_up(s, 0)
+                    add_up(s, 1)
                 linear(s, 2)
                 linear(s, 3)
             if p >= 1:
@@ -389,20 +417,23 @@ def tile_nonlocalmp_pa_t_w4_kernel(tc, F_bytes, F_scale, W1_words, W1_scales, b1
             if p == last:
                 quantise_h(p - 1)
             leaky(p)
+            if p == 0:
+                quantise_f(6, TILES)
             if 1 <= p < last:
                 quantise_h(p - 1)
-        finish(TILES - 2)
+        finish(TILES - 2, 0, CHUNKS, (nc.sync, nc.sync))
         quantise_h(last)
-        second_product(last - 1)
-        add_up(last - 2, 2)
-        add_up(last - 2, 3)
-        linear(last - 1, 2)
-        linear(last - 1, 3)
-        for c in range(CHUNKS):
-            rectify(last, c, message(last, c))
+        for c in range(3):
+            rectify(last - 1, c, message(last - 1, c))
+        rectify(last - 1, 3, message(last - 1, 3, "a", 1))
+        for j in range(SENDERS):
+            linear(last - 1, j)
         for j in range(SENDERS):
             linear(last, j)
         leave_linear(TILES - 1)
         for c in range(CHUNKS):
+            rectify(last, c, message(last, c))
+        for c in range(CHUNKS):
             add_up(last, c)
-        finish(TILES - 1)
+            if c % 2 == 1:
+                finish(TILES - 1, c - 1, c + 1, (nc.sync, nc.scalar))

@@ -55,10 +55,12 @@ def tile_nonlocalmp_pa_t_w4_kernel(tc, F_bytes, F_scale, W1_words, W1_scales, b1
         nc.sync.dma_start(out=w1raw[:].bitcast(I32), in_=W1_words.rearrange("g p n -> p g n").bitcast(I32))
         w1sraw = const.tile([P, 2, C], U8, align_bytes=64)
         w2s = const.tile([P, C], U8, align_bytes=64)
-        nc.vector.memset(w1sraw[:].rearrange("p g n -> p (g n)").bitcast(I32), 0)
-        nc.vector.memset(w2s[:].bitcast(I32), 0)
+        fours = const.tile([P, P], BF16)
         b2row = const.tile([P, C], BF16)
+        nc.vector.memset(w1sraw[:].rearrange("p g n -> p (g n)").bitcast(I32), 0)
+        nc.vector.memset(fours[:], 4.0)
         nc.vector.memset(b2row[:], 0.0)
+        nc.vector.memset(w2s[:].bitcast(I32), 0)
         w1s_src = W1_scales.rearrange("g (q r) n -> r q g n", r=4)
         w2s_src = W2_scales.rearrange("g (q r) n -> r q (g n)", r=4)
         for r in range(4):
@@ -72,14 +74,11 @@ def tile_nonlocalmp_pa_t_w4_kernel(tc, F_bytes, F_scale, W1_words, W1_scales, b1
             nc.sync.dma_start(out=w2s[r:P:32, :].bitcast(I32), in_=w2s_src[r].bitcast(I32))
         b2raw = const.tile([P, P], BF16)
         nc.sync.dma_start(out=b2raw[0:4, :], in_=b2.rearrange("(c p) -> c p", p=P))
-        nc.sync.dma_start(out=b2row[0:1, :], in_=b2.rearrange("(o c) -> o c", o=1))
 
         ident = const.tile([P, P], F32)
         make_identity(nc, ident[:])
         b2f = const.tile([P, P], F32)
         nc.vector.memset(b2f[:], 0.0)
-        fours = const.tile([P, P], BF16)
-        nc.vector.memset(fours[:], 4.0)
         twelves = const.tile([P, P], BF16)
         nc.vector.memset(twelves[:], 12.0)
         ident16 = const.tile([P, P], BF16)
@@ -347,13 +346,22 @@ def tile_nonlocalmp_pa_t_w4_kernel(tc, F_bytes, F_scale, W1_words, W1_scales, b1
             linear(u, 1)
             rectify(u, 3, message(u, 3))
 
+        def warm_up(n):
+            idle = ps.tile([P, C], F32, name="idle", tag="message", bufs=3)
+            for i in range(n):
+                nc.tensor.matmul(idle[:], lhsT=fours[:], rhs=b2row[:], start=True, stop=True)
+
+        warm_up(4)
         widen(0, nc.vector.tensor_copy)
         for m in range(1, TILES - 1):
             widen(m, nc.scalar.copy)
         nc.scalar.copy(out=b1wide[:], in_=b1raw[:].unsqueeze(2).to_broadcast([P, 4, P]))
         turn_f([0], "sum", 2)
         turn_f([1], "lin", 2)
+        warm_up(2)
         turn_f([2, 3], "sum", 2)
+        warm_up(2)
+        nc.sync.dma_start(out=b2row[0:1, :], in_=b2.rearrange("(o c) -> o c", o=1))
         permute_w1a()
         scale_f(0)
         scale_f(1)

@@ -25,8 +25,9 @@ UNITS = TILES * STEPS
 CHUNKS = C // P
 
 
+WIDE = 46
 SHARE = 36
-MOST = 46
+MOST = 44
 
 
 def scalar_columns(u):
@@ -191,9 +192,9 @@ def tile_nonlocalmp_pa_t_w4_kernel(tc, F_bytes, F_scale, W1_words, W1_scales, b1
                 )
 
         def receivers_rest(m):
-            rest = work.tile([P, 2, SHARE, 4], F32, name="rest", bufs=2, align_bytes=64)
+            rest = work.tile([P, 2, WIDE, 4], F32, name="rest", bufs=2, align_bytes=64)
             rest_of[m] = rest
-            nc.scalar.copy(out=rest[:], in_=a_of[m][:].rearrange("p t (h b) -> p h b t", h=2)[:, :, SETS - SHARE :, :])
+            nc.scalar.copy(out=rest[:], in_=a_of[m][:].rearrange("p t (h b) -> p h b t", h=2)[:, :, SETS - WIDE :, :])
 
         v_all = const.tile([P, SENDERS, P + MOST, 4], F32, align_bytes=64)
 
@@ -219,12 +220,12 @@ def tile_nonlocalmp_pa_t_w4_kernel(tc, F_bytes, F_scale, W1_words, W1_scales, b1
                 op=ALU.add,
             )
 
-        def add_rest(u, h):
+        def add_rest(u, h, n):
             m, q = divmod(u, STEPS)
             nc.gpsimd.tensor_tensor(
-                out=v_of(u)[:, :, SETS * (h + 1) - SHARE : SETS * (h + 1), :],
-                in0=rest_of[m][:, h].unsqueeze(1).to_broadcast([P, SENDERS, SHARE, 4]),
-                in1=bp[:, SENDERS * q : SENDERS * (q + 1), SETS - SHARE :, :],
+                out=v_of(u)[:, :, SETS * (h + 1) - n : SETS * (h + 1), :],
+                in0=rest_of[m][:, h, WIDE - n :].unsqueeze(1).to_broadcast([P, SENDERS, n, 4]),
+                in1=bp[:, SENDERS * q : SENDERS * (q + 1), SETS - n :, :],
                 op=ALU.add,
             )
 
@@ -309,10 +310,6 @@ def tile_nonlocalmp_pa_t_w4_kernel(tc, F_bytes, F_scale, W1_words, W1_scales, b1
         def add_up(u, c):
             m, q = divmod(u, STEPS)
             halves = m == TILES - 1
-            if q == 0 and c == 0:
-                open_sum(m, (0, 1) if halves else (0, 1, 2, 3), "sum")
-            if q == 0 and c == 2 and halves:
-                open_sum(m, (2, 3), "lin")
             for j in range(SENDERS):
                 last = q == STEPS - 1 and j == SENDERS - 1 and (c == 3 or (c == 1 and halves))
                 nc.tensor.matmul(sum_of[m, c], lhsT=relu_of[u, c][:, j, :], rhs=ident[:], is_transpose=True, start=False, stop=last)
@@ -386,9 +383,10 @@ def tile_nonlocalmp_pa_t_w4_kernel(tc, F_bytes, F_scale, W1_words, W1_scales, b1
         last = UNITS - 1
         for p in range(UNITS):
             s = p - 2
-            add_rest(p, 1 - p % 2)
+            n = WIDE if (p % STEPS == STEPS - 1 and STEPS < p < last) or p == 0 else SHARE
+            add_rest(p, 1 - p % 2, n)
             add(p, p % 2, SETS)
-            add(p, 1 - p % 2, SETS - SHARE)
+            add(p, 1 - p % 2, SETS - n)
             if s >= 2 and (s - 2) % STEPS == STEPS - 1 and p < last:
                 finish((s - 2) // STEPS, 0, CHUNKS, (nc.sync, nc.sync))
             if p == 0:
@@ -411,6 +409,10 @@ def tile_nonlocalmp_pa_t_w4_kernel(tc, F_bytes, F_scale, W1_words, W1_scales, b1
             scalar_part(p, 1)
             if p == 0:
                 leave_b2()
+            if s >= 0 and s % STEPS == 0:
+                open_sum(s // STEPS, (0, 1) if s // STEPS == TILES - 1 else (0, 1, 2, 3), "sum")
+            if p == last:
+                open_sum(TILES - 1, (2, 3), "lin")
             if s >= 1:
                 add_up(s - 1, 2)
                 add_up(s - 1, 3)

@@ -18,24 +18,32 @@ SETS, NODES, C = 64, 16, 512
 SLOPE = 0.2
 FLOPS = 2 * SETS * NODES * C * 2 * C + 2 * SETS * NODES * NODES * C * C
 
-TILES = 8
+TILES = NODES // 2
 SENDERS = 4
-STEPS = NODES // SENDERS
-UNITS = TILES * STEPS
+UNITS_A_TILE = NODES // SENDERS
+UNITS = TILES * UNITS_A_TILE
+LAST = UNITS - 1
 CHUNKS = C // P
+LAG = 2
 
-
-WIDE = 46
 SHARE = 36
+WIDE = 46
 MOST = 44
+EARLY = 30
+EARLY_UNITS = 3
+CHAINED = 2
 
 
-def scalar_columns(u):
-    if u < 3:
-        return 30
-    if u >= UNITS - 2:
+def scalar_columns(unit):
+    if unit < EARLY_UNITS:
+        return EARLY
+    if unit >= UNITS - CHAINED:
         return 0
     return MOST
+
+
+def finishes_tile(step):
+    return step % UNITS_A_TILE == UNITS_A_TILE - 1 and UNITS_A_TILE < step < LAST
 
 
 def tile_nonlocalmp_pa_t_w4_kernel(tc, F_bytes, F_scale, W1_words, W1_scales, b1, W2_words, W2_scales, b2, out):
@@ -46,7 +54,7 @@ def tile_nonlocalmp_pa_t_w4_kernel(tc, F_bytes, F_scale, W1_words, W1_scales, b1
         work = ctx.enter_context(tc.tile_pool(name="work", bufs=3))
         ps = ctx.enter_context(tc.psum_pool(name="ps", bufs=1))
 
-        f_src = F_bytes.rearrange("b (h m) k -> (b h) (m k)", h=2)
+        f_src = F_bytes.rearrange("b (side m) k -> (b side) (m k)", side=2)
         fbytes0 = const.tile([P, 4 * C], U8, align_bytes=64)
         fbytes1 = const.tile([P, 4 * C], U8, align_bytes=64)
         nc.sync.dma_start(out=fbytes0[:], in_=f_src[:, 0 : 4 * C])
@@ -64,17 +72,17 @@ def tile_nonlocalmp_pa_t_w4_kernel(tc, F_bytes, F_scale, W1_words, W1_scales, b1
         nc.vector.memset(w2s[:].bitcast(I32), 0)
         w1s_src = W1_scales.rearrange("g (q r) n -> r q g n", r=4)
         w2s_src = W2_scales.rearrange("g (q r) n -> r q (g n)", r=4)
-        for r in range(4):
-            nc.sync.dma_start(out=w1sraw[r:P:32, :, :].bitcast(I32), in_=w1s_src[r].bitcast(I32))
+        for row in range(4):
+            nc.sync.dma_start(out=w1sraw[row:P:32, :, :].bitcast(I32), in_=w1s_src[row].bitcast(I32))
         nc.sync.dma_start(out=fbytes1[:], in_=f_src[:, 4 * C : 8 * C])
         b1raw = const.tile([P, 4], BF16)
         nc.sync.dma_start(out=b1raw[:], in_=b1.rearrange("(p t) -> p t", t=4))
         w2 = const.tile([P, 2 * C], U8, align_bytes=64)
         nc.sync.dma_start(out=w2[:].bitcast(I32), in_=W2_words[0].bitcast(I32))
-        for r in range(4):
-            nc.sync.dma_start(out=w2s[r:P:32, :].bitcast(I32), in_=w2s_src[r].bitcast(I32))
+        for row in range(4):
+            nc.sync.dma_start(out=w2s[row:P:32, :].bitcast(I32), in_=w2s_src[row].bitcast(I32))
         b2raw = const.tile([P, P], BF16)
-        nc.sync.dma_start(out=b2raw[0:4, :], in_=b2.rearrange("(c p) -> c p", p=P))
+        nc.sync.dma_start(out=b2raw[0:CHUNKS, :], in_=b2.rearrange("(c p) -> c p", p=P))
 
         ident = const.tile([P, P], F32)
         make_identity(nc, ident[:])
@@ -82,6 +90,8 @@ def tile_nonlocalmp_pa_t_w4_kernel(tc, F_bytes, F_scale, W1_words, W1_scales, b1
         nc.vector.memset(b2f[:], 0.0)
         twelves = const.tile([P, P], BF16)
         nc.vector.memset(twelves[:], 12.0)
+        eights = const.tile([P, P], BF16)
+        nc.vector.memset(eights[:], 8.0)
         ident16 = const.tile([P, P], BF16)
         nc.scalar.copy(out=ident16[:], in_=ident[:])
         b1wide = const.tile([P, 4, P], BF16)
@@ -107,29 +117,29 @@ def tile_nonlocalmp_pa_t_w4_kernel(tc, F_bytes, F_scale, W1_words, W1_scales, b1
             src = fbytes0[:, m * C : (m + 1) * C] if m < 4 else fbytes1[:, (m - 4) * C : (m - 3) * C]
             copy(out=fwide[:, m, :], in_=src.bitcast(FP8))
 
-        xt_of = {}
+        turned_of = {}
 
-        def turn_f(tiles, tag, bufs):
-            xt = ps.tile([P, len(tiles), 2, P], F32, name="xt", tag=tag, bufs=bufs)
+        def turn_f(tiles, tag):
+            xt = ps.tile([P, len(tiles), 2, P], F32, name="xt", tag=tag, bufs=2)
             for i, m in enumerate(tiles):
-                xt_of[m] = xt[:, i]
+                turned_of[m] = xt[:, i]
                 words = fwide[:, m, :].bitcast(F32)
-                for u in range(2):
-                    nc.tensor.transpose(xt[:, i, u, :], words[:, u::2], ident[:])
+                for w in range(2):
+                    nc.tensor.transpose(xt[:, i, w, :], words[:, w::2], ident[:])
 
         def scale_f(m):
-            sc = fsc[:].rearrange("p (o u e) -> p o u e", o=1, u=2).to_broadcast([P, SETS, 2, 2])
-            src = xt_of[m].bitcast(BF16).rearrange("p u (b h e) -> p h b u e", h=2, e=2)
-            for h in range(2):
-                to = fg[:, m, SETS * h : SETS * (h + 1), :].rearrange("p b (u e) -> p b u e", e=2)
-                nc.vector.tensor_tensor(out=to, in0=src[:, h], in1=sc, op=ALU.mult)
+            sc = fsc[:].rearrange("p (o w e) -> p o w e", o=1, w=2).to_broadcast([P, SETS, 2, 2])
+            src = turned_of[m].bitcast(BF16).rearrange("p w (b side e) -> p side b w e", side=2, e=2)
+            for side in range(2):
+                to = fg[:, m, SETS * side : SETS * (side + 1), :].rearrange("p b (w e) -> p b w e", e=2)
+                nc.vector.tensor_tensor(out=to, in0=src[:, side], in1=sc, op=ALU.mult)
 
         def quantise_f(first, end):
-            mm = slice(first, end)
+            tiles = slice(first, end)
             nc.vector.quantize_mx(
-                out=fq[:, mm, :].rearrange("p m r -> p (m r)").bitcast(FP8X4),
-                scales=fs[:, mm, :].rearrange("p m r -> p (m r)"),
-                in_=fg[:, mm].rearrange("p m r t -> p (m r t)"),
+                out=fq[:, tiles, :].rearrange("p m r -> p (m r)").bitcast(FP8X4),
+                scales=fs[:, tiles, :].rearrange("p m r -> p (m r)"),
+                in_=fg[:, tiles].rearrange("p m r t -> p (m r t)"),
             )
 
         rows_of = {}
@@ -157,25 +167,24 @@ def tile_nonlocalmp_pa_t_w4_kernel(tc, F_bytes, F_scale, W1_words, W1_scales, b1
                 nc.tensor.matmul(flat, lhsT=ident16[:], rhs=b1wide[:].rearrange("p t r -> p (t r)"), start=True, stop=False)
                 for t in range(4):
                     nc.tensor.matmul(bank[:, t, :], lhsT=rows_of[m][:, t, :], rhs=ident[:], is_transpose=True, start=False, stop=(t == 3))
-                nc.scalar.copy(out=bp[:, 2 * m : 2 * m + 2, :, :].rearrange("p h b t -> p (h b) t"), in_=bank[:].rearrange("p t r -> p r t"))
+                to = bp[:, 2 * m : 2 * m + 2, :, :].rearrange("p side b t -> p (side b) t")
+                nc.scalar.copy(out=to, in_=bank[:].rearrange("p t r -> p r t"))
 
         b2c = const.tile([P, CHUNKS], F32)
         b2neg = const.tile([P, CHUNKS], F32)
 
-        b2_bank = []
-
         def turn_b2():
-            nc.scalar.copy(out=b2f[0:4, :], in_=b2raw[0:4, :])
+            nc.scalar.copy(out=b2f[0:CHUNKS, :], in_=b2raw[0:CHUNKS, :])
             bt = ps.tile([P, P], F32, name="bt", tag="lin", bufs=2)
             nc.tensor.transpose(bt[:], b2f[:], ident[:])
-            b2_bank.append(bt)
+            return bt
 
-        def leave_b2():
-            bt = b2_bank[0]
+        def leave_b2(bt):
             nc.scalar.copy(out=b2c[:], in_=bt[:, 0:CHUNKS])
             nc.scalar.activation(out=b2neg[:], in_=bt[:, 0:CHUNKS], func=ACT.Copy, scale=-1.0)
 
-        a_of, rest_of, h_of, part_of, hq_of, relu_of, lin_of, sum_of, bank_of, fifth_of = {}, {}, {}, {}, {}, {}, {}, {}, {}, {}
+        a_of, a_copy_of, h_of, part_of, hq_of, relu_of = {}, {}, {}, {}, {}, {}
+        lin_of, sum_of, sum_bank_of, fifth_of = {}, {}, {}, {}
 
         def receivers(m):
             bank = ps.tile([P, 4, P], F32, name="bank", tag="a", bufs=1)
@@ -191,75 +200,73 @@ def tile_nonlocalmp_pa_t_w4_kernel(tc, F_bytes, F_scale, W1_words, W1_scales, b1
                     stop=True,
                 )
 
-        def receivers_rest(m):
+        def copy_receivers(m):
             rest = work.tile([P, 2, WIDE, 4], F32, name="rest", bufs=2, align_bytes=64)
-            rest_of[m] = rest
-            nc.scalar.copy(out=rest[:], in_=a_of[m][:].rearrange("p t (h b) -> p h b t", h=2)[:, :, SETS - WIDE :, :])
+            a_copy_of[m] = rest
+            nc.scalar.copy(out=rest[:], in_=a_of[m][:].rearrange("p t (side b) -> p side b t", side=2)[:, :, SETS - WIDE :, :])
 
         v_all = const.tile([P, SENDERS, P + MOST, 4], F32, align_bytes=64)
 
-        def v_of(u):
-            first = MOST * (u % 2)
+        def v_of(unit):
+            first = MOST * (unit % 2)
             return v_all[:, :, first : first + P, :]
 
-        def by_scalar(u):
-            x = scalar_columns(u)
-            return slice(0, x) if u % 2 == 0 else slice(P - x, P)
+        def by_scalar(unit):
+            width = scalar_columns(unit)
+            return slice(0, width) if unit % 2 == 0 else slice(P - width, P)
 
-        def by_vector(u):
-            x = scalar_columns(u)
-            return slice(x, P) if u % 2 == 0 else slice(0, P - x)
+        def by_vector(unit):
+            width = scalar_columns(unit)
+            return slice(width, P) if unit % 2 == 0 else slice(0, P - width)
 
-        def add(u, h, n):
-            m, q = divmod(u, STEPS)
-            cols = slice(SETS * h, SETS * h + n)
+        def add(unit, side, sets):
+            m, q = divmod(unit, UNITS_A_TILE)
+            cols = slice(SETS * side, SETS * side + sets)
             nc.vector.tensor_tensor(
-                out=v_of(u)[:, :, cols, :],
-                in0=a_of[m][:].rearrange("p t r -> p r t")[:, cols, :].unsqueeze(1).to_broadcast([P, SENDERS, n, 4]),
-                in1=bp[:, SENDERS * q : SENDERS * (q + 1), 0:n, :],
+                out=v_of(unit)[:, :, cols, :],
+                in0=a_of[m][:].rearrange("p t r -> p r t")[:, cols, :].unsqueeze(1).to_broadcast([P, SENDERS, sets, 4]),
+                in1=bp[:, SENDERS * q : SENDERS * (q + 1), 0:sets, :],
                 op=ALU.add,
             )
 
-        def add_rest(u, h, n):
-            m, q = divmod(u, STEPS)
+        def add_on_gpsimd(unit, side, sets):
+            m, q = divmod(unit, UNITS_A_TILE)
             nc.gpsimd.tensor_tensor(
-                out=v_of(u)[:, :, SETS * (h + 1) - n : SETS * (h + 1), :],
-                in0=rest_of[m][:, h, WIDE - n :].unsqueeze(1).to_broadcast([P, SENDERS, n, 4]),
-                in1=bp[:, SENDERS * q : SENDERS * (q + 1), SETS - n :, :],
+                out=v_of(unit)[:, :, SETS * (side + 1) - sets : SETS * (side + 1), :],
+                in0=a_copy_of[m][:, side, WIDE - sets :].unsqueeze(1).to_broadcast([P, SENDERS, sets, 4]),
+                in1=bp[:, SENDERS * q : SENDERS * (q + 1), SETS - sets :, :],
                 op=ALU.add,
             )
 
-        def scalar_part(u, sign):
-            x = scalar_columns(u)
-            if x == 0:
+        def scalar_part(unit, sign):
+            width = scalar_columns(unit)
+            if width == 0:
                 return
-            part = work.tile([P, SENDERS, x, 4], BF16, name="part", bufs=4, align_bytes=64)
-            part_of[u, sign] = part
-            nc.scalar.activation(out=part[:], in_=v_of(u)[:, :, by_scalar(u), :], func=ACT.Relu, scale=(1.0, -SLOPE)[sign])
+            part = work.tile([P, SENDERS, width, 4], BF16, name="part", bufs=4, align_bytes=64)
+            part_of[unit, sign] = part
+            nc.scalar.activation(out=part[:], in_=v_of(unit)[:, :, by_scalar(unit), :], func=ACT.Relu, scale=(1.0, -SLOPE)[sign])
 
-        def h_tile(u):
-            if u not in h_of:
-                h = work.tile([P, SENDERS, P, 4], BF16, name="h", align_bytes=64)
-                h_of[u] = h
-            return h_of[u]
-
-        def leaky(u):
-            src = v_of(u)[:, :, by_vector(u), :].rearrange("p j r t -> p j (r t)")
-            to = h_tile(u)[:, :, by_vector(u), :].rearrange("p j r t -> p j (r t)")
+        def leaky(unit):
+            tag, bufs = ("h_last", 1) if unit == LAST else ("h", 3)
+            h = work.tile([P, SENDERS, P, 4], BF16, name="h", tag=tag, bufs=bufs, align_bytes=64)
+            h_of[unit] = h
+            src = v_of(unit)[:, :, by_vector(unit), :].rearrange("p j r t -> p j (r t)")
+            to = h[:, :, by_vector(unit), :].rearrange("p j r t -> p j (r t)")
             nc.vector.scalar_tensor_tensor(out=to, in0=src, scalar=SLOPE, in1=src, op0=ALU.mult, op1=ALU.max)
 
-        def join(u):
-            if scalar_columns(u) > 0:
-                nc.vector.tensor_tensor(out=h_tile(u)[:, :, by_scalar(u), :], in0=part_of[u, 0][:], in1=part_of[u, 1][:], op=ALU.subtract)
+        def join(unit):
+            if scalar_columns(unit) > 0:
+                to = h_of[unit][:, :, by_scalar(unit), :]
+                nc.vector.tensor_tensor(out=to, in0=part_of[unit, 0][:], in1=part_of[unit, 1][:], op=ALU.subtract)
 
-        def quantise_h(u):
+        def quantise_h(unit):
             hq = work.tile([P, SENDERS * P], I32, name="hq", align_bytes=64)
             hs = work.tile([P, SENDERS * P], U8, name="hs", align_bytes=64)
-            hq_of[u] = (hq, hs)
-            nc.vector.quantize_mx(out=hq[:].bitcast(FP8X4), scales=hs[:], in_=h_of[u][:].rearrange("p j r t -> p (j r t)"))
+            hq_of[unit] = (hq, hs)
+            nc.vector.quantize_mx(out=hq[:].bitcast(FP8X4), scales=hs[:], in_=h_of[unit][:].rearrange("p j r t -> p (j r t)"))
 
-        def message(u, c, tag="message", bufs=3):
-            hq, hs = hq_of[u]
+        def message(unit, c, tag="message", bufs=3):
+            hq, hs = hq_of[unit]
             bank = ps.tile([P, SENDERS * P], F32, name="bank", tag=tag, bufs=bufs)
             nc.tensor.matmul_mx(
                 out=bank[:],
@@ -270,11 +277,18 @@ def tile_nonlocalmp_pa_t_w4_kernel(tc, F_bytes, F_scale, W1_words, W1_scales, b1
                 start=True,
                 stop=True,
             )
-            return bank
+            relu = work.tile([P, SENDERS, P], F32, name="relu", bufs=10, align_bytes=64)
+            relu_of[unit, c] = relu
+            flat = relu[:].rearrange("p j r -> p (j r)")
+            if unit == LAST or (unit == LAST - 1 and c >= 2):
+                before = relu_of[unit - 1, c][:].rearrange("p j r -> p (j r)")
+                nc.vector.scalar_tensor_tensor(out=flat, in0=bank[:], scalar=b2neg[:, c : c + 1], in1=before, op0=ALU.max, op1=ALU.add)
+            else:
+                nc.scalar.activation(out=flat, in_=bank[:], func=ACT.Relu, bias=b2c[:, c : c + 1], scale=1.0)
 
-        def linear(u, j):
-            m, q = divmod(u, STEPS)
-            hq, hs = hq_of[u]
+        def linear(unit, j):
+            m, q = divmod(unit, UNITS_A_TILE)
+            hq, hs = hq_of[unit]
             if q == 0 and j == 0:
                 lin = ps.tile([P, C], F32, name="lin", tag="lin", bufs=2)
                 lin_of[m] = lin
@@ -285,67 +299,49 @@ def tile_nonlocalmp_pa_t_w4_kernel(tc, F_bytes, F_scale, W1_words, W1_scales, b1
                 rhs=w2[:].bitcast(FP4X4),
                 rhs_scale=w2s[:],
                 start=(q == 0 and j == 0),
-                stop=(q == STEPS - 1 and j == SENDERS - 1),
+                stop=(q == UNITS_A_TILE - 1 and j == SENDERS - 1),
             )
-
-        def rectify(u, c, bank):
-            relu = work.tile([P, SENDERS, P], F32, name="relu", bufs=10, align_bytes=64)
-            relu_of[u, c] = relu
-            flat = relu[:].rearrange("p j r -> p (j r)")
-            if u >= UNITS - 2:
-                before = relu_of[u - 1, c][:].rearrange("p j r -> p (j r)")
-                nc.vector.scalar_tensor_tensor(out=flat, in0=bank[:], scalar=b2neg[:, c : c + 1], in1=before, op0=ALU.max, op1=ALU.add)
-            else:
-                nc.scalar.activation(out=flat, in_=bank[:], func=ACT.Relu, bias=b2c[:, c : c + 1], scale=1.0)
 
         def open_sum(m, chunks, tag):
             total = ps.tile([P, len(chunks), P], F32, name="total", tag=tag, bufs=2)
             for i, c in enumerate(chunks):
                 sum_of[m, c] = total[:, i, :]
-            bank_of[m, chunks[0]] = total
-            times = fours if m < TILES - 1 else twelves
-            row = b2row[:, P * chunks[0] : P * (chunks[-1] + 1)]
-            nc.tensor.matmul(total[:].rearrange("p c r -> p (c r)"), lhsT=times[:], rhs=row, start=True, stop=False)
+            sum_bank_of[m, chunks[0]] = total
+            times = fours if m < TILES - 1 else eights if chunks[0] == 0 else twelves
+            b2_part = b2row[:, P * chunks[0] : P * (chunks[-1] + 1)]
+            nc.tensor.matmul(total[:].rearrange("p c r -> p (c r)"), lhsT=times[:], rhs=b2_part, start=True, stop=False)
 
-        def add_up(u, c):
-            m, q = divmod(u, STEPS)
-            halves = m == TILES - 1
+        def add_up(unit, c):
+            m, q = divmod(unit, UNITS_A_TILE)
+            closing_chunks = (1, 3) if m == TILES - 1 else (3,)
             for j in range(SENDERS):
-                last = q == STEPS - 1 and j == SENDERS - 1 and (c == 3 or (c == 1 and halves))
-                nc.tensor.matmul(sum_of[m, c], lhsT=relu_of[u, c][:, j, :], rhs=ident[:], is_transpose=True, start=False, stop=last)
+                closes = q == UNITS_A_TILE - 1 and j == SENDERS - 1 and c in closing_chunks
+                nc.tensor.matmul(sum_of[m, c], lhsT=relu_of[unit, c][:, j, :], rhs=ident[:], is_transpose=True, start=False, stop=closes)
 
         def leave_linear(m):
             fifth = work.tile([P, C], F32, name="fifth", bufs=2)
             fifth_of[m] = fifth
             nc.scalar.activation(out=fifth[:], in_=lin_of[m][:], func=ACT.Copy, scale=SLOPE)
 
-        out_v = out.rearrange("b (h m) c -> m h b c", h=2)
+        out_v = out.rearrange("b (side m) c -> m side b c", side=2)
 
         def finish(m, first, end, queues):
             cols = slice(P * first, P * end)
             st = work.tile([P, P * (end - first)], F32, name="st", bufs=2)
             nc.vector.scalar_tensor_tensor(
                 out=st[:],
-                in0=bank_of[m, first][:].rearrange("p c r -> p (c r)"),
+                in0=sum_bank_of[m, first][:].rearrange("p c r -> p (c r)"),
                 scalar=1.0 - SLOPE,
                 in1=fifth_of[m][:, cols],
                 op0=ALU.mult,
                 op1=ALU.add,
             )
-            for h in range(2):
-                queues[h].dma_start(out=out_v[m, h][:, cols], in_=st[SETS * h : SETS * (h + 1), :])
+            for side in range(2):
+                queues[side].dma_start(out=out_v[m, side][:, cols], in_=st[SETS * side : SETS * (side + 1), :])
 
-        def second_product(u):
-            rectify(u, 0, message(u, 0))
-            linear(u, 0)
-            rectify(u, 1, message(u, 1))
-            rectify(u, 2, message(u, 2))
-            linear(u, 1)
-            rectify(u, 3, message(u, 3))
-
-        def warm_up(n):
+        def warm_up(count):
             idle = ps.tile([P, C], F32, name="idle", tag="message", bufs=3)
-            for i in range(n):
+            for i in range(count):
                 nc.tensor.matmul(idle[:], lhsT=fours[:], rhs=b2row[:], start=True, stop=True)
 
         warm_up(4)
@@ -353,10 +349,10 @@ def tile_nonlocalmp_pa_t_w4_kernel(tc, F_bytes, F_scale, W1_words, W1_scales, b1
         for m in range(1, TILES - 1):
             widen(m, nc.scalar.copy)
         nc.scalar.copy(out=b1wide[:], in_=b1raw[:].unsqueeze(2).to_broadcast([P, 4, P]))
-        turn_f([0], "sum", 2)
-        turn_f([1], "lin", 2)
+        turn_f([0], "sum")
+        turn_f([1], "lin")
         warm_up(2)
-        turn_f([2, 3], "sum", 2)
+        turn_f([2, 3], "sum")
         warm_up(2)
         nc.sync.dma_start(out=b2row[0:1, :], in_=b2.rearrange("(o c) -> o c", o=1))
         permute_w1a()
@@ -366,84 +362,105 @@ def tile_nonlocalmp_pa_t_w4_kernel(tc, F_bytes, F_scale, W1_words, W1_scales, b1
         quantise_f(0, 2)
         scale_f(2)
         scale_f(3)
-        turn_f([4, 5], "sum", 2)
+        turn_f([4, 5], "sum")
         sender_rows(0)
         receivers(0)
         widen(TILES - 1, nc.vector.tensor_copy)
         quantise_f(2, 4)
-        receivers_rest(0)
+        copy_receivers(0)
         sender_columns(0)
-        turn_f([6, 7], "lin", 2)
+        turn_f([6, 7], "lin")
         sender_rows(1)
         sender_columns(1)
         scale_f(4)
         scale_f(5)
         quantise_f(4, 6)
 
-        last = UNITS - 1
-        for p in range(UNITS):
-            s = p - 2
-            n = WIDE if (p % STEPS == STEPS - 1 and STEPS < p < last) or p == 0 else SHARE
-            add_rest(p, 1 - p % 2, n)
-            add(p, p % 2, SETS)
-            add(p, 1 - p % 2, SETS - n)
-            if s >= 2 and (s - 2) % STEPS == STEPS - 1 and p < last:
-                finish((s - 2) // STEPS, 0, CHUNKS, (nc.sync, nc.sync))
-            if p == 0:
+        for step in range(UNITS):
+            behind = step - LAG
+            tile, place = divmod(step, UNITS_A_TILE)
+            whole, shared = step % 2, 1 - step % 2
+            sets = WIDE if finishes_tile(step) or step == 0 else SHARE
+            add_on_gpsimd(step, shared, sets)
+            add(step, whole, SETS)
+            add(step, shared, SETS - sets)
+            if finishes_tile(step):
+                finish(tile - 1, 0, CHUNKS, (nc.sync, nc.sync))
+            if step == 0:
                 scale_f(6)
                 scale_f(7)
-            if s >= 0:
-                second_product(s)
-            if s > 0 and s % STEPS == 0:
-                leave_linear(s // STEPS - 1)
-            if p % STEPS == STEPS - 1 and p // STEPS + 1 < TILES:
-                receivers(p // STEPS + 1)
-                receivers_rest(p // STEPS + 1)
-            if p + 2 < STEPS:
-                sender_rows(p + 2)
-            scalar_part(p, 0)
-            if p + 2 < STEPS:
-                sender_columns(p + 2)
-            if p == 0:
-                turn_b2()
-            scalar_part(p, 1)
-            if p == 0:
-                leave_b2()
-            if s >= 0 and s % STEPS == 0:
-                open_sum(s // STEPS, (0, 1) if s // STEPS == TILES - 1 else (0, 1, 2, 3), "sum")
-            if p == last:
-                open_sum(TILES - 1, (2, 3), "lin")
-            if s >= 1:
-                add_up(s - 1, 2)
-                add_up(s - 1, 3)
-            if s >= 0:
-                if p < last:
-                    add_up(s, 0)
-                    add_up(s, 1)
-                linear(s, 2)
-                linear(s, 3)
-            if p >= 1:
-                join(p - 1)
-            if p == last:
-                quantise_h(p - 1)
-            leaky(p)
-            if p == 0:
+            if behind >= 0:
+                message(behind, 0)
+                linear(behind, 0)
+                message(behind, 1)
+                message(behind, 2)
+                linear(behind, 1)
+                message(behind, 3)
+            opens_tile = behind >= 0 and behind % UNITS_A_TILE == 0
+            if opens_tile and tile > 0:
+                leave_linear(tile - 1)
+            if place == UNITS_A_TILE - 1 and tile + 1 < TILES:
+                receivers(tile + 1)
+                copy_receivers(tile + 1)
+            senders_to_come = step + 2 < UNITS_A_TILE
+            if senders_to_come:
+                sender_rows(step + 2)
+            scalar_part(step, 0)
+            if senders_to_come:
+                sender_columns(step + 2)
+            if step == 0:
+                b2_bank = turn_b2()
+            scalar_part(step, 1)
+            if step == 0:
+                leave_b2(b2_bank)
+            if opens_tile:
+                open_sum(tile, (0, 1) if tile == TILES - 1 else (0, 1, 2, 3), "sum")
+            if step == LAST:
+                open_sum(tile, (2, 3), "lin")
+            if behind >= 1:
+                add_up(behind - 1, 2)
+                add_up(behind - 1, 3)
+            if behind >= 0:
+                if behind < LAST - CHAINED:
+                    add_up(behind, 0)
+                    add_up(behind, 1)
+                linear(behind, 2)
+                linear(behind, 3)
+            if step >= 1:
+                join(step - 1)
+            if step == LAST:
+                quantise_h(step - 1)
+            leaky(step)
+            if step == 0:
                 quantise_f(6, TILES)
-            if 1 <= p < last:
-                quantise_h(p - 1)
+            if 1 <= step < LAST:
+                quantise_h(step - 1)
+
+        def add_pair(c):
+            both = work.tile([P, SENDERS, P], F32, name="both", tag=("h_last", "both")[c], bufs=1, align_bytes=64)
+            nc.gpsimd.tensor_tensor(out=both[:], in0=relu_of[LAST - 2, c][:], in1=relu_of[LAST - 1, c][:], op=ALU.add)
+            relu_of[LAST - 1, c] = both
+
         finish(TILES - 2, 0, CHUNKS, (nc.sync, nc.sync))
-        quantise_h(last)
-        for c in range(3):
-            rectify(last - 1, c, message(last - 1, c))
-        rectify(last - 1, 3, message(last - 1, 3, "a", 1))
+        quantise_h(LAST)
+        message(LAST - 1, 0)
+        message(LAST - 1, 1)
+        add_pair(0)
+        add_pair(1)
+        message(LAST - 1, 2)
+        message(LAST - 1, 3, "a", 1)
         for j in range(SENDERS):
-            linear(last - 1, j)
-        for j in range(SENDERS):
-            linear(last, j)
+            linear(LAST - 1, j)
+        message(LAST, 2)
+        message(LAST, 3)
+        message(LAST, 0)
+        linear(LAST, 0)
+        linear(LAST, 1)
+        message(LAST, 1)
+        linear(LAST, 2)
+        linear(LAST, 3)
         leave_linear(TILES - 1)
-        for c in range(CHUNKS):
-            rectify(last, c, message(last, c))
-        for c in range(CHUNKS):
-            add_up(last, c)
+        for c in (2, 3, 0, 1):
+            add_up(LAST, c)
             if c % 2 == 1:
                 finish(TILES - 1, c - 1, c + 1, (nc.sync, nc.scalar))

@@ -18,50 +18,61 @@ SETS, NODES, C = 64, 16, 512
 SLOPE = 0.2
 FLOPS = 2 * SETS * NODES * C * 2 * C + 2 * SETS * NODES * NODES * C * C
 
-TILES = NODES // 2
+GROUP = P // NODES
+TILES = SETS // GROUP
 SENDERS = 4
-UNITS_A_TILE = NODES // SENDERS
-UNITS = TILES * UNITS_A_TILE
-LAST = UNITS - 1
 CHUNKS = C // P
 LAG = 2
 
-SHARE = 36
-WIDE = 46
+FIRST_TILE = (4, 4, 4, 4)
+LAST_TILE = (4, 4, 4, 4)
 MOST = 44
-EARLY = 30
-EARLY_UNITS = 3
+EARLY = 64
+EARLY_UNITS = 2
 CHAINED = 2
-
-
-def scalar_columns(unit):
-    if unit < EARLY_UNITS:
-        return EARLY
-    if unit >= UNITS - CHAINED:
-        return 0
-    return MOST
-
-
-def finishes_tile(step):
-    return step % UNITS_A_TILE == UNITS_A_TILE - 1 and UNITS_A_TILE < step < LAST
+LATE = (0, 0)
+WIDE = 48
+SHARE = 32
+AHEAD = 2
+FIRST_SHARE = 24
+HQ = 3
 
 
 def tile_nonlocalmp_pa_t_w4_kernel(tc, F_bytes, F_scale, W1_words, W1_scales, b1, W2_words, W2_scales, b2, out):
     nc = tc.nc
+    units, first, last = [], {}, {}
+    for m in range(TILES):
+        sizes = FIRST_TILE if m == 0 else LAST_TILE if m == TILES - 1 else (SENDERS,) * (NODES // SENDERS)
+        first[m] = len(units)
+        for n, size in enumerate(sizes):
+            units.append((m, sum(sizes[:n]), size))
+        last[m] = len(units) - 1
+    LAST = len(units) - 1
+    ROW = max(MOST, EARLY)
+
+    def scalar_columns(unit):
+        if unit > LAST - CHAINED:
+            return LATE[unit - LAST + CHAINED - 1]
+        return EARLY if unit < EARLY_UNITS else MOST
+
     with ExitStack() as ctx:
         ctx.enter_context(tc.manual_schedule())
         const = ctx.enter_context(tc.tile_pool(name="const", bufs=1))
         work = ctx.enter_context(tc.tile_pool(name="work", bufs=3))
         ps = ctx.enter_context(tc.psum_pool(name="ps", bufs=1))
 
-        f_src = F_bytes.rearrange("b (side m) k -> (b side) (m k)", side=2)
-        fbytes0 = const.tile([P, 4 * C], U8, align_bytes=64)
-        fbytes1 = const.tile([P, 4 * C], U8, align_bytes=64)
-        nc.sync.dma_start(out=fbytes0[:], in_=f_src[:, 0 : 4 * C])
+        def tokens(dram, m):
+            return dram[GROUP * m : GROUP * (m + 1)].rearrange("b i c -> i b c")
+
+        fbytes = []
+        for m in range(TILES):
+            fb = const.tile([P, C], U8, name="fbytes%d" % m, align_bytes=64)
+            fbytes.append(fb)
+        nc.sync.dma_start(out=fbytes[0][:], in_=tokens(F_bytes, 0))
+        w1raw = const.tile([P, 2, 2 * C], U8, align_bytes=64)
+        nc.sync.dma_start(out=w1raw[:, 0, :].bitcast(I32), in_=W1_words[0].bitcast(I32))
         fsc = const.tile([P, 4], F32)
         nc.sync.dma_start(out=fsc[:], in_=F_scale.rearrange("a c (p t) -> p (a c t)", t=4))
-        w1raw = const.tile([P, 2, 2 * C], U8, align_bytes=64)
-        nc.sync.dma_start(out=w1raw[:].bitcast(I32), in_=W1_words.rearrange("g p n -> p g n").bitcast(I32))
         w1sraw = const.tile([P, 2, C], U8, align_bytes=64)
         w2s = const.tile([P, C], U8, align_bytes=64)
         fours = const.tile([P, P], BF16)
@@ -74,15 +85,18 @@ def tile_nonlocalmp_pa_t_w4_kernel(tc, F_bytes, F_scale, W1_words, W1_scales, b1
         w2s_src = W2_scales.rearrange("g (q r) n -> r q (g n)", r=4)
         for row in range(4):
             nc.sync.dma_start(out=w1sraw[row:P:32, :, :].bitcast(I32), in_=w1s_src[row].bitcast(I32))
-        nc.sync.dma_start(out=fbytes1[:], in_=f_src[:, 4 * C : 8 * C])
+        nc.sync.dma_start(out=w1raw[:, 1, :].bitcast(I32), in_=W1_words[1].bitcast(I32))
         b1raw = const.tile([P, 4], BF16)
         nc.sync.dma_start(out=b1raw[:], in_=b1.rearrange("(p t) -> p t", t=4))
+        nc.sync.dma_start(out=fbytes[1][:], in_=tokens(F_bytes, 1))
+        b2raw = const.tile([P, P], BF16)
+        nc.sync.dma_start(out=b2raw[0:CHUNKS, :], in_=b2.rearrange("(c p) -> c p", p=P))
         w2 = const.tile([P, 2 * C], U8, align_bytes=64)
         nc.sync.dma_start(out=w2[:].bitcast(I32), in_=W2_words[0].bitcast(I32))
         for row in range(4):
             nc.sync.dma_start(out=w2s[row:P:32, :].bitcast(I32), in_=w2s_src[row].bitcast(I32))
-        b2raw = const.tile([P, P], BF16)
-        nc.sync.dma_start(out=b2raw[0:CHUNKS, :], in_=b2.rearrange("(c p) -> c p", p=P))
+        for m in range(2, TILES):
+            nc.sync.dma_start(out=fbytes[m][:], in_=tokens(F_bytes, m))
 
         ident = const.tile([P, P], F32)
         make_identity(nc, ident[:])
@@ -92,124 +106,89 @@ def tile_nonlocalmp_pa_t_w4_kernel(tc, F_bytes, F_scale, W1_words, W1_scales, b1
         nc.vector.memset(twelves[:], 12.0)
         eights = const.tile([P, P], BF16)
         nc.vector.memset(eights[:], 8.0)
-        ident16 = const.tile([P, P], BF16)
-        nc.scalar.copy(out=ident16[:], in_=ident[:])
-        b1wide = const.tile([P, 4, P], BF16)
 
-        w1p = const.tile([P, 4, 2 * P], U8, align_bytes=64)
-        w1s = const.tile([P, 4, P], U8, align_bytes=64)
+        w1p = const.tile([P, 2, 4, 2 * P], U8, align_bytes=64)
+        w1s = const.tile([P, 2, 4, P], U8, align_bytes=64)
 
-        def permute_w1a():
+        def permute_words(g):
             nc.vector.tensor_copy(
-                out=w1p[:].rearrange("p t (m e) -> p t m e", e=2), in_=w1raw[:, 0, :].rearrange("p (m t e) -> p t m e", t=4, e=2)
+                out=w1p[:, g].rearrange("p t (m e) -> p t m e", e=2), in_=w1raw[:, g, :].rearrange("p (m t e) -> p t m e", t=4, e=2)
             )
 
-        def permute_w1a_scales():
-            nc.vector.tensor_copy(out=w1s[:], in_=w1sraw[:, 0, :].rearrange("p (m t) -> p t m", t=4))
+        def permute_scales(g):
+            nc.vector.tensor_copy(out=w1s[:, g], in_=w1sraw[:, g, :].rearrange("p (m t) -> p t m", t=4))
 
         fwide = const.tile([P, TILES, C], BF16, align_bytes=64)
-        fg = const.tile([P, TILES, P, 4], BF16, align_bytes=64)
-        fq = const.tile([P, TILES, P], I32, align_bytes=64)
-        fs = const.tile([P, TILES, P], U8, align_bytes=64)
-        bp = const.tile([P, NODES, SETS, 4], F32, align_bytes=64)
+        turned_of, grouped_of, fq_of = {}, {}, {}
 
         def widen(m, copy):
-            src = fbytes0[:, m * C : (m + 1) * C] if m < 4 else fbytes1[:, (m - 4) * C : (m - 3) * C]
-            copy(out=fwide[:, m, :], in_=src.bitcast(FP8))
+            copy(out=fwide[:, m, :], in_=fbytes[m][:].bitcast(FP8))
 
-        turned_of = {}
-
-        def turn_f(tiles, tag):
-            xt = ps.tile([P, len(tiles), 2, P], F32, name="xt", tag=tag, bufs=2)
-            for i, m in enumerate(tiles):
-                turned_of[m] = xt[:, i]
-                words = fwide[:, m, :].bitcast(F32)
-                for w in range(2):
-                    nc.tensor.transpose(xt[:, i, w, :], words[:, w::2], ident[:])
+        def turn_f(m, tag):
+            xt = ps.tile([P, 2, P], F32, name="xt", tag=tag)
+            turned_of[m] = xt
+            words = fwide[:, m, :].bitcast(F32)
+            for w in range(2):
+                nc.tensor.transpose(xt[:, w, :], words[:, w::2], ident[:])
 
         def scale_f(m):
-            sc = fsc[:].rearrange("p (o w e) -> p o w e", o=1, w=2).to_broadcast([P, SETS, 2, 2])
-            src = turned_of[m].bitcast(BF16).rearrange("p w (b side e) -> p side b w e", side=2, e=2)
-            for side in range(2):
-                to = fg[:, m, SETS * side : SETS * (side + 1), :].rearrange("p b (w e) -> p b w e", e=2)
-                nc.vector.tensor_tensor(out=to, in0=src[:, side], in1=sc, op=ALU.mult)
+            fg = work.tile([P, P, 2, 2], BF16, name="fg", bufs=2, align_bytes=64)
+            grouped_of[m] = fg
+            sc = fsc[:].rearrange("p (o w e) -> p o w e", o=1, w=2).to_broadcast([P, P, 2, 2])
+            nc.vector.tensor_tensor(out=fg[:], in0=turned_of[m][:].bitcast(BF16).rearrange("p w (n e) -> p n w e", e=2), in1=sc, op=ALU.mult)
 
-        def quantise_f(first, end):
-            tiles = slice(first, end)
-            nc.vector.quantize_mx(
-                out=fq[:, tiles, :].rearrange("p m r -> p (m r)").bitcast(FP8X4),
-                scales=fs[:, tiles, :].rearrange("p m r -> p (m r)"),
-                in_=fg[:, tiles].rearrange("p m r t -> p (m r t)"),
-            )
+        def quantise_f(m):
+            fq = work.tile([P, P], I32, name="fq", bufs=3, align_bytes=64)
+            fs = work.tile([P, P], U8, name="fs", bufs=3, align_bytes=64)
+            fq_of[m] = (fq, fs)
+            nc.vector.quantize_mx(out=fq[:].bitcast(FP8X4), scales=fs[:], in_=grouped_of[m][:].rearrange("p n w e -> p (n w e)"))
 
-        rows_of = {}
+        bank_of, a_of, b_of = {}, {}, {}
 
-        def sender_rows(q):
-            for m in (2 * q, 2 * q + 1):
-                bank = ps.tile([P, C], F32, name="bank", tag="message", bufs=3)
+        def first_product(m, g, tag):
+            fq, fs = fq_of[m]
+            bank = ps.tile([P, 4, P], F32, name="bank", tag=tag)
+            bank_of[m, g] = bank
+            for t in range(4):
                 nc.tensor.matmul_mx(
-                    out=bank[:],
-                    lhsT=fq[:, m, :].bitcast(FP8X4),
-                    lhsT_scale=fs[:, m, :],
-                    rhs=w1raw[:, 1, :].bitcast(FP4X4),
-                    rhs_scale=w1sraw[:, 1, :],
+                    out=bank[:, t, :],
+                    lhsT=w1p[:, g, t, :].bitcast(FP4X4),
+                    lhsT_scale=w1s[:, g, t, :],
+                    rhs=fq[:].bitcast(FP8X4),
+                    rhs_scale=fs[:],
                     start=True,
                     stop=True,
                 )
-                rows = work.tile([P, 4, P], F32, name="rows", bufs=2, align_bytes=64)
-                rows_of[m] = rows
-                nc.scalar.copy(out=rows[:], in_=bank[:].rearrange("r (p t) -> r t p", t=4))
 
-        def sender_columns(q):
-            for m in (2 * q, 2 * q + 1):
-                bank = ps.tile([P, 4, P], F32, name="bank", tag="message", bufs=3)
-                flat = bank[:].rearrange("p t r -> p (t r)")
-                nc.tensor.matmul(flat, lhsT=ident16[:], rhs=b1wide[:].rearrange("p t r -> p (t r)"), start=True, stop=False)
-                for t in range(4):
-                    nc.tensor.matmul(bank[:, t, :], lhsT=rows_of[m][:, t, :], rhs=ident[:], is_transpose=True, start=False, stop=(t == 3))
-                to = bp[:, 2 * m : 2 * m + 2, :, :].rearrange("p side b t -> p (side b) t")
-                nc.scalar.copy(out=to, in_=bank[:].rearrange("p t r -> p r t"))
+        def leave_receivers(m):
+            a = work.tile([P, P, 4], F32, name="a", bufs=2, align_bytes=64)
+            a_of[m] = a
+            nc.vector.tensor_tensor(
+                out=a[:], in0=bank_of[m, 0][:].rearrange("p t n -> p n t"), in1=b1raw[:].unsqueeze(1).to_broadcast([P, P, 4]), op=ALU.add
+            )
+
+        def copy_senders(m):
+            b = work.tile([P, P, 4], F32, name="b", bufs=2, align_bytes=64)
+            b_of[m] = b
+            nc.scalar.copy(out=b[:], in_=bank_of[m, 1][:].rearrange("p t n -> p n t"))
 
         b2c = const.tile([P, CHUNKS], F32)
         b2neg = const.tile([P, CHUNKS], F32)
 
         def turn_b2():
             nc.scalar.copy(out=b2f[0:CHUNKS, :], in_=b2raw[0:CHUNKS, :])
-            bt = ps.tile([P, P], F32, name="bt", tag="lin", bufs=2)
+            bt = ps.tile([P, P], F32, name="bt", tag="sum1")
             nc.tensor.transpose(bt[:], b2f[:], ident[:])
-            return bt
-
-        def leave_b2(bt):
             nc.scalar.copy(out=b2c[:], in_=bt[:, 0:CHUNKS])
             nc.scalar.activation(out=b2neg[:], in_=bt[:, 0:CHUNKS], func=ACT.Copy, scale=-1.0)
 
-        a_of, a_copy_of, h_of, part_of, hq_of, relu_of = {}, {}, {}, {}, {}, {}
+        h_of, part_of, hq_of, relu_of = {}, {}, {}, {}
         lin_of, sum_of, sum_bank_of, fifth_of = {}, {}, {}, {}
-
-        def receivers(m):
-            bank = ps.tile([P, 4, P], F32, name="bank", tag="a", bufs=1)
-            a_of[m] = bank
-            for t in range(4):
-                nc.tensor.matmul_mx(
-                    out=bank[:, t, :],
-                    lhsT=w1p[:, t, :].bitcast(FP4X4),
-                    lhsT_scale=w1s[:, t, :],
-                    rhs=fq[:, m, :].bitcast(FP8X4),
-                    rhs_scale=fs[:, m, :],
-                    start=True,
-                    stop=True,
-                )
-
-        def copy_receivers(m):
-            rest = work.tile([P, 2, WIDE, 4], F32, name="rest", bufs=2, align_bytes=64)
-            a_copy_of[m] = rest
-            nc.scalar.copy(out=rest[:], in_=a_of[m][:].rearrange("p t (side b) -> p side b t", side=2)[:, :, SETS - WIDE :, :])
-
-        v_all = const.tile([P, SENDERS, P + MOST, 4], F32, align_bytes=64)
+        v_all = const.tile([P, SENDERS, P + ROW, 4], F32, align_bytes=64)
 
         def v_of(unit):
-            first = MOST * (unit % 2)
-            return v_all[:, :, first : first + P, :]
+            start = ROW * (unit % 2)
+            return v_all[:, 0 : units[unit][2], start : start + P, :]
 
         def by_scalar(unit):
             width = scalar_columns(unit)
@@ -219,39 +198,39 @@ def tile_nonlocalmp_pa_t_w4_kernel(tc, F_bytes, F_scale, W1_words, W1_scales, b1
             width = scalar_columns(unit)
             return slice(width, P) if unit % 2 == 0 else slice(0, P - width)
 
-        def add(unit, side, sets):
-            m, q = divmod(unit, UNITS_A_TILE)
-            cols = slice(SETS * side, SETS * side + sets)
-            nc.vector.tensor_tensor(
-                out=v_of(unit)[:, :, cols, :],
-                in0=a_of[m][:].rearrange("p t r -> p r t")[:, cols, :].unsqueeze(1).to_broadcast([P, SENDERS, sets, 4]),
-                in1=bp[:, SENDERS * q : SENDERS * (q + 1), 0:sets, :],
+        def add(unit, engine, nodes, senders):
+            m, j, size = units[unit]
+            shape = [P, nodes.stop - nodes.start, size, GROUP, 4]
+            engine.tensor_tensor(
+                out=v_of(unit).rearrange("p j (i b) t -> p i j b t", b=GROUP)[:, nodes],
+                in0=senders[:, j : j + size].unsqueeze(1).to_broadcast(shape),
+                in1=a_of[m][:].rearrange("p (i b) t -> p i b t", b=GROUP)[:, nodes].unsqueeze(2).to_broadcast(shape),
                 op=ALU.add,
             )
 
-        def add_on_gpsimd(unit, side, sets):
-            m, q = divmod(unit, UNITS_A_TILE)
-            nc.gpsimd.tensor_tensor(
-                out=v_of(unit)[:, :, SETS * (side + 1) - sets : SETS * (side + 1), :],
-                in0=a_copy_of[m][:, side, WIDE - sets :].unsqueeze(1).to_broadcast([P, SENDERS, sets, 4]),
-                in1=bp[:, SENDERS * q : SENDERS * (q + 1), SETS - sets :, :],
-                op=ALU.add,
-            )
+        def adds(unit, columns):
+            m = units[unit][0]
+            share = columns // GROUP
+            mine, other = (slice(0, NODES - share), slice(NODES - share, NODES)) if unit % 2 == 0 else (slice(share, NODES), slice(0, share))
+            if share > 0:
+                add(unit, nc.gpsimd, other, b_of[m][:].rearrange("p (j b) t -> p j b t", b=GROUP))
+            add(unit, nc.vector, mine, bank_of[m, 1][:].rearrange("p t (j b) -> p j b t", b=GROUP))
 
         def scalar_part(unit, sign):
             width = scalar_columns(unit)
             if width == 0:
                 return
-            part = work.tile([P, SENDERS, width, 4], BF16, name="part", bufs=4, align_bytes=64)
+            part = work.tile([P, units[unit][2], width, 4], BF16, name="part", bufs=4, align_bytes=64)
             part_of[unit, sign] = part
             nc.scalar.activation(out=part[:], in_=v_of(unit)[:, :, by_scalar(unit), :], func=ACT.Relu, scale=(1.0, -SLOPE)[sign])
 
-        def leaky(unit):
-            tag, bufs = ("h_last", 1) if unit == LAST else ("h", 3)
-            h = work.tile([P, SENDERS, P, 4], BF16, name="h", tag=tag, bufs=bufs, align_bytes=64)
-            h_of[unit] = h
-            src = v_of(unit)[:, :, by_vector(unit), :].rearrange("p j r t -> p j (r t)")
-            to = h[:, :, by_vector(unit), :].rearrange("p j r t -> p j (r t)")
+        def leaky(unit, senders=slice(0, SENDERS)):
+            if senders.start == 0:
+                tag, bufs = ("h_last", 1) if unit == LAST else ("h", 3)
+                h = work.tile([P, units[unit][2], P, 4], BF16, name="h", tag=tag, bufs=bufs, align_bytes=64)
+                h_of[unit] = h
+            src = v_of(unit)[:, senders, by_vector(unit), :].rearrange("p j r t -> p j (r t)")
+            to = h_of[unit][:, senders, by_vector(unit), :].rearrange("p j r t -> p j (r t)")
             nc.vector.scalar_tensor_tensor(out=to, in0=src, scalar=SLOPE, in1=src, op0=ALU.mult, op1=ALU.max)
 
         def join(unit):
@@ -259,15 +238,19 @@ def tile_nonlocalmp_pa_t_w4_kernel(tc, F_bytes, F_scale, W1_words, W1_scales, b1
                 to = h_of[unit][:, :, by_scalar(unit), :]
                 nc.vector.tensor_tensor(out=to, in0=part_of[unit, 0][:], in1=part_of[unit, 1][:], op=ALU.subtract)
 
-        def quantise_h(unit):
-            hq = work.tile([P, SENDERS * P], I32, name="hq", align_bytes=64)
-            hs = work.tile([P, SENDERS * P], U8, name="hs", align_bytes=64)
-            hq_of[unit] = (hq, hs)
-            nc.vector.quantize_mx(out=hq[:].bitcast(FP8X4), scales=hs[:], in_=h_of[unit][:].rearrange("p j r t -> p (j r t)"))
+        def quantise_h(unit, senders=slice(0, SENDERS)):
+            if senders.start == 0:
+                hq = work.tile([P, SENDERS * P], I32, name="hq", bufs=HQ, align_bytes=64)
+                hs = work.tile([P, SENDERS * P], U8, name="hs", bufs=HQ, align_bytes=64)
+                hq_of[unit] = (hq, hs)
+            hq, hs = hq_of[unit]
+            cols = slice(P * senders.start, P * senders.stop)
+            nc.vector.quantize_mx(out=hq[:, cols].bitcast(FP8X4), scales=hs[:, cols], in_=h_of[unit][:, senders].rearrange("p j r t -> p (j r t)"))
 
         def message(unit, c, tag="message", bufs=3):
             hq, hs = hq_of[unit]
-            bank = ps.tile([P, SENDERS * P], F32, name="bank", tag=tag, bufs=bufs)
+            size = units[unit][2]
+            bank = ps.tile([P, size * P], F32, name="bank", tag=tag, bufs=bufs)
             nc.tensor.matmul_mx(
                 out=bank[:],
                 lhsT=w2[:, 2 * P * c : 2 * P * (c + 1)].bitcast(FP4X4),
@@ -277,20 +260,22 @@ def tile_nonlocalmp_pa_t_w4_kernel(tc, F_bytes, F_scale, W1_words, W1_scales, b1
                 start=True,
                 stop=True,
             )
-            relu = work.tile([P, SENDERS, P], F32, name="relu", bufs=10, align_bytes=64)
+            relu = work.tile([P, size, P], F32, name="relu", bufs=12, align_bytes=64)
             relu_of[unit, c] = relu
             flat = relu[:].rearrange("p j r -> p (j r)")
-            if unit == LAST or (unit == LAST - 1 and c >= 2):
+            if (unit == LAST and c != 1) or (unit == LAST - 1 and c >= 2):
                 before = relu_of[unit - 1, c][:].rearrange("p j r -> p (j r)")
                 nc.vector.scalar_tensor_tensor(out=flat, in0=bank[:], scalar=b2neg[:, c : c + 1], in1=before, op0=ALU.max, op1=ALU.add)
             else:
                 nc.scalar.activation(out=flat, in_=bank[:], func=ACT.Relu, bias=b2c[:, c : c + 1], scale=1.0)
 
         def linear(unit, j):
-            m, q = divmod(unit, UNITS_A_TILE)
+            m, j0, size = units[unit]
+            if j >= size:
+                return
             hq, hs = hq_of[unit]
-            if q == 0 and j == 0:
-                lin = ps.tile([P, C], F32, name="lin", tag="lin", bufs=2)
+            if j0 + j == 0:
+                lin = ps.tile([P, C], F32, name="lin", tag="ring%d" % (m % 3))
                 lin_of[m] = lin
             nc.tensor.matmul_mx(
                 out=lin_of[m][:],
@@ -298,24 +283,27 @@ def tile_nonlocalmp_pa_t_w4_kernel(tc, F_bytes, F_scale, W1_words, W1_scales, b1
                 lhsT_scale=hs[:, P * j : P * (j + 1)],
                 rhs=w2[:].bitcast(FP4X4),
                 rhs_scale=w2s[:],
-                start=(q == 0 and j == 0),
-                stop=(q == UNITS_A_TILE - 1 and j == SENDERS - 1),
+                start=(j0 + j == 0),
+                stop=(j0 + j == NODES - 1),
             )
 
         def open_sum(m, chunks, tag):
-            total = ps.tile([P, len(chunks), P], F32, name="total", tag=tag, bufs=2)
+            total = ps.tile([P, len(chunks), P], F32, name="total", tag=tag)
             for i, c in enumerate(chunks):
                 sum_of[m, c] = total[:, i, :]
             sum_bank_of[m, chunks[0]] = total
-            times = fours if m < TILES - 1 else eights if chunks[0] == 0 else twelves
+            if m == TILES - 1 and chunks[0] == 0:
+                nc.tensor.matmul(total[:, 0, :], lhsT=eights[:], rhs=b2row[:, 0:P], start=True, stop=False)
+                nc.tensor.matmul(total[:, 1, :], lhsT=fours[:], rhs=b2row[:, P : 2 * P], start=False, stop=False)
+                return
+            times = fours if m < TILES - 1 else twelves
             b2_part = b2row[:, P * chunks[0] : P * (chunks[-1] + 1)]
             nc.tensor.matmul(total[:].rearrange("p c r -> p (c r)"), lhsT=times[:], rhs=b2_part, start=True, stop=False)
 
-        def add_up(unit, c):
-            m, q = divmod(unit, UNITS_A_TILE)
-            closing_chunks = (1, 3) if m == TILES - 1 else (3,)
-            for j in range(SENDERS):
-                closes = q == UNITS_A_TILE - 1 and j == SENDERS - 1 and c in closing_chunks
+        def add_up(unit, c, closing=False):
+            m, j0, size = units[unit]
+            for j in range(size):
+                closes = closing and j == size - 1
                 nc.tensor.matmul(sum_of[m, c], lhsT=relu_of[unit, c][:, j, :], rhs=ident[:], is_transpose=True, start=False, stop=closes)
 
         def leave_linear(m):
@@ -323,21 +311,18 @@ def tile_nonlocalmp_pa_t_w4_kernel(tc, F_bytes, F_scale, W1_words, W1_scales, b1
             fifth_of[m] = fifth
             nc.scalar.activation(out=fifth[:], in_=lin_of[m][:], func=ACT.Copy, scale=SLOPE)
 
-        out_v = out.rearrange("b (side m) c -> m side b c", side=2)
-
-        def finish(m, first, end, queues):
-            cols = slice(P * first, P * end)
-            st = work.tile([P, P * (end - first)], F32, name="st", bufs=2)
+        def finish(m, start, end, queue):
+            cols = slice(P * start, P * end)
+            st = work.tile([P, P * (end - start)], F32, name="st", bufs=2)
             nc.vector.scalar_tensor_tensor(
                 out=st[:],
-                in0=sum_bank_of[m, first][:].rearrange("p c r -> p (c r)"),
+                in0=sum_bank_of[m, start][:].rearrange("p c r -> p (c r)"),
                 scalar=1.0 - SLOPE,
                 in1=fifth_of[m][:, cols],
                 op0=ALU.mult,
                 op1=ALU.add,
             )
-            for side in range(2):
-                queues[side].dma_start(out=out_v[m, side][:, cols], in_=st[SETS * side : SETS * (side + 1), :])
+            queue.dma_start(out=tokens(out, m)[:, :, cols], in_=st[:])
 
         def warm_up(count):
             idle = ps.tile([P, C], F32, name="idle", tag="message", bufs=3)
@@ -346,121 +331,135 @@ def tile_nonlocalmp_pa_t_w4_kernel(tc, F_bytes, F_scale, W1_words, W1_scales, b1
 
         warm_up(4)
         widen(0, nc.vector.tensor_copy)
-        for m in range(1, TILES - 1):
-            widen(m, nc.scalar.copy)
-        nc.scalar.copy(out=b1wide[:], in_=b1raw[:].unsqueeze(2).to_broadcast([P, 4, P]))
-        turn_f([0], "sum")
-        turn_f([1], "lin")
-        warm_up(2)
-        turn_f([2, 3], "sum")
-        warm_up(2)
+        widen(1, nc.scalar.copy)
+        turn_f(0, "sum1")
+        warm_up(4)
         nc.sync.dma_start(out=b2row[0:1, :], in_=b2.rearrange("(o c) -> o c", o=1))
-        permute_w1a()
+        permute_words(0)
         scale_f(0)
-        scale_f(1)
-        permute_w1a_scales()
-        quantise_f(0, 2)
-        scale_f(2)
-        scale_f(3)
-        turn_f([4, 5], "sum")
-        sender_rows(0)
-        receivers(0)
-        widen(TILES - 1, nc.vector.tensor_copy)
-        quantise_f(2, 4)
-        copy_receivers(0)
-        sender_columns(0)
-        turn_f([6, 7], "lin")
-        sender_rows(1)
-        sender_columns(1)
-        scale_f(4)
-        scale_f(5)
-        quantise_f(4, 6)
+        permute_scales(0)
+        quantise_f(0)
+        permute_words(1)
+        permute_scales(1)
+        first_product(0, 0, "ring2")
+        first_product(0, 1, "ring1")
+        resident = bank_of[0, 1]
+        first_product(0, 1, "sum1")
+        copy_senders(0)
+        bank_of[0, 1] = resident
+        turn_f(1, "ring0")
+        leave_receivers(0)
+        turn_b2()
+        widen(2, nc.scalar.copy)
+        turn_f(2, "sum0")
 
-        for step in range(UNITS):
+        closed = {last[m] + LAG + 2: m for m in range(TILES - 1)}
+        scaled = {first[m] + 2: m + 2 for m in range(TILES - 2)}
+        scaled[0] = 1
+        received = {first[m] + 1: m + 1 for m in range(TILES - 1)}
+        LOW, HIGH = slice(0, SENDERS // 2), slice(SENDERS // 2, SENDERS)
+        extra_product = None
+        for step in range(LAST + 1):
             behind = step - LAG
-            tile, place = divmod(step, UNITS_A_TILE)
-            whole, shared = step % 2, 1 - step % 2
-            sets = WIDE if finishes_tile(step) or step == 0 else SHARE
-            add_on_gpsimd(step, shared, sets)
-            add(step, whole, SETS)
-            add(step, shared, SETS - sets)
-            if finishes_tile(step):
-                finish(tile - 1, 0, CHUNKS, (nc.sync, nc.sync))
-            if step == 0:
-                scale_f(6)
-                scale_f(7)
-            if behind >= 0:
-                message(behind, 0)
+            tile = units[step][0] if step <= LAST else TILES
+            if step <= LAST:
+                adds(step, FIRST_SHARE if step == 0 else WIDE if step in scaled or step in received or step in closed else SHARE)
+            if step in scaled:
+                scale_f(scaled[step])
+            if step in received:
+                leave_receivers(received[step])
+            if step in closed:
+                finish(closed[step], 0, CHUNKS, nc.sync)
+            live = 0 <= behind <= LAST
+            ends_tile = tile + 1 < TILES and step == last[tile]
+            if ends_tile:
+                first_product(tile + 1, 1, "ring%d" % ((tile + 2) % 3))
+                copy_senders(tile + 1)
+            if live:
+                for c in range(AHEAD):
+                    message(behind, c)
+                if behind >= 1:
+                    linear(behind - 1, 2)
+                    linear(behind - 1, 3)
+                if extra_product is not None:
+                    first_product(*extra_product)
+                for c in range(AHEAD, 3):
+                    message(behind, c)
                 linear(behind, 0)
-                message(behind, 1)
-                message(behind, 2)
                 linear(behind, 1)
                 message(behind, 3)
-            opens_tile = behind >= 0 and behind % UNITS_A_TILE == 0
-            if opens_tile and tile > 0:
-                leave_linear(tile - 1)
-            if place == UNITS_A_TILE - 1 and tile + 1 < TILES:
-                receivers(tile + 1)
-                copy_receivers(tile + 1)
-            senders_to_come = step + 2 < UNITS_A_TILE
-            if senders_to_come:
-                sender_rows(step + 2)
-            scalar_part(step, 0)
-            if senders_to_come:
-                sender_columns(step + 2)
-            if step == 0:
-                b2_bank = turn_b2()
-            scalar_part(step, 1)
-            if step == 0:
-                leave_b2(b2_bank)
-            if opens_tile:
-                open_sum(tile, (0, 1) if tile == TILES - 1 else (0, 1, 2, 3), "sum")
+            extra_product = None
+            if behind >= 1 and behind - 1 in last.values():
+                leave_linear(units[behind - 1][0])
+            if step <= LAST:
+                scalar_part(step, 0)
+                scalar_part(step, 1)
+            if step < LAG:
+                for m in range(3 + 3 * step, min(TILES, 6 + 3 * step)):
+                    widen(m, nc.scalar.copy)
             if step == LAST:
-                open_sum(tile, (2, 3), "lin")
+                open_sum(tile, (2, 3), "ring%d" % ((tile - 1) % 3))
             if behind >= 1:
                 add_up(behind - 1, 2)
-                add_up(behind - 1, 3)
-            if behind >= 0:
+                add_up(behind - 1, 3, behind - 1 in last.values())
+            if live:
+                if units[behind][1] == 0:
+                    open_sum(tile, (0, 1) if tile == TILES - 1 else (0, 1, 2, 3), "sum%d" % (tile % 2))
                 if behind < LAST - CHAINED:
                     add_up(behind, 0)
                     add_up(behind, 1)
-                linear(behind, 2)
-                linear(behind, 3)
-            if step >= 1:
+            if ends_tile and tile + 3 < TILES:
+                turn_f(tile + 3, "sum%d" % ((tile + 1) % 2))
+            if ends_tile and tile + 2 < TILES:
+                extra_product = (tile + 2, 0, "ring%d" % ((tile + 1) % 3))
+            if 1 <= step <= LAST + 1:
                 join(step - 1)
-            if step == LAST:
+            if step in scaled and step > 0:
+                quantise_f(scaled[step])
+            if step < LAST - 1:
+                leaky(step)
+                if step == 0:
+                    quantise_f(1)
+                    first_product(1, 0, "ring0")
+                else:
+                    quantise_h(step - 1)
+            elif step == LAST - 1:
+                leaky(step, LOW)
                 quantise_h(step - 1)
-            leaky(step)
-            if step == 0:
-                quantise_f(6, TILES)
-            if 1 <= step < LAST:
-                quantise_h(step - 1)
+                leaky(step, HIGH)
+                quantise_h(step, LOW)
+            else:
+                quantise_h(step - 1, HIGH)
+                leaky(step, LOW)
+                leaky(step, HIGH)
+                quantise_h(step, LOW)
+                quantise_h(step, HIGH)
 
         def add_pair(c):
             both = work.tile([P, SENDERS, P], F32, name="both", tag=("h_last", "both")[c], bufs=1, align_bytes=64)
             nc.gpsimd.tensor_tensor(out=both[:], in0=relu_of[LAST - 2, c][:], in1=relu_of[LAST - 1, c][:], op=ALU.add)
             relu_of[LAST - 1, c] = both
 
-        finish(TILES - 2, 0, CHUNKS, (nc.sync, nc.sync))
-        quantise_h(LAST)
         message(LAST - 1, 0)
         message(LAST - 1, 1)
+        linear(LAST - 2, 2)
+        linear(LAST - 2, 3)
         add_pair(0)
         add_pair(1)
         message(LAST - 1, 2)
-        message(LAST - 1, 3, "a", 1)
+        message(LAST - 1, 3, "ring%d" % (TILES % 3), 1)
         for j in range(SENDERS):
             linear(LAST - 1, j)
-        message(LAST, 2)
-        message(LAST, 3)
-        message(LAST, 0)
-        linear(LAST, 0)
-        linear(LAST, 1)
-        message(LAST, 1)
-        linear(LAST, 2)
-        linear(LAST, 3)
+        for c in (2, 3, 1):
+            message(LAST, c)
+        message(LAST, 0, "sum%d" % (TILES % 2), 1)
+        for j in range(SENDERS):
+            linear(LAST, j)
         leave_linear(TILES - 1)
-        for c in (2, 3, 0, 1):
-            add_up(LAST, c)
-            if c % 2 == 1:
-                finish(TILES - 1, c - 1, c + 1, (nc.sync, nc.scalar))
+        add_up(LAST, 2)
+        add_up(LAST, 3, True)
+        finish(TILES - 1, 2, 4, nc.sync)
+        add_up(LAST, 1)
+        add_up(LAST, 0)
+        add_up(LAST - 1, 1, True)
+        finish(TILES - 1, 0, 2, nc.scalar)

@@ -26,13 +26,13 @@ LAG = 2
 
 FIRST_TILE = (4, 4, 4, 4)
 LAST_TILE = (4, 4, 4, 4)
-MOST = 44
+MOST = 46
 EARLY = 64
 EARLY_UNITS = 2
 CHAINED = 2
 LATE = (0, 0)
 WIDE = 48
-SHARE = 32
+SHARE = 40
 AHEAD = 2
 FIRST_SHARE = 24
 HQ = 3

@@ -26,7 +26,7 @@ LAG = 2
 
 FIRST_TILE = (4, 4, 4, 4)
 LAST_TILE = (4, 4, 4, 4)
-MOST = 46
+MOST = 47
 EARLY = 64
 EARLY_UNITS = 2
 CHAINED = 2
@@ -36,6 +36,11 @@ SHARE = 40
 AHEAD = 2
 FIRST_SHARE = 24
 HQ = 3
+FOURTH = 1
+DELAY = 0
+WARM = 3
+LATE_FINISH = 0
+LAST_TILE_MOST = 47
 
 
 def tile_nonlocalmp_pa_t_w4_kernel(tc, F_bytes, F_scale, W1_words, W1_scales, b1, W2_words, W2_scales, b2, out):
@@ -53,6 +58,8 @@ def tile_nonlocalmp_pa_t_w4_kernel(tc, F_bytes, F_scale, W1_words, W1_scales, b1
     def scalar_columns(unit):
         if unit > LAST - CHAINED:
             return LATE[unit - LAST + CHAINED - 1]
+        if unit >= first[TILES - 1]:
+            return LAST_TILE_MOST
         return EARLY if unit < EARLY_UNITS else MOST
 
     with ExitStack() as ctx:
@@ -329,18 +336,18 @@ def tile_nonlocalmp_pa_t_w4_kernel(tc, F_bytes, F_scale, W1_words, W1_scales, b1
             for i in range(count):
                 nc.tensor.matmul(idle[:], lhsT=fours[:], rhs=b2row[:], start=True, stop=True)
 
-        warm_up(4)
+        warm_up(WARM)
         widen(0, nc.vector.tensor_copy)
         widen(1, nc.scalar.copy)
         turn_f(0, "sum1")
         warm_up(4)
         nc.sync.dma_start(out=b2row[0:1, :], in_=b2.rearrange("(o c) -> o c", o=1))
         permute_words(0)
-        scale_f(0)
         permute_scales(0)
+        scale_f(0)
+        permute_scales(1)
         quantise_f(0)
         permute_words(1)
-        permute_scales(1)
         first_product(0, 0, "ring2")
         first_product(0, 1, "ring1")
         resident = bank_of[0, 1]
@@ -353,7 +360,7 @@ def tile_nonlocalmp_pa_t_w4_kernel(tc, F_bytes, F_scale, W1_words, W1_scales, b1
         widen(2, nc.scalar.copy)
         turn_f(2, "sum0")
 
-        closed = {last[m] + LAG + 2: m for m in range(TILES - 1)}
+        closed = {min(LAST, last[m] + LAG + 2 + DELAY): m for m in range(TILES - 1 - LATE_FINISH)}
         scaled = {first[m] + 2: m + 2 for m in range(TILES - 2)}
         scaled[0] = 1
         received = {first[m] + 1: m + 1 for m in range(TILES - 1)}
@@ -381,13 +388,18 @@ def tile_nonlocalmp_pa_t_w4_kernel(tc, F_bytes, F_scale, W1_words, W1_scales, b1
                 if behind >= 1:
                     linear(behind - 1, 2)
                     linear(behind - 1, 3)
-                if extra_product is not None:
-                    first_product(*extra_product)
                 for c in range(AHEAD, 3):
                     message(behind, c)
+                if FOURTH == 0:
+                    message(behind, 3)
                 linear(behind, 0)
+                if FOURTH == 1:
+                    message(behind, 3)
+                if extra_product is not None:
+                    first_product(*extra_product)
                 linear(behind, 1)
-                message(behind, 3)
+                if FOURTH == 2:
+                    message(behind, 3)
             extra_product = None
             if behind >= 1 and behind - 1 in last.values():
                 leave_linear(units[behind - 1][0])
@@ -408,8 +420,10 @@ def tile_nonlocalmp_pa_t_w4_kernel(tc, F_bytes, F_scale, W1_words, W1_scales, b1
                 if behind < LAST - CHAINED:
                     add_up(behind, 0)
                     add_up(behind, 1)
-            if ends_tile and tile + 3 < TILES:
+            if DELAY == 0 and ends_tile and tile + 3 < TILES:
                 turn_f(tile + 3, "sum%d" % ((tile + 1) % 2))
+            if DELAY == 1 and step == first[tile] and 1 <= tile < TILES - 2:
+                turn_f(tile + 2, "sum%d" % (tile % 2))
             if ends_tile and tile + 2 < TILES:
                 extra_product = (tile + 2, 0, "ring%d" % ((tile + 1) % 3))
             if 1 <= step <= LAST + 1:
@@ -440,10 +454,10 @@ def tile_nonlocalmp_pa_t_w4_kernel(tc, F_bytes, F_scale, W1_words, W1_scales, b1
             nc.gpsimd.tensor_tensor(out=both[:], in0=relu_of[LAST - 2, c][:], in1=relu_of[LAST - 1, c][:], op=ALU.add)
             relu_of[LAST - 1, c] = both
 
-        message(LAST - 1, 0)
-        message(LAST - 1, 1)
         linear(LAST - 2, 2)
         linear(LAST - 2, 3)
+        message(LAST - 1, 0)
+        message(LAST - 1, 1)
         add_pair(0)
         add_pair(1)
         message(LAST - 1, 2)
@@ -452,9 +466,16 @@ def tile_nonlocalmp_pa_t_w4_kernel(tc, F_bytes, F_scale, W1_words, W1_scales, b1
             linear(LAST - 1, j)
         for c in (2, 3, 1):
             message(LAST, c)
-        message(LAST, 0, "sum%d" % (TILES % 2), 1)
-        for j in range(SENDERS):
-            linear(LAST, j)
+        if LATE_FINISH:
+            linear(LAST, 0)
+            message(LAST, 0, "ring%d" % (TILES % 3), 1)
+            for j in range(1, SENDERS):
+                linear(LAST, j)
+            finish(TILES - 2, 0, CHUNKS, nc.sync)
+        else:
+            message(LAST, 0, "sum%d" % (TILES % 2), 1)
+            for j in range(SENDERS):
+                linear(LAST, j)
         leave_linear(TILES - 1)
         add_up(LAST, 2)
         add_up(LAST, 3, True)

@@ -343,11 +343,11 @@ def tile_nonlocalmp_pa_t_w4_kernel(tc, F_bytes, F_scale, W1_words, W1_scales, b1
         warm_up(4)
         nc.sync.dma_start(out=b2row[0:1, :], in_=b2.rearrange("(o c) -> o c", o=1))
         permute_words(0)
-        permute_scales(0)
         scale_f(0)
-        permute_scales(1)
+        permute_scales(0)
         quantise_f(0)
         permute_words(1)
+        permute_scales(1)
         first_product(0, 0, "ring2")
         first_product(0, 1, "ring1")
         resident = bank_of[0, 1]

@@ -21,52 +21,43 @@ FLOPS = 2 * SETS * NODES * C * 2 * C + 2 * SETS * NODES * NODES * C * C
 GROUP = P // NODES
 TILES = SETS // GROUP
 SENDERS = 4
+PLACES = NODES // SENDERS
+LAST = TILES * PLACES - 1
 CHUNKS = C // P
 LAG = 2
+RECEIVERS, SENDING = 0, 1
+LOW, HIGH, ALL = slice(0, SENDERS // 2), slice(SENDERS // 2, SENDERS), slice(0, SENDERS)
 
-FIRST_TILE = (4, 4, 4, 4)
-LAST_TILE = (4, 4, 4, 4)
-MOST = 47
-EARLY = 64
-EARLY_UNITS = 2
-CHAINED = 2
-LATE = (0, 0)
-WIDE = 48
 SHARE = 40
-AHEAD = 2
+WIDE = 48
 FIRST_SHARE = 24
-HQ = 3
-FOURTH = 1
-DELAY = 0
-WARM = 3
-LATE_FINISH = 0
-LAST_TILE_MOST = 47
+MOST = 50
+FEWER = 42
+EARLY = 64
+CHAINED = 2
+
+
+def scalar_columns(unit):
+    if unit < LAG:
+        return EARLY
+    if unit > LAST - CHAINED:
+        return 0
+    return FEWER if unit % PLACES == PLACES - 1 else MOST
 
 
 def tile_nonlocalmp_pa_t_w4_kernel(tc, F_bytes, F_scale, W1_words, W1_scales, b1, W2_words, W2_scales, b2, out):
     nc = tc.nc
-    units, first, last = [], {}, {}
-    for m in range(TILES):
-        sizes = FIRST_TILE if m == 0 else LAST_TILE if m == TILES - 1 else (SENDERS,) * (NODES // SENDERS)
-        first[m] = len(units)
-        for n, size in enumerate(sizes):
-            units.append((m, sum(sizes[:n]), size))
-        last[m] = len(units) - 1
-    LAST = len(units) - 1
-    ROW = max(MOST, EARLY)
-
-    def scalar_columns(unit):
-        if unit > LAST - CHAINED:
-            return LATE[unit - LAST + CHAINED - 1]
-        if unit >= first[TILES - 1]:
-            return LAST_TILE_MOST
-        return EARLY if unit < EARLY_UNITS else MOST
-
     with ExitStack() as ctx:
         ctx.enter_context(tc.manual_schedule())
         const = ctx.enter_context(tc.tile_pool(name="const", bufs=1))
         work = ctx.enter_context(tc.tile_pool(name="work", bufs=3))
         ps = ctx.enter_context(tc.psum_pool(name="ps", bufs=1))
+
+        def sum_bank(m):
+            return "sum%d" % (m % 2)
+
+        def ring_bank(m):
+            return "ring%d" % (m % 3)
 
         def tokens(dram, m):
             return dram[GROUP * m : GROUP * (m + 1)].rearrange("b i c -> i b c")
@@ -77,7 +68,7 @@ def tile_nonlocalmp_pa_t_w4_kernel(tc, F_bytes, F_scale, W1_words, W1_scales, b1
             fbytes.append(fb)
         nc.sync.dma_start(out=fbytes[0][:], in_=tokens(F_bytes, 0))
         w1raw = const.tile([P, 2, 2 * C], U8, align_bytes=64)
-        nc.sync.dma_start(out=w1raw[:, 0, :].bitcast(I32), in_=W1_words[0].bitcast(I32))
+        nc.sync.dma_start(out=w1raw[:, RECEIVERS, :].bitcast(I32), in_=W1_words[RECEIVERS].bitcast(I32))
         fsc = const.tile([P, 4], F32)
         nc.sync.dma_start(out=fsc[:], in_=F_scale.rearrange("a c (p t) -> p (a c t)", t=4))
         w1sraw = const.tile([P, 2, C], U8, align_bytes=64)
@@ -92,7 +83,7 @@ def tile_nonlocalmp_pa_t_w4_kernel(tc, F_bytes, F_scale, W1_words, W1_scales, b1
         w2s_src = W2_scales.rearrange("g (q r) n -> r q (g n)", r=4)
         for row in range(4):
             nc.sync.dma_start(out=w1sraw[row:P:32, :, :].bitcast(I32), in_=w1s_src[row].bitcast(I32))
-        nc.sync.dma_start(out=w1raw[:, 1, :].bitcast(I32), in_=W1_words[1].bitcast(I32))
+        nc.sync.dma_start(out=w1raw[:, SENDING, :].bitcast(I32), in_=W1_words[SENDING].bitcast(I32))
         b1raw = const.tile([P, 4], BF16)
         nc.sync.dma_start(out=b1raw[:], in_=b1.rearrange("(p t) -> p t", t=4))
         nc.sync.dma_start(out=fbytes[1][:], in_=tokens(F_bytes, 1))
@@ -117,16 +108,27 @@ def tile_nonlocalmp_pa_t_w4_kernel(tc, F_bytes, F_scale, W1_words, W1_scales, b1
         w1p = const.tile([P, 2, 4, 2 * P], U8, align_bytes=64)
         w1s = const.tile([P, 2, 4, P], U8, align_bytes=64)
 
-        def permute_words(g):
+        def permute_words(half):
             nc.vector.tensor_copy(
-                out=w1p[:, g].rearrange("p t (m e) -> p t m e", e=2), in_=w1raw[:, g, :].rearrange("p (m t e) -> p t m e", t=4, e=2)
+                out=w1p[:, half].rearrange("p t (m e) -> p t m e", e=2),
+                in_=w1raw[:, half, :].rearrange("p (m t e) -> p t m e", t=4, e=2),
             )
 
-        def permute_scales(g):
-            nc.vector.tensor_copy(out=w1s[:, g], in_=w1sraw[:, g, :].rearrange("p (m t) -> p t m", t=4))
+        def permute_scales(half):
+            nc.vector.tensor_copy(out=w1s[:, half], in_=w1sraw[:, half, :].rearrange("p (m t) -> p t m", t=4))
+
+        b2c = const.tile([P, CHUNKS], F32)
+        b2neg = const.tile([P, CHUNKS], F32)
+
+        def turn_b2():
+            nc.scalar.copy(out=b2f[0:CHUNKS, :], in_=b2raw[0:CHUNKS, :])
+            bt = ps.tile([P, P], F32, name="bt", tag=sum_bank(1))
+            nc.tensor.transpose(bt[:], b2f[:], ident[:])
+            nc.scalar.copy(out=b2c[:], in_=bt[:, 0:CHUNKS])
+            nc.scalar.activation(out=b2neg[:], in_=bt[:, 0:CHUNKS], func=ACT.Copy, scale=-1.0)
 
         fwide = const.tile([P, TILES, C], BF16, align_bytes=64)
-        turned_of, grouped_of, fq_of = {}, {}, {}
+        turned_of, grouped_of, fq_of, a_of, b_of = {}, {}, {}, {}, {}
 
         def widen(m, copy):
             copy(out=fwide[:, m, :], in_=fbytes[m][:].bitcast(FP8))
@@ -142,60 +144,57 @@ def tile_nonlocalmp_pa_t_w4_kernel(tc, F_bytes, F_scale, W1_words, W1_scales, b1
             fg = work.tile([P, P, 2, 2], BF16, name="fg", bufs=2, align_bytes=64)
             grouped_of[m] = fg
             sc = fsc[:].rearrange("p (o w e) -> p o w e", o=1, w=2).to_broadcast([P, P, 2, 2])
-            nc.vector.tensor_tensor(out=fg[:], in0=turned_of[m][:].bitcast(BF16).rearrange("p w (n e) -> p n w e", e=2), in1=sc, op=ALU.mult)
+            src = turned_of[m][:].bitcast(BF16).rearrange("p w (n e) -> p n w e", e=2)
+            nc.vector.tensor_tensor(out=fg[:], in0=src, in1=sc, op=ALU.mult)
 
         def quantise_f(m):
-            fq = work.tile([P, P], I32, name="fq", bufs=3, align_bytes=64)
-            fs = work.tile([P, P], U8, name="fs", bufs=3, align_bytes=64)
+            fq = work.tile([P, P], I32, name="fq", align_bytes=64)
+            fs = work.tile([P, P], U8, name="fs", align_bytes=64)
             fq_of[m] = (fq, fs)
             nc.vector.quantize_mx(out=fq[:].bitcast(FP8X4), scales=fs[:], in_=grouped_of[m][:].rearrange("p n w e -> p (n w e)"))
 
-        bank_of, a_of, b_of = {}, {}, {}
-
-        def first_product(m, g, tag):
+        def first_product(m, half, tag):
             fq, fs = fq_of[m]
             bank = ps.tile([P, 4, P], F32, name="bank", tag=tag)
-            bank_of[m, g] = bank
             for t in range(4):
                 nc.tensor.matmul_mx(
                     out=bank[:, t, :],
-                    lhsT=w1p[:, g, t, :].bitcast(FP4X4),
-                    lhsT_scale=w1s[:, g, t, :],
+                    lhsT=w1p[:, half, t, :].bitcast(FP4X4),
+                    lhsT_scale=w1s[:, half, t, :],
                     rhs=fq[:].bitcast(FP8X4),
                     rhs_scale=fs[:],
                     start=True,
                     stop=True,
                 )
+            return bank
+
+        a_bank_of, b_bank_of = {}, {}
+
+        def receivers(m):
+            a_bank_of[m] = first_product(m, RECEIVERS, ring_bank(m - 1))
+
+        def senders(m):
+            b_bank_of[m] = first_product(m, SENDING, ring_bank(m + 1))
 
         def leave_receivers(m):
             a = work.tile([P, P, 4], F32, name="a", bufs=2, align_bytes=64)
             a_of[m] = a
-            nc.vector.tensor_tensor(
-                out=a[:], in0=bank_of[m, 0][:].rearrange("p t n -> p n t"), in1=b1raw[:].unsqueeze(1).to_broadcast([P, P, 4]), op=ALU.add
-            )
+            bias = b1raw[:].unsqueeze(1).to_broadcast([P, P, 4])
+            nc.vector.tensor_tensor(out=a[:], in0=a_bank_of[m][:].rearrange("p t n -> p n t"), in1=bias, op=ALU.add)
 
-        def copy_senders(m):
+        def copy_senders(m, bank):
             b = work.tile([P, P, 4], F32, name="b", bufs=2, align_bytes=64)
             b_of[m] = b
-            nc.scalar.copy(out=b[:], in_=bank_of[m, 1][:].rearrange("p t n -> p n t"))
-
-        b2c = const.tile([P, CHUNKS], F32)
-        b2neg = const.tile([P, CHUNKS], F32)
-
-        def turn_b2():
-            nc.scalar.copy(out=b2f[0:CHUNKS, :], in_=b2raw[0:CHUNKS, :])
-            bt = ps.tile([P, P], F32, name="bt", tag="sum1")
-            nc.tensor.transpose(bt[:], b2f[:], ident[:])
-            nc.scalar.copy(out=b2c[:], in_=bt[:, 0:CHUNKS])
-            nc.scalar.activation(out=b2neg[:], in_=bt[:, 0:CHUNKS], func=ACT.Copy, scale=-1.0)
+            nc.scalar.copy(out=b[:], in_=bank[:].rearrange("p t n -> p n t"))
 
         h_of, part_of, hq_of, relu_of = {}, {}, {}, {}
-        lin_of, sum_of, sum_bank_of, fifth_of = {}, {}, {}, {}
-        v_all = const.tile([P, SENDERS, P + ROW, 4], F32, align_bytes=64)
+        lin_of, sum_of, total_of, fifth_of = {}, {}, {}, {}
+
+        v_all = const.tile([P, SENDERS, P + EARLY, 4], F32, align_bytes=64)
 
         def v_of(unit):
-            start = ROW * (unit % 2)
-            return v_all[:, 0 : units[unit][2], start : start + P, :]
+            start = EARLY * (unit % 2)
+            return v_all[:, :, start : start + P, :]
 
         def by_scalar(unit):
             width = scalar_columns(unit)
@@ -205,59 +204,58 @@ def tile_nonlocalmp_pa_t_w4_kernel(tc, F_bytes, F_scale, W1_words, W1_scales, b1
             width = scalar_columns(unit)
             return slice(width, P) if unit % 2 == 0 else slice(0, P - width)
 
-        def add(unit, engine, nodes, senders):
-            m, j, size = units[unit]
-            shape = [P, nodes.stop - nodes.start, size, GROUP, 4]
+        def add(unit, engine, nodes, bp):
+            m, place = divmod(unit, PLACES)
+            shape = [P, nodes.stop - nodes.start, SENDERS, GROUP, 4]
             engine.tensor_tensor(
                 out=v_of(unit).rearrange("p j (i b) t -> p i j b t", b=GROUP)[:, nodes],
-                in0=senders[:, j : j + size].unsqueeze(1).to_broadcast(shape),
+                in0=bp[:, SENDERS * place : SENDERS * (place + 1)].unsqueeze(1).to_broadcast(shape),
                 in1=a_of[m][:].rearrange("p (i b) t -> p i b t", b=GROUP)[:, nodes].unsqueeze(2).to_broadcast(shape),
                 op=ALU.add,
             )
 
         def adds(unit, columns):
-            m = units[unit][0]
-            share = columns // GROUP
-            mine, other = (slice(0, NODES - share), slice(NODES - share, NODES)) if unit % 2 == 0 else (slice(share, NODES), slice(0, share))
-            if share > 0:
-                add(unit, nc.gpsimd, other, b_of[m][:].rearrange("p (j b) t -> p j b t", b=GROUP))
-            add(unit, nc.vector, mine, bank_of[m, 1][:].rearrange("p t (j b) -> p j b t", b=GROUP))
+            m = unit // PLACES
+            cut = NODES - columns // GROUP if unit % 2 == 0 else columns // GROUP
+            below, above = slice(0, cut), slice(cut, NODES)
+            for_vector, for_gpsimd = (below, above) if unit % 2 == 0 else (above, below)
+            add(unit, nc.gpsimd, for_gpsimd, b_of[m][:].rearrange("p (j b) t -> p j b t", b=GROUP))
+            add(unit, nc.vector, for_vector, b_bank_of[m][:].rearrange("p t (j b) -> p j b t", b=GROUP))
 
-        def scalar_part(unit, sign):
+        def scalar_parts(unit):
             width = scalar_columns(unit)
-            if width == 0:
-                return
-            part = work.tile([P, units[unit][2], width, 4], BF16, name="part", bufs=4, align_bytes=64)
-            part_of[unit, sign] = part
-            nc.scalar.activation(out=part[:], in_=v_of(unit)[:, :, by_scalar(unit), :], func=ACT.Relu, scale=(1.0, -SLOPE)[sign])
+            if width > 0:
+                for factor in (1.0, -SLOPE):
+                    part = work.tile([P, SENDERS, width, 4], BF16, name="part", bufs=4, align_bytes=64)
+                    part_of[unit, factor] = part
+                    nc.scalar.activation(out=part[:], in_=v_of(unit)[:, :, by_scalar(unit), :], func=ACT.Relu, scale=factor)
 
-        def leaky(unit, senders=slice(0, SENDERS)):
-            if senders.start == 0:
+        def leaky(unit, which=ALL):
+            if which.start == 0:
                 tag, bufs = ("h_last", 1) if unit == LAST else ("h", 3)
-                h = work.tile([P, units[unit][2], P, 4], BF16, name="h", tag=tag, bufs=bufs, align_bytes=64)
+                h = work.tile([P, SENDERS, P, 4], BF16, name="h", tag=tag, bufs=bufs, align_bytes=64)
                 h_of[unit] = h
-            src = v_of(unit)[:, senders, by_vector(unit), :].rearrange("p j r t -> p j (r t)")
-            to = h_of[unit][:, senders, by_vector(unit), :].rearrange("p j r t -> p j (r t)")
+            src = v_of(unit)[:, which, by_vector(unit), :].rearrange("p j r t -> p j (r t)")
+            to = h_of[unit][:, which, by_vector(unit), :].rearrange("p j r t -> p j (r t)")
             nc.vector.scalar_tensor_tensor(out=to, in0=src, scalar=SLOPE, in1=src, op0=ALU.mult, op1=ALU.max)
 
         def join(unit):
             if scalar_columns(unit) > 0:
                 to = h_of[unit][:, :, by_scalar(unit), :]
-                nc.vector.tensor_tensor(out=to, in0=part_of[unit, 0][:], in1=part_of[unit, 1][:], op=ALU.subtract)
+                nc.vector.tensor_tensor(out=to, in0=part_of[unit, 1.0][:], in1=part_of[unit, -SLOPE][:], op=ALU.subtract)
 
-        def quantise_h(unit, senders=slice(0, SENDERS)):
-            if senders.start == 0:
-                hq = work.tile([P, SENDERS * P], I32, name="hq", bufs=HQ, align_bytes=64)
-                hs = work.tile([P, SENDERS * P], U8, name="hs", bufs=HQ, align_bytes=64)
-                hq_of[unit] = (hq, hs)
+        def quantise_h(unit, which=ALL):
+            if which.start == 0:
+                codes = work.tile([P, SENDERS * P], I32, name="hq", align_bytes=64)
+                scales = work.tile([P, SENDERS * P], U8, name="hs", align_bytes=64)
+                hq_of[unit] = (codes, scales)
             hq, hs = hq_of[unit]
-            cols = slice(P * senders.start, P * senders.stop)
-            nc.vector.quantize_mx(out=hq[:, cols].bitcast(FP8X4), scales=hs[:, cols], in_=h_of[unit][:, senders].rearrange("p j r t -> p (j r t)"))
+            cols = slice(P * which.start, P * which.stop)
+            nc.vector.quantize_mx(out=hq[:, cols].bitcast(FP8X4), scales=hs[:, cols], in_=h_of[unit][:, which].rearrange("p j r t -> p (j r t)"))
 
         def message(unit, c, tag="message", bufs=3):
             hq, hs = hq_of[unit]
-            size = units[unit][2]
-            bank = ps.tile([P, size * P], F32, name="bank", tag=tag, bufs=bufs)
+            bank = ps.tile([P, SENDERS * P], F32, name="bank", tag=tag, bufs=bufs)
             nc.tensor.matmul_mx(
                 out=bank[:],
                 lhsT=w2[:, 2 * P * c : 2 * P * (c + 1)].bitcast(FP4X4),
@@ -267,7 +265,7 @@ def tile_nonlocalmp_pa_t_w4_kernel(tc, F_bytes, F_scale, W1_words, W1_scales, b1
                 start=True,
                 stop=True,
             )
-            relu = work.tile([P, size, P], F32, name="relu", bufs=12, align_bytes=64)
+            relu = work.tile([P, SENDERS, P], F32, name="relu", bufs=12, align_bytes=64)
             relu_of[unit, c] = relu
             flat = relu[:].rearrange("p j r -> p (j r)")
             if (unit == LAST and c != 1) or (unit == LAST - 1 and c >= 2):
@@ -277,12 +275,11 @@ def tile_nonlocalmp_pa_t_w4_kernel(tc, F_bytes, F_scale, W1_words, W1_scales, b1
                 nc.scalar.activation(out=flat, in_=bank[:], func=ACT.Relu, bias=b2c[:, c : c + 1], scale=1.0)
 
         def linear(unit, j):
-            m, j0, size = units[unit]
-            if j >= size:
-                return
+            m, place = divmod(unit, PLACES)
+            node = SENDERS * place + j
             hq, hs = hq_of[unit]
-            if j0 + j == 0:
-                lin = ps.tile([P, C], F32, name="lin", tag="ring%d" % (m % 3))
+            if node == 0:
+                lin = ps.tile([P, C], F32, name="lin", tag=ring_bank(m))
                 lin_of[m] = lin
             nc.tensor.matmul_mx(
                 out=lin_of[m][:],
@@ -290,40 +287,39 @@ def tile_nonlocalmp_pa_t_w4_kernel(tc, F_bytes, F_scale, W1_words, W1_scales, b1
                 lhsT_scale=hs[:, P * j : P * (j + 1)],
                 rhs=w2[:].bitcast(FP4X4),
                 rhs_scale=w2s[:],
-                start=(j0 + j == 0),
-                stop=(j0 + j == NODES - 1),
+                start=(node == 0),
+                stop=(node == NODES - 1),
             )
 
-        def open_sum(m, chunks, tag):
-            total = ps.tile([P, len(chunks), P], F32, name="total", tag=tag)
-            for i, c in enumerate(chunks):
-                sum_of[m, c] = total[:, i, :]
-            sum_bank_of[m, chunks[0]] = total
-            if m == TILES - 1 and chunks[0] == 0:
-                nc.tensor.matmul(total[:, 0, :], lhsT=eights[:], rhs=b2row[:, 0:P], start=True, stop=False)
-                nc.tensor.matmul(total[:, 1, :], lhsT=fours[:], rhs=b2row[:, P : 2 * P], start=False, stop=False)
-                return
-            times = fours if m < TILES - 1 else twelves
-            b2_part = b2row[:, P * chunks[0] : P * (chunks[-1] + 1)]
-            nc.tensor.matmul(total[:].rearrange("p c r -> p (c r)"), lhsT=times[:], rhs=b2_part, start=True, stop=False)
+        def open_sum(m, first, runs, tag):
+            count = sum(chunks for chunks, times in runs)
+            total = ps.tile([P, count, P], F32, name="total", tag=tag)
+            total_of[m, first] = total
+            for i in range(count):
+                sum_of[m, first + i] = total[:, i, :]
+            done = 0
+            for chunks, times in runs:
+                to = total[:, done : done + chunks, :].rearrange("p c r -> p (c r)")
+                b2_part = b2row[:, P * (first + done) : P * (first + done + chunks)]
+                nc.tensor.matmul(to, lhsT=times[:], rhs=b2_part, start=(done == 0), stop=False)
+                done += chunks
 
         def add_up(unit, c, closing=False):
-            m, j0, size = units[unit]
-            for j in range(size):
-                closes = closing and j == size - 1
-                nc.tensor.matmul(sum_of[m, c], lhsT=relu_of[unit, c][:, j, :], rhs=ident[:], is_transpose=True, start=False, stop=closes)
+            for j in range(SENDERS):
+                stop = closing and j == SENDERS - 1
+                nc.tensor.matmul(sum_of[unit // PLACES, c], lhsT=relu_of[unit, c][:, j, :], rhs=ident[:], is_transpose=True, start=False, stop=stop)
 
         def leave_linear(m):
             fifth = work.tile([P, C], F32, name="fifth", bufs=2)
             fifth_of[m] = fifth
             nc.scalar.activation(out=fifth[:], in_=lin_of[m][:], func=ACT.Copy, scale=SLOPE)
 
-        def finish(m, start, end, queue):
-            cols = slice(P * start, P * end)
-            st = work.tile([P, P * (end - start)], F32, name="st", bufs=2)
+        def finish(m, first, end, queue):
+            cols = slice(P * first, P * end)
+            st = work.tile([P, P * (end - first)], F32, name="st", bufs=2)
             nc.vector.scalar_tensor_tensor(
                 out=st[:],
-                in0=sum_bank_of[m, start][:].rearrange("p c r -> p (c r)"),
+                in0=total_of[m, first][:].rearrange("p c r -> p (c r)"),
                 scalar=1.0 - SLOPE,
                 in1=fifth_of[m][:, cols],
                 op0=ALU.mult,
@@ -336,107 +332,92 @@ def tile_nonlocalmp_pa_t_w4_kernel(tc, F_bytes, F_scale, W1_words, W1_scales, b1
             for i in range(count):
                 nc.tensor.matmul(idle[:], lhsT=fours[:], rhs=b2row[:], start=True, stop=True)
 
-        warm_up(WARM)
+        warm_up(3)
         widen(0, nc.vector.tensor_copy)
         widen(1, nc.scalar.copy)
-        turn_f(0, "sum1")
+        turn_f(0, sum_bank(1))
         warm_up(4)
         nc.sync.dma_start(out=b2row[0:1, :], in_=b2.rearrange("(o c) -> o c", o=1))
-        permute_words(0)
+        permute_words(RECEIVERS)
         scale_f(0)
-        permute_scales(0)
+        permute_scales(RECEIVERS)
         quantise_f(0)
-        permute_words(1)
-        permute_scales(1)
-        first_product(0, 0, "ring2")
-        first_product(0, 1, "ring1")
-        resident = bank_of[0, 1]
-        first_product(0, 1, "sum1")
-        copy_senders(0)
-        bank_of[0, 1] = resident
-        turn_f(1, "ring0")
+        permute_words(SENDING)
+        permute_scales(SENDING)
+        receivers(0)
+        senders(0)
+        copy_senders(0, first_product(0, SENDING, sum_bank(1)))
+        turn_f(1, ring_bank(0))
         leave_receivers(0)
         turn_b2()
         widen(2, nc.scalar.copy)
-        turn_f(2, "sum0")
+        turn_f(2, sum_bank(0))
 
-        closed = {min(LAST, last[m] + LAG + 2 + DELAY): m for m in range(TILES - 1 - LATE_FINISH)}
-        scaled = {first[m] + 2: m + 2 for m in range(TILES - 2)}
-        scaled[0] = 1
-        received = {first[m] + 1: m + 1 for m in range(TILES - 1)}
-        LOW, HIGH = slice(0, SENDERS // 2), slice(SENDERS // 2, SENDERS)
-        extra_product = None
         for step in range(LAST + 1):
+            tile, place = divmod(step, PLACES)
             behind = step - LAG
-            tile = units[step][0] if step <= LAST else TILES
-            if step <= LAST:
-                adds(step, FIRST_SHARE if step == 0 else WIDE if step in scaled or step in received or step in closed else SHARE)
-            if step in scaled:
-                scale_f(scaled[step])
-            if step in received:
-                leave_receivers(received[step])
-            if step in closed:
-                finish(closed[step], 0, CHUNKS, nc.sync)
-            live = 0 <= behind <= LAST
-            ends_tile = tile + 1 < TILES and step == last[tile]
-            if ends_tile:
-                first_product(tile + 1, 1, "ring%d" % ((tile + 2) % 3))
-                copy_senders(tile + 1)
-            if live:
-                for c in range(AHEAD):
-                    message(behind, c)
+            receives = place == 1 and tile + 1 < TILES
+            scales = place == 2 and tile + 2 < TILES
+            finishes = place == 3 and tile >= 1
+            ends_tile = place == PLACES - 1
+
+            adds(step, FIRST_SHARE if step == 0 else WIDE if receives or scales or finishes else SHARE)
+            if step == 0:
+                scale_f(1)
+            if scales:
+                scale_f(tile + 2)
+            if receives:
+                leave_receivers(tile + 1)
+            if finishes:
+                finish(tile - 1, 0, CHUNKS, nc.sync)
+
+            if behind >= 0:
+                message(behind, 0)
+                message(behind, 1)
+                if ends_tile and tile + 1 < TILES:
+                    senders(tile + 1)
+                    copy_senders(tile + 1, b_bank_of[tile + 1])
                 if behind >= 1:
                     linear(behind - 1, 2)
                     linear(behind - 1, 3)
-                for c in range(AHEAD, 3):
-                    message(behind, c)
-                if FOURTH == 0:
-                    message(behind, 3)
+                message(behind, 2)
                 linear(behind, 0)
-                if FOURTH == 1:
-                    message(behind, 3)
-                if extra_product is not None:
-                    first_product(*extra_product)
+                message(behind, 3)
+                if place == 0 and tile + 1 < TILES:
+                    receivers(tile + 1)
                 linear(behind, 1)
-                if FOURTH == 2:
-                    message(behind, 3)
-            extra_product = None
-            if behind >= 1 and behind - 1 in last.values():
-                leave_linear(units[behind - 1][0])
-            if step <= LAST:
-                scalar_part(step, 0)
-                scalar_part(step, 1)
+            opens_tile = place == LAG
+            if opens_tile and tile >= 1:
+                leave_linear(tile - 1)
+            scalar_parts(step)
             if step < LAG:
                 for m in range(3 + 3 * step, min(TILES, 6 + 3 * step)):
                     widen(m, nc.scalar.copy)
+
             if step == LAST:
-                open_sum(tile, (2, 3), "ring%d" % ((tile - 1) % 3))
+                open_sum(tile, 2, [(2, twelves)], ring_bank(tile - 1))
             if behind >= 1:
                 add_up(behind - 1, 2)
-                add_up(behind - 1, 3, behind - 1 in last.values())
-            if live:
-                if units[behind][1] == 0:
-                    open_sum(tile, (0, 1) if tile == TILES - 1 else (0, 1, 2, 3), "sum%d" % (tile % 2))
-                if behind < LAST - CHAINED:
-                    add_up(behind, 0)
-                    add_up(behind, 1)
-            if DELAY == 0 and ends_tile and tile + 3 < TILES:
-                turn_f(tile + 3, "sum%d" % ((tile + 1) % 2))
-            if DELAY == 1 and step == first[tile] and 1 <= tile < TILES - 2:
-                turn_f(tile + 2, "sum%d" % (tile % 2))
-            if ends_tile and tile + 2 < TILES:
-                extra_product = (tile + 2, 0, "ring%d" % ((tile + 1) % 3))
-            if 1 <= step <= LAST + 1:
+                add_up(behind - 1, 3, closing=opens_tile)
+            if opens_tile:
+                open_sum(tile, 0, [(1, eights), (1, fours)] if tile == TILES - 1 else [(CHUNKS, fours)], sum_bank(tile))
+            if 0 <= behind < LAST - CHAINED:
+                add_up(behind, 0)
+                add_up(behind, 1)
+            if ends_tile and tile + 3 < TILES:
+                turn_f(tile + 3, sum_bank(tile + 1))
+
+            if step >= 1:
                 join(step - 1)
-            if step in scaled and step > 0:
-                quantise_f(scaled[step])
-            if step < LAST - 1:
+            if scales:
+                quantise_f(tile + 2)
+            if step == 0:
                 leaky(step)
-                if step == 0:
-                    quantise_f(1)
-                    first_product(1, 0, "ring0")
-                else:
-                    quantise_h(step - 1)
+                quantise_f(1)
+                receivers(1)
+            elif step < LAST - 1:
+                leaky(step)
+                quantise_h(step - 1)
             elif step == LAST - 1:
                 leaky(step, LOW)
                 quantise_h(step - 1)
@@ -461,26 +442,19 @@ def tile_nonlocalmp_pa_t_w4_kernel(tc, F_bytes, F_scale, W1_words, W1_scales, b1
         add_pair(0)
         add_pair(1)
         message(LAST - 1, 2)
-        message(LAST - 1, 3, "ring%d" % (TILES % 3), 1)
+        message(LAST - 1, 3, ring_bank(TILES), 1)
         for j in range(SENDERS):
             linear(LAST - 1, j)
         for c in (2, 3, 1):
             message(LAST, c)
-        if LATE_FINISH:
-            linear(LAST, 0)
-            message(LAST, 0, "ring%d" % (TILES % 3), 1)
-            for j in range(1, SENDERS):
-                linear(LAST, j)
-            finish(TILES - 2, 0, CHUNKS, nc.sync)
-        else:
-            message(LAST, 0, "sum%d" % (TILES % 2), 1)
-            for j in range(SENDERS):
-                linear(LAST, j)
+        message(LAST, 0, sum_bank(TILES), 1)
+        for j in range(SENDERS):
+            linear(LAST, j)
         leave_linear(TILES - 1)
         add_up(LAST, 2)
-        add_up(LAST, 3, True)
-        finish(TILES - 1, 2, 4, nc.sync)
+        add_up(LAST, 3, closing=True)
+        finish(TILES - 1, 2, CHUNKS, nc.sync)
         add_up(LAST, 1)
         add_up(LAST, 0)
-        add_up(LAST - 1, 1, True)
+        add_up(LAST - 1, 1, closing=True)
         finish(TILES - 1, 0, 2, nc.scalar)

@@ -6,6 +6,7 @@ from concourse.masks import make_identity
 F32 = mybir.dt.float32
 BF16 = mybir.dt.bfloat16
 I32 = mybir.dt.int32
+U16 = mybir.dt.uint16
 U8 = mybir.dt.uint8
 FP8 = mybir.dt.float8_e4m3fn
 FP8X4 = mybir.dt.float8_e4m3fn_x4
@@ -30,10 +31,15 @@ LOW, HIGH, ALL = slice(0, SENDERS // 2), slice(SENDERS // 2, SENDERS), slice(0, 
 
 SHARE = 40
 WIDE = 48
-FIRST_SHARE = 24
+FIRST_SHARE = 32
 MOST = 50
 FEWER = 42
-EARLY = 64
+EARLY = 80
+SECOND = 40
+MB = 3
+SHIFT = P - SHARE
+WA = 5
+WB = 7
 CHAINED = 2
 
 
@@ -71,6 +77,7 @@ def tile_nonlocalmp_pa_t_w4_kernel(tc, F_bytes, F_scale, W1_words, W1_scales, b1
         nc.sync.dma_start(out=w1raw[:, RECEIVERS, :].bitcast(I32), in_=W1_words[RECEIVERS].bitcast(I32))
         fsc = const.tile([P, 4], F32)
         nc.sync.dma_start(out=fsc[:], in_=F_scale.rearrange("a c (p t) -> p (a c t)", t=4))
+        nc.sync.dma_start(out=fbytes[1][:], in_=tokens(F_bytes, 1))
         w1sraw = const.tile([P, 2, C], U8, align_bytes=64)
         w2s = const.tile([P, C], U8, align_bytes=64)
         fours = const.tile([P, P], BF16)
@@ -86,15 +93,14 @@ def tile_nonlocalmp_pa_t_w4_kernel(tc, F_bytes, F_scale, W1_words, W1_scales, b1
         nc.sync.dma_start(out=w1raw[:, SENDING, :].bitcast(I32), in_=W1_words[SENDING].bitcast(I32))
         b1raw = const.tile([P, 4], BF16)
         nc.sync.dma_start(out=b1raw[:], in_=b1.rearrange("(p t) -> p t", t=4))
-        nc.sync.dma_start(out=fbytes[1][:], in_=tokens(F_bytes, 1))
+        for m in range(2, TILES):
+            nc.sync.dma_start(out=fbytes[m][:], in_=tokens(F_bytes, m))
         b2raw = const.tile([P, P], BF16)
         nc.sync.dma_start(out=b2raw[0:CHUNKS, :], in_=b2.rearrange("(c p) -> c p", p=P))
         w2 = const.tile([P, 2 * C], U8, align_bytes=64)
         nc.sync.dma_start(out=w2[:].bitcast(I32), in_=W2_words[0].bitcast(I32))
         for row in range(4):
             nc.sync.dma_start(out=w2s[row:P:32, :].bitcast(I32), in_=w2s_src[row].bitcast(I32))
-        for m in range(2, TILES):
-            nc.sync.dma_start(out=fbytes[m][:], in_=tokens(F_bytes, m))
 
         ident = const.tile([P, P], F32)
         make_identity(nc, ident[:])
@@ -109,10 +115,7 @@ def tile_nonlocalmp_pa_t_w4_kernel(tc, F_bytes, F_scale, W1_words, W1_scales, b1
         w1s = const.tile([P, 2, 4, P], U8, align_bytes=64)
 
         def permute_words(half):
-            nc.vector.tensor_copy(
-                out=w1p[:, half].rearrange("p t (m e) -> p t m e", e=2),
-                in_=w1raw[:, half, :].rearrange("p (m t e) -> p t m e", t=4, e=2),
-            )
+            nc.scalar.copy(out=w1p[:, half].bitcast(U16), in_=w1raw[:, half, :].bitcast(U16).rearrange("p (m t) -> p t m", t=4))
 
         def permute_scales(half):
             nc.vector.tensor_copy(out=w1s[:, half], in_=w1sraw[:, half, :].rearrange("p (m t) -> p t m", t=4))
@@ -124,6 +127,8 @@ def tile_nonlocalmp_pa_t_w4_kernel(tc, F_bytes, F_scale, W1_words, W1_scales, b1
             nc.scalar.copy(out=b2f[0:CHUNKS, :], in_=b2raw[0:CHUNKS, :])
             bt = ps.tile([P, P], F32, name="bt", tag=sum_bank(1))
             nc.tensor.transpose(bt[:], b2f[:], ident[:])
+            for m in range(WA, WB):
+                widen(m, nc.scalar.copy)
             nc.scalar.copy(out=b2c[:], in_=bt[:, 0:CHUNKS])
             nc.scalar.activation(out=b2neg[:], in_=bt[:, 0:CHUNKS], func=ACT.Copy, scale=-1.0)
 
@@ -190,10 +195,10 @@ def tile_nonlocalmp_pa_t_w4_kernel(tc, F_bytes, F_scale, W1_words, W1_scales, b1
         h_of, part_of, hq_of, relu_of = {}, {}, {}, {}
         lin_of, sum_of, total_of, fifth_of = {}, {}, {}, {}
 
-        v_all = const.tile([P, SENDERS, P + EARLY, 4], F32, align_bytes=64)
+        v_all = const.tile([P, SENDERS, P + SHIFT, 4], F32, align_bytes=64)
 
         def v_of(unit):
-            start = EARLY * (unit % 2)
+            start = SHIFT * (unit % 2)
             return v_all[:, :, start : start + P, :]
 
         def by_scalar(unit):
@@ -253,7 +258,7 @@ def tile_nonlocalmp_pa_t_w4_kernel(tc, F_bytes, F_scale, W1_words, W1_scales, b1
             cols = slice(P * which.start, P * which.stop)
             nc.vector.quantize_mx(out=hq[:, cols].bitcast(FP8X4), scales=hs[:, cols], in_=h_of[unit][:, which].rearrange("p j r t -> p (j r t)"))
 
-        def message(unit, c, tag="message", bufs=3):
+        def message(unit, c, tag="message", bufs=MB):
             hq, hs = hq_of[unit]
             bank = ps.tile([P, SENDERS * P], F32, name="bank", tag=tag, bufs=bufs)
             nc.tensor.matmul_mx(
@@ -328,42 +333,48 @@ def tile_nonlocalmp_pa_t_w4_kernel(tc, F_bytes, F_scale, W1_words, W1_scales, b1
             queue.dma_start(out=tokens(out, m)[:, :, cols], in_=st[:])
 
         def warm_up(count):
-            idle = ps.tile([P, C], F32, name="idle", tag="message", bufs=3)
+            idle = ps.tile([P, C], F32, name="idle", tag="message", bufs=MB)
             for i in range(count):
                 nc.tensor.matmul(idle[:], lhsT=fours[:], rhs=b2row[:], start=True, stop=True)
 
         warm_up(3)
         widen(0, nc.vector.tensor_copy)
-        widen(1, nc.scalar.copy)
+        widen(1, nc.vector.tensor_copy)
+        permute_words(RECEIVERS)
         turn_f(0, sum_bank(1))
+        turn_f(1, ring_bank(0))
         warm_up(4)
         nc.sync.dma_start(out=b2row[0:1, :], in_=b2.rearrange("(o c) -> o c", o=1))
-        permute_words(RECEIVERS)
         scale_f(0)
         permute_scales(RECEIVERS)
         quantise_f(0)
         permute_words(SENDING)
         permute_scales(SENDING)
+        for m in range(2, WA):
+            widen(m, nc.scalar.copy)
         receivers(0)
         senders(0)
         copy_senders(0, first_product(0, SENDING, sum_bank(1)))
-        turn_f(1, ring_bank(0))
+        scale_f(1)
         leave_receivers(0)
-        turn_b2()
-        widen(2, nc.scalar.copy)
+        quantise_f(1)
         turn_f(2, sum_bank(0))
+        receivers(1)
+        turn_b2()
 
         for step in range(LAST + 1):
             tile, place = divmod(step, PLACES)
             behind = step - LAG
-            receives = place == 1 and tile + 1 < TILES
-            scales = place == 2 and tile + 2 < TILES
+            receives = place == 1 and 1 <= tile < TILES - 1
+            scales = place == 2 and 1 <= tile < TILES - 2
             finishes = place == 3 and tile >= 1
             ends_tile = place == PLACES - 1
 
-            adds(step, FIRST_SHARE if step == 0 else WIDE if receives or scales or finishes else SHARE)
+            adds(step, FIRST_SHARE if step == 0 else WIDE if receives or scales or finishes else SECOND if step == 1 else SHARE)
             if step == 0:
-                scale_f(1)
+                leave_receivers(1)
+            if step == 1:
+                scale_f(2)
             if scales:
                 scale_f(tile + 2)
             if receives:
@@ -374,7 +385,7 @@ def tile_nonlocalmp_pa_t_w4_kernel(tc, F_bytes, F_scale, W1_words, W1_scales, b1
             if behind >= 0:
                 message(behind, 0)
                 message(behind, 1)
-                if ends_tile and tile + 1 < TILES:
+                if ends_tile and 1 <= tile < TILES - 1:
                     senders(tile + 1)
                     copy_senders(tile + 1, b_bank_of[tile + 1])
                 if behind >= 1:
@@ -390,16 +401,19 @@ def tile_nonlocalmp_pa_t_w4_kernel(tc, F_bytes, F_scale, W1_words, W1_scales, b1
             if opens_tile and tile >= 1:
                 leave_linear(tile - 1)
             scalar_parts(step)
-            if step < LAG:
-                for m in range(3 + 3 * step, min(TILES, 6 + 3 * step)):
+            if step == 1:
+                for m in range(WB, TILES):
                     widen(m, nc.scalar.copy)
+                open_sum(0, 0, [(CHUNKS, fours)], sum_bank(0))
+                senders(1)
+                copy_senders(1, b_bank_of[1])
 
             if step == LAST:
                 open_sum(tile, 2, [(2, twelves)], ring_bank(tile - 1))
             if behind >= 1:
                 add_up(behind - 1, 2)
                 add_up(behind - 1, 3, closing=opens_tile)
-            if opens_tile:
+            if opens_tile and tile >= 1:
                 open_sum(tile, 0, [(1, eights), (1, fours)] if tile == TILES - 1 else [(CHUNKS, fours)], sum_bank(tile))
             if 0 <= behind < LAST - CHAINED:
                 add_up(behind, 0)
@@ -409,12 +423,12 @@ def tile_nonlocalmp_pa_t_w4_kernel(tc, F_bytes, F_scale, W1_words, W1_scales, b1
 
             if step >= 1:
                 join(step - 1)
+            if step == 1:
+                quantise_f(2)
             if scales:
                 quantise_f(tile + 2)
             if step == 0:
                 leaky(step)
-                quantise_f(1)
-                receivers(1)
             elif step < LAST - 1:
                 leaky(step)
                 quantise_h(step - 1)

@@ -31,14 +31,17 @@ LOW, HIGH, ALL = slice(0, SENDERS // 2), slice(SENDERS // 2, SENDERS), slice(0, 
 
 SHARE = 40
 WIDE = 48
-FIRST_SHARE = 32
+FIRST_SHARE = 24
 MOST = 50
 FEWER = 42
 EARLY = 80
 SECOND = 40
 MB = 3
+W3 = 2
+W1 = 3
+W2N = 2
 SHIFT = P - SHARE
-WA = 5
+WA = 4
 WB = 7
 CHAINED = 2
 
@@ -74,7 +77,7 @@ def tile_nonlocalmp_pa_t_w4_kernel(tc, F_bytes, F_scale, W1_words, W1_scales, b1
             fbytes.append(fb)
         nc.sync.dma_start(out=fbytes[0][:], in_=tokens(F_bytes, 0))
         w1raw = const.tile([P, 2, 2 * C], U8, align_bytes=64)
-        nc.sync.dma_start(out=w1raw[:, RECEIVERS, :].bitcast(I32), in_=W1_words[RECEIVERS].bitcast(I32))
+        nc.sync.dma_start(out=w1raw[:].bitcast(I32), in_=W1_words.rearrange("g p n -> p g n").bitcast(I32))
         fsc = const.tile([P, 4], F32)
         nc.sync.dma_start(out=fsc[:], in_=F_scale.rearrange("a c (p t) -> p (a c t)", t=4))
         nc.sync.dma_start(out=fbytes[1][:], in_=tokens(F_bytes, 1))
@@ -90,7 +93,6 @@ def tile_nonlocalmp_pa_t_w4_kernel(tc, F_bytes, F_scale, W1_words, W1_scales, b1
         w2s_src = W2_scales.rearrange("g (q r) n -> r q (g n)", r=4)
         for row in range(4):
             nc.sync.dma_start(out=w1sraw[row:P:32, :, :].bitcast(I32), in_=w1s_src[row].bitcast(I32))
-        nc.sync.dma_start(out=w1raw[:, SENDING, :].bitcast(I32), in_=W1_words[SENDING].bitcast(I32))
         b1raw = const.tile([P, 4], BF16)
         nc.sync.dma_start(out=b1raw[:], in_=b1.rearrange("(p t) -> p t", t=4))
         for m in range(2, TILES):
@@ -337,18 +339,18 @@ def tile_nonlocalmp_pa_t_w4_kernel(tc, F_bytes, F_scale, W1_words, W1_scales, b1
             for i in range(count):
                 nc.tensor.matmul(idle[:], lhsT=fours[:], rhs=b2row[:], start=True, stop=True)
 
-        warm_up(3)
+        warm_up(W1)
         widen(0, nc.vector.tensor_copy)
         widen(1, nc.vector.tensor_copy)
         permute_words(RECEIVERS)
+        permute_words(SENDING)
         turn_f(0, sum_bank(1))
         turn_f(1, ring_bank(0))
-        warm_up(4)
+        warm_up(W2N)
         nc.sync.dma_start(out=b2row[0:1, :], in_=b2.rearrange("(o c) -> o c", o=1))
         scale_f(0)
         permute_scales(RECEIVERS)
         quantise_f(0)
-        permute_words(SENDING)
         permute_scales(SENDING)
         for m in range(2, WA):
             widen(m, nc.scalar.copy)
@@ -407,14 +409,16 @@ def tile_nonlocalmp_pa_t_w4_kernel(tc, F_bytes, F_scale, W1_words, W1_scales, b1
                 open_sum(0, 0, [(CHUNKS, fours)], sum_bank(0))
                 senders(1)
                 copy_senders(1, b_bank_of[1])
+                if W3:
+                    warm_up(W3)
 
             if step == LAST:
                 open_sum(tile, 2, [(2, twelves)], ring_bank(tile - 1))
+            if opens_tile and tile >= 1:
+                open_sum(tile, 0, [(1, eights), (1, fours)] if tile == TILES - 1 else [(CHUNKS, fours)], sum_bank(tile))
             if behind >= 1:
                 add_up(behind - 1, 2)
                 add_up(behind - 1, 3, closing=opens_tile)
-            if opens_tile and tile >= 1:
-                open_sum(tile, 0, [(1, eights), (1, fours)] if tile == TILES - 1 else [(CHUNKS, fours)], sum_bank(tile))
             if 0 <= behind < LAST - CHAINED:
                 add_up(behind, 0)
                 add_up(behind, 1)

@@ -37,6 +37,8 @@ FEWER = 42
 EARLY = 80
 SECOND = 40
 MB = 3
+C1 = 1
+LF = 1
 W3 = 2
 W1 = 3
 W2N = 2
@@ -239,8 +241,7 @@ def tile_nonlocalmp_pa_t_w4_kernel(tc, F_bytes, F_scale, W1_words, W1_scales, b1
 
         def leaky(unit, which=ALL):
             if which.start == 0:
-                tag, bufs = ("h_last", 1) if unit == LAST else ("h", 3)
-                h = work.tile([P, SENDERS, P, 4], BF16, name="h", tag=tag, bufs=bufs, align_bytes=64)
+                h = work.tile([P, SENDERS, P, 4], BF16, name="h", align_bytes=64)
                 h_of[unit] = h
             src = v_of(unit)[:, which, by_vector(unit), :].rearrange("p j r t -> p j (r t)")
             to = h_of[unit][:, which, by_vector(unit), :].rearrange("p j r t -> p j (r t)")
@@ -275,7 +276,7 @@ def tile_nonlocalmp_pa_t_w4_kernel(tc, F_bytes, F_scale, W1_words, W1_scales, b1
             relu = work.tile([P, SENDERS, P], F32, name="relu", bufs=12, align_bytes=64)
             relu_of[unit, c] = relu
             flat = relu[:].rearrange("p j r -> p (j r)")
-            if (unit == LAST and c != 1) or (unit == LAST - 1 and c >= 2):
+            if (unit == LAST and (c != 1 or C1)) or (unit == LAST - 1 and c >= 2):
                 before = relu_of[unit - 1, c][:].rearrange("p j r -> p (j r)")
                 nc.vector.scalar_tensor_tensor(out=flat, in0=bank[:], scalar=b2neg[:, c : c + 1], in1=before, op0=ALU.max, op1=ALU.add)
             else:
@@ -323,7 +324,7 @@ def tile_nonlocalmp_pa_t_w4_kernel(tc, F_bytes, F_scale, W1_words, W1_scales, b1
 
         def finish(m, first, end, queue):
             cols = slice(P * first, P * end)
-            st = work.tile([P, P * (end - first)], F32, name="st", bufs=2)
+            st = work.tile([P, P * (end - first)], F32, name="st", bufs=TILES + 1)
             nc.vector.scalar_tensor_tensor(
                 out=st[:],
                 in0=total_of[m, first][:].rearrange("p c r -> p (c r)"),
@@ -415,11 +416,11 @@ def tile_nonlocalmp_pa_t_w4_kernel(tc, F_bytes, F_scale, W1_words, W1_scales, b1
             if step == LAST:
                 open_sum(tile, 2, [(2, twelves)], ring_bank(tile - 1))
             if opens_tile and tile >= 1:
-                open_sum(tile, 0, [(1, eights), (1, fours)] if tile == TILES - 1 else [(CHUNKS, fours)], sum_bank(tile))
+                open_sum(tile, 0, ([(2, eights)] if C1 else [(1, eights), (1, fours)]) if tile == TILES - 1 else [(CHUNKS, fours)], sum_bank(tile))
             if behind >= 1:
                 add_up(behind - 1, 2)
                 add_up(behind - 1, 3, closing=opens_tile)
-            if 0 <= behind < LAST - CHAINED:
+            if behind >= 0:
                 add_up(behind, 0)
                 add_up(behind, 1)
             if ends_tile and tile + 3 < TILES:
@@ -448,31 +449,33 @@ def tile_nonlocalmp_pa_t_w4_kernel(tc, F_bytes, F_scale, W1_words, W1_scales, b1
                 quantise_h(step, LOW)
                 quantise_h(step, HIGH)
 
-        def add_pair(c):
-            both = work.tile([P, SENDERS, P], F32, name="both", tag=("h_last", "both")[c], bufs=1, align_bytes=64)
-            nc.gpsimd.tensor_tensor(out=both[:], in0=relu_of[LAST - 2, c][:], in1=relu_of[LAST - 1, c][:], op=ALU.add)
-            relu_of[LAST - 1, c] = both
-
         linear(LAST - 2, 2)
         linear(LAST - 2, 3)
+        for j in range(LF):
+            linear(LAST - 1, j)
         message(LAST - 1, 0)
         message(LAST - 1, 1)
-        add_pair(0)
-        add_pair(1)
         message(LAST - 1, 2)
         message(LAST - 1, 3, ring_bank(TILES), 1)
-        for j in range(SENDERS):
+        for j in range(LF, SENDERS):
             linear(LAST - 1, j)
-        for c in (2, 3, 1):
+        for j in range(LF):
+            linear(LAST, j)
+        message(LAST, 2, sum_bank(TILES), 1)
+        for c in ((3, 0, 1) if C1 else (3, 1, 0)):
             message(LAST, c)
-        message(LAST, 0, sum_bank(TILES), 1)
-        for j in range(SENDERS):
+        for j in range(LF, SENDERS):
             linear(LAST, j)
         leave_linear(TILES - 1)
+        if not C1:
+            add_up(LAST - 1, 1)
         add_up(LAST, 2)
         add_up(LAST, 3, closing=True)
         finish(TILES - 1, 2, CHUNKS, nc.sync)
-        add_up(LAST, 1)
-        add_up(LAST, 0)
-        add_up(LAST - 1, 1, closing=True)
+        if not C1:
+            add_up(LAST, 1)
+            add_up(LAST, 0, closing=True)
+        else:
+            add_up(LAST, 0)
+            add_up(LAST, 1, closing=True)
         finish(TILES - 1, 0, 2, nc.scalar)

@@ -35,16 +35,8 @@ FIRST_SHARE = 24
 MOST = 50
 FEWER = 42
 EARLY = 80
-SECOND = 40
-MB = 3
-C1 = 1
-LF = 1
-W3 = 2
-W1 = 3
-W2N = 2
 SHIFT = P - SHARE
-WA = 4
-WB = 7
+MESSAGE_BANKS = 3
 CHAINED = 2
 
 
@@ -131,8 +123,9 @@ def tile_nonlocalmp_pa_t_w4_kernel(tc, F_bytes, F_scale, W1_words, W1_scales, b1
             nc.scalar.copy(out=b2f[0:CHUNKS, :], in_=b2raw[0:CHUNKS, :])
             bt = ps.tile([P, P], F32, name="bt", tag=sum_bank(1))
             nc.tensor.transpose(bt[:], b2f[:], ident[:])
-            for m in range(WA, WB):
-                widen(m, nc.scalar.copy)
+            return bt
+
+        def leave_b2(bt):
             nc.scalar.copy(out=b2c[:], in_=bt[:, 0:CHUNKS])
             nc.scalar.activation(out=b2neg[:], in_=bt[:, 0:CHUNKS], func=ACT.Copy, scale=-1.0)
 
@@ -261,7 +254,7 @@ def tile_nonlocalmp_pa_t_w4_kernel(tc, F_bytes, F_scale, W1_words, W1_scales, b1
             cols = slice(P * which.start, P * which.stop)
             nc.vector.quantize_mx(out=hq[:, cols].bitcast(FP8X4), scales=hs[:, cols], in_=h_of[unit][:, which].rearrange("p j r t -> p (j r t)"))
 
-        def message(unit, c, tag="message", bufs=MB):
+        def message(unit, c, tag="message", bufs=MESSAGE_BANKS):
             hq, hs = hq_of[unit]
             bank = ps.tile([P, SENDERS * P], F32, name="bank", tag=tag, bufs=bufs)
             nc.tensor.matmul_mx(
@@ -276,7 +269,7 @@ def tile_nonlocalmp_pa_t_w4_kernel(tc, F_bytes, F_scale, W1_words, W1_scales, b1
             relu = work.tile([P, SENDERS, P], F32, name="relu", bufs=12, align_bytes=64)
             relu_of[unit, c] = relu
             flat = relu[:].rearrange("p j r -> p (j r)")
-            if (unit == LAST and (c != 1 or C1)) or (unit == LAST - 1 and c >= 2):
+            if unit == LAST or (unit == LAST - 1 and c >= 2):
                 before = relu_of[unit - 1, c][:].rearrange("p j r -> p (j r)")
                 nc.vector.scalar_tensor_tensor(out=flat, in0=bank[:], scalar=b2neg[:, c : c + 1], in1=before, op0=ALU.max, op1=ALU.add)
             else:
@@ -299,18 +292,13 @@ def tile_nonlocalmp_pa_t_w4_kernel(tc, F_bytes, F_scale, W1_words, W1_scales, b1
                 stop=(node == NODES - 1),
             )
 
-        def open_sum(m, first, runs, tag):
-            count = sum(chunks for chunks, times in runs)
+        def open_sum(m, first, count, times, tag):
             total = ps.tile([P, count, P], F32, name="total", tag=tag)
             total_of[m, first] = total
             for i in range(count):
                 sum_of[m, first + i] = total[:, i, :]
-            done = 0
-            for chunks, times in runs:
-                to = total[:, done : done + chunks, :].rearrange("p c r -> p (c r)")
-                b2_part = b2row[:, P * (first + done) : P * (first + done + chunks)]
-                nc.tensor.matmul(to, lhsT=times[:], rhs=b2_part, start=(done == 0), stop=False)
-                done += chunks
+            b2_part = b2row[:, P * first : P * (first + count)]
+            nc.tensor.matmul(total[:].rearrange("p c r -> p (c r)"), lhsT=times[:], rhs=b2_part, start=True, stop=False)
 
         def add_up(unit, c, closing=False):
             for j in range(SENDERS):
@@ -335,25 +323,18 @@ def tile_nonlocalmp_pa_t_w4_kernel(tc, F_bytes, F_scale, W1_words, W1_scales, b1
             )
             queue.dma_start(out=tokens(out, m)[:, :, cols], in_=st[:])
 
-        def warm_up(count):
-            idle = ps.tile([P, C], F32, name="idle", tag="message", bufs=MB)
-            for i in range(count):
-                nc.tensor.matmul(idle[:], lhsT=fours[:], rhs=b2row[:], start=True, stop=True)
-
-        warm_up(W1)
         widen(0, nc.vector.tensor_copy)
         widen(1, nc.vector.tensor_copy)
         permute_words(RECEIVERS)
         permute_words(SENDING)
         turn_f(0, sum_bank(1))
         turn_f(1, ring_bank(0))
-        warm_up(W2N)
         nc.sync.dma_start(out=b2row[0:1, :], in_=b2.rearrange("(o c) -> o c", o=1))
         scale_f(0)
         permute_scales(RECEIVERS)
         quantise_f(0)
         permute_scales(SENDING)
-        for m in range(2, WA):
+        for m in range(2, TILES // 2):
             widen(m, nc.scalar.copy)
         receivers(0)
         senders(0)
@@ -363,7 +344,10 @@ def tile_nonlocalmp_pa_t_w4_kernel(tc, F_bytes, F_scale, W1_words, W1_scales, b1
         quantise_f(1)
         turn_f(2, sum_bank(0))
         receivers(1)
-        turn_b2()
+        turned_b2 = turn_b2()
+        for m in range(TILES // 2, TILES - 1):
+            widen(m, nc.scalar.copy)
+        leave_b2(turned_b2)
 
         for step in range(LAST + 1):
             tile, place = divmod(step, PLACES)
@@ -373,7 +357,7 @@ def tile_nonlocalmp_pa_t_w4_kernel(tc, F_bytes, F_scale, W1_words, W1_scales, b1
             finishes = place == 3 and tile >= 1
             ends_tile = place == PLACES - 1
 
-            adds(step, FIRST_SHARE if step == 0 else WIDE if receives or scales or finishes else SECOND if step == 1 else SHARE)
+            adds(step, FIRST_SHARE if step == 0 else WIDE if receives or scales or finishes else SHARE)
             if step == 0:
                 leave_receivers(1)
             if step == 1:
@@ -405,18 +389,17 @@ def tile_nonlocalmp_pa_t_w4_kernel(tc, F_bytes, F_scale, W1_words, W1_scales, b1
                 leave_linear(tile - 1)
             scalar_parts(step)
             if step == 1:
-                for m in range(WB, TILES):
-                    widen(m, nc.scalar.copy)
-                open_sum(0, 0, [(CHUNKS, fours)], sum_bank(0))
+                widen(TILES - 1, nc.scalar.copy)
+                open_sum(0, 0, CHUNKS, fours, sum_bank(0))
                 senders(1)
                 copy_senders(1, b_bank_of[1])
-                if W3:
-                    warm_up(W3)
 
             if step == LAST:
-                open_sum(tile, 2, [(2, twelves)], ring_bank(tile - 1))
-            if opens_tile and tile >= 1:
-                open_sum(tile, 0, ([(2, eights)] if C1 else [(1, eights), (1, fours)]) if tile == TILES - 1 else [(CHUNKS, fours)], sum_bank(tile))
+                open_sum(tile, 2, 2, twelves, ring_bank(tile - 1))
+            if opens_tile and 1 <= tile < TILES - 1:
+                open_sum(tile, 0, CHUNKS, fours, sum_bank(tile))
+            if opens_tile and tile == TILES - 1:
+                open_sum(tile, 0, 2, eights, sum_bank(tile))
             if behind >= 1:
                 add_up(behind - 1, 2)
                 add_up(behind - 1, 3, closing=opens_tile)
@@ -451,31 +434,21 @@ def tile_nonlocalmp_pa_t_w4_kernel(tc, F_bytes, F_scale, W1_words, W1_scales, b1
 
         linear(LAST - 2, 2)
         linear(LAST - 2, 3)
-        for j in range(LF):
-            linear(LAST - 1, j)
+        linear(LAST - 1, 0)
         message(LAST - 1, 0)
         message(LAST - 1, 1)
         message(LAST - 1, 2)
         message(LAST - 1, 3, ring_bank(TILES), 1)
-        for j in range(LF, SENDERS):
+        for j in range(1, SENDERS):
             linear(LAST - 1, j)
-        for j in range(LF):
-            linear(LAST, j)
+        linear(LAST, 0)
         message(LAST, 2, sum_bank(TILES), 1)
-        for c in ((3, 0, 1) if C1 else (3, 1, 0)):
+        for c in (3, 0, 1):
             message(LAST, c)
-        for j in range(LF, SENDERS):
+        for j in range(1, SENDERS):
             linear(LAST, j)
         leave_linear(TILES - 1)
-        if not C1:
-            add_up(LAST - 1, 1)
-        add_up(LAST, 2)
-        add_up(LAST, 3, closing=True)
-        finish(TILES - 1, 2, CHUNKS, nc.sync)
-        if not C1:
-            add_up(LAST, 1)
-            add_up(LAST, 0, closing=True)
-        else:
-            add_up(LAST, 0)
-            add_up(LAST, 1, closing=True)
-        finish(TILES - 1, 0, 2, nc.scalar)
+        for first, queue in ((2, nc.sync), (0, nc.scalar)):
+            add_up(LAST, first)
+            add_up(LAST, first + 1, closing=True)
+            finish(TILES - 1, first, first + 2, queue)

from contextlib import ExitStack

import concourse.mybir as mybir
from concourse.masks import make_identity

F32 = mybir.dt.float32
BF16 = mybir.dt.bfloat16
I32 = mybir.dt.int32
U16 = mybir.dt.uint16
U8 = mybir.dt.uint8
FP8 = mybir.dt.float8_e4m3fn
FP8X4 = mybir.dt.float8_e4m3fn_x4
FP4X4 = mybir.dt.float4_e2m1fn_x4
ALU = mybir.AluOpType
ACT = mybir.ActivationFunctionType

P = 128
SETS, NODES, C = 64, 16, 512
SLOPE = 0.2
FLOPS = 2 * SETS * NODES * C * 2 * C + 2 * SETS * NODES * NODES * C * C

GROUP = P // NODES
TILES = SETS // GROUP
SENDERS = 4
PLACES = NODES // SENDERS
LAST = TILES * PLACES - 1
CHUNKS = C // P
LAG = 2
RECEIVERS, SENDING = 0, 1
LOW, HIGH, ALL = slice(0, SENDERS // 2), slice(SENDERS // 2, SENDERS), slice(0, SENDERS)

SHARE = 40
WIDE = 48
FIRST_SHARE = 24
MOST = 50
FEWER = 42
EARLY = 80
SHIFT = P - SHARE
MESSAGE_BANKS = 3
CHAINED = 2


def scalar_columns(unit):
    if unit < LAG:
        return EARLY
    if unit > LAST - CHAINED:
        return 0
    return FEWER if unit % PLACES == PLACES - 1 else MOST


def tile_nonlocalmp_pa_t_w4_kernel(tc, F_bytes, F_scale, W1_words, W1_scales, b1, W2_words, W2_scales, b2, out):
    nc = tc.nc
    with ExitStack() as ctx:
        ctx.enter_context(tc.manual_schedule())
        const = ctx.enter_context(tc.tile_pool(name="const", bufs=1))
        work = ctx.enter_context(tc.tile_pool(name="work", bufs=3))
        ps = ctx.enter_context(tc.psum_pool(name="ps", bufs=1))

        def sum_bank(m):
            return "sum%d" % (m % 2)

        def ring_bank(m):
            return "ring%d" % (m % 3)

        def tokens(dram, m):
            return dram[GROUP * m : GROUP * (m + 1)].rearrange("b i c -> i b c")

        fbytes = []
        for m in range(TILES):
            fb = const.tile([P, C], U8, name="fbytes%d" % m, align_bytes=64)
            fbytes.append(fb)
        nc.sync.dma_start(out=fbytes[0][:], in_=tokens(F_bytes, 0))
        w1raw = const.tile([P, 2, 2 * C], U8, align_bytes=64)
        nc.sync.dma_start(out=w1raw[:].bitcast(I32), in_=W1_words.rearrange("g p n -> p g n").bitcast(I32))
        fsc = const.tile([P, 4], F32)
        nc.sync.dma_start(out=fsc[:], in_=F_scale.rearrange("a c (p t) -> p (a c t)", t=4))
        nc.sync.dma_start(out=fbytes[1][:], in_=tokens(F_bytes, 1))
        w1sraw = const.tile([P, 2, C], U8, align_bytes=64)
        w2s = const.tile([P, C], U8, align_bytes=64)
        fours = const.tile([P, P], BF16)
        b2row = const.tile([P, C], BF16)
        nc.vector.memset(w1sraw[:].rearrange("p g n -> p (g n)").bitcast(I32), 0)
        nc.vector.memset(fours[:], 4.0)
        nc.vector.memset(b2row[:], 0.0)
        nc.vector.memset(w2s[:].bitcast(I32), 0)
        w1s_src = W1_scales.rearrange("g (q r) n -> r q g n", r=4)
        w2s_src = W2_scales.rearrange("g (q r) n -> r q (g n)", r=4)
        for row in range(4):
            nc.sync.dma_start(out=w1sraw[row:P:32, :, :].bitcast(I32), in_=w1s_src[row].bitcast(I32))
        b1raw = const.tile([P, 4], BF16)
        nc.sync.dma_start(out=b1raw[:], in_=b1.rearrange("(p t) -> p t", t=4))
        for m in range(2, TILES):
            nc.sync.dma_start(out=fbytes[m][:], in_=tokens(F_bytes, m))
        b2raw = const.tile([P, P], BF16)
        nc.sync.dma_start(out=b2raw[0:CHUNKS, :], in_=b2.rearrange("(c p) -> c p", p=P))
        w2 = const.tile([P, 2 * C], U8, align_bytes=64)
        nc.sync.dma_start(out=w2[:].bitcast(I32), in_=W2_words[0].bitcast(I32))
        for row in range(4):
            nc.sync.dma_start(out=w2s[row:P:32, :].bitcast(I32), in_=w2s_src[row].bitcast(I32))

        ident = const.tile([P, P], F32)
        make_identity(nc, ident[:])
        b2f = const.tile([P, P], F32)
        nc.vector.memset(b2f[:], 0.0)
        twelves = const.tile([P, P], BF16)
        nc.vector.memset(twelves[:], 12.0)
        eights = const.tile([P, P], BF16)
        nc.vector.memset(eights[:], 8.0)

        w1p = const.tile([P, 2, 4, 2 * P], U8, align_bytes=64)
        w1s = const.tile([P, 2, 4, P], U8, align_bytes=64)

        def permute_words(half):
            nc.scalar.copy(out=w1p[:, half].bitcast(U16), in_=w1raw[:, half, :].bitcast(U16).rearrange("p (m t) -> p t m", t=4))

        def permute_scales(half):
            nc.vector.tensor_copy(out=w1s[:, half], in_=w1sraw[:, half, :].rearrange("p (m t) -> p t m", t=4))

        b2c = const.tile([P, CHUNKS], F32)
        b2neg = const.tile([P, CHUNKS], F32)

        def turn_b2():
            nc.scalar.copy(out=b2f[0:CHUNKS, :], in_=b2raw[0:CHUNKS, :])
            bt = ps.tile([P, P], F32, name="bt", tag=sum_bank(1))
            nc.tensor.transpose(bt[:], b2f[:], ident[:])
            return bt

        def leave_b2(bt):
            nc.scalar.copy(out=b2c[:], in_=bt[:, 0:CHUNKS])
            nc.scalar.activation(out=b2neg[:], in_=bt[:, 0:CHUNKS], func=ACT.Copy, scale=-1.0)

        fwide = const.tile([P, TILES, C], BF16, align_bytes=64)
        turned_of, grouped_of, fq_of, a_of, b_of = {}, {}, {}, {}, {}

        def widen(m, copy):
            copy(out=fwide[:, m, :], in_=fbytes[m][:].bitcast(FP8))

        def turn_f(m, tag):
            xt = ps.tile([P, 2, P], F32, name="xt", tag=tag)
            turned_of[m] = xt
            words = fwide[:, m, :].bitcast(F32)
            for w in range(2):
                nc.tensor.transpose(xt[:, w, :], words[:, w::2], ident[:])

        def scale_f(m):
            fg = work.tile([P, P, 2, 2], BF16, name="fg", bufs=2, align_bytes=64)
            grouped_of[m] = fg
            sc = fsc[:].rearrange("p (o w e) -> p o w e", o=1, w=2).to_broadcast([P, P, 2, 2])
            src = turned_of[m][:].bitcast(BF16).rearrange("p w (n e) -> p n w e", e=2)
            nc.vector.tensor_tensor(out=fg[:], in0=src, in1=sc, op=ALU.mult)

        def quantise_f(m):
            fq = work.tile([P, P], I32, name="fq", align_bytes=64)
            fs = work.tile([P, P], U8, name="fs", align_bytes=64)
            fq_of[m] = (fq, fs)
            nc.vector.quantize_mx(out=fq[:].bitcast(FP8X4), scales=fs[:], in_=grouped_of[m][:].rearrange("p n w e -> p (n w e)"))

        def first_product(m, half, tag):
            fq, fs = fq_of[m]
            bank = ps.tile([P, 4, P], F32, name="bank", tag=tag)
            for t in range(4):
                nc.tensor.matmul_mx(
                    out=bank[:, t, :],
                    lhsT=w1p[:, half, t, :].bitcast(FP4X4),
                    lhsT_scale=w1s[:, half, t, :],
                    rhs=fq[:].bitcast(FP8X4),
                    rhs_scale=fs[:],
                    start=True,
                    stop=True,
                )
            return bank

        a_bank_of, b_bank_of = {}, {}

        def receivers(m):
            a_bank_of[m] = first_product(m, RECEIVERS, ring_bank(m - 1))

        def senders(m):
            b_bank_of[m] = first_product(m, SENDING, ring_bank(m + 1))

        def leave_receivers(m):
            a = work.tile([P, P, 4], F32, name="a", bufs=2, align_bytes=64)
            a_of[m] = a
            bias = b1raw[:].unsqueeze(1).to_broadcast([P, P, 4])
            nc.vector.tensor_tensor(out=a[:], in0=a_bank_of[m][:].rearrange("p t n -> p n t"), in1=bias, op=ALU.add)

        def copy_senders(m, bank):
            b = work.tile([P, P, 4], F32, name="b", bufs=2, align_bytes=64)
            b_of[m] = b
            nc.scalar.copy(out=b[:], in_=bank[:].rearrange("p t n -> p n t"))

        h_of, part_of, hq_of, relu_of = {}, {}, {}, {}
        lin_of, sum_of, total_of, fifth_of = {}, {}, {}, {}

        v_all = const.tile([P, SENDERS, P + SHIFT, 4], F32, align_bytes=64)

        def v_of(unit):
            start = SHIFT * (unit % 2)
            return v_all[:, :, start : start + P, :]

        def by_scalar(unit):
            width = scalar_columns(unit)
            return slice(0, width) if unit % 2 == 0 else slice(P - width, P)

        def by_vector(unit):
            width = scalar_columns(unit)
            return slice(width, P) if unit % 2 == 0 else slice(0, P - width)

        def add(unit, engine, nodes, bp):
            m, place = divmod(unit, PLACES)
            shape = [P, nodes.stop - nodes.start, SENDERS, GROUP, 4]
            engine.tensor_tensor(
                out=v_of(unit).rearrange("p j (i b) t -> p i j b t", b=GROUP)[:, nodes],
                in0=bp[:, SENDERS * place : SENDERS * (place + 1)].unsqueeze(1).to_broadcast(shape),
                in1=a_of[m][:].rearrange("p (i b) t -> p i b t", b=GROUP)[:, nodes].unsqueeze(2).to_broadcast(shape),
                op=ALU.add,
            )

        def adds(unit, columns):
            m = unit // PLACES
            cut = NODES - columns // GROUP if unit % 2 == 0 else columns // GROUP
            below, above = slice(0, cut), slice(cut, NODES)
            for_vector, for_gpsimd = (below, above) if unit % 2 == 0 else (above, below)
            add(unit, nc.gpsimd, for_gpsimd, b_of[m][:].rearrange("p (j b) t -> p j b t", b=GROUP))
            add(unit, nc.vector, for_vector, b_bank_of[m][:].rearrange("p t (j b) -> p j b t", b=GROUP))

        def scalar_parts(unit):
            width = scalar_columns(unit)
            if width > 0:
                for factor in (1.0, -SLOPE):
                    part = work.tile([P, SENDERS, width, 4], BF16, name="part", bufs=4, align_bytes=64)
                    part_of[unit, factor] = part
                    nc.scalar.activation(out=part[:], in_=v_of(unit)[:, :, by_scalar(unit), :], func=ACT.Relu, scale=factor)

        def leaky(unit, which=ALL):
            if which.start == 0:
                h = work.tile([P, SENDERS, P, 4], BF16, name="h", align_bytes=64)
                h_of[unit] = h
            src = v_of(unit)[:, which, by_vector(unit), :].rearrange("p j r t -> p j (r t)")
            to = h_of[unit][:, which, by_vector(unit), :].rearrange("p j r t -> p j (r t)")
            nc.vector.scalar_tensor_tensor(out=to, in0=src, scalar=SLOPE, in1=src, op0=ALU.mult, op1=ALU.max)

        def join(unit):
            if scalar_columns(unit) > 0:
                to = h_of[unit][:, :, by_scalar(unit), :]
                nc.vector.tensor_tensor(out=to, in0=part_of[unit, 1.0][:], in1=part_of[unit, -SLOPE][:], op=ALU.subtract)

        def quantise_h(unit, which=ALL):
            if which.start == 0:
                codes = work.tile([P, SENDERS * P], I32, name="hq", align_bytes=64)
                scales = work.tile([P, SENDERS * P], U8, name="hs", align_bytes=64)
                hq_of[unit] = (codes, scales)
            hq, hs = hq_of[unit]
            cols = slice(P * which.start, P * which.stop)
            nc.vector.quantize_mx(out=hq[:, cols].bitcast(FP8X4), scales=hs[:, cols], in_=h_of[unit][:, which].rearrange("p j r t -> p (j r t)"))

        def message(unit, c, tag="message", bufs=MESSAGE_BANKS):
            hq, hs = hq_of[unit]
            bank = ps.tile([P, SENDERS * P], F32, name="bank", tag=tag, bufs=bufs)
            nc.tensor.matmul_mx(
                out=bank[:],
                lhsT=w2[:, 2 * P * c : 2 * P * (c + 1)].bitcast(FP4X4),
                lhsT_scale=w2s[:, P * c : P * (c + 1)],
                rhs=hq[:].bitcast(FP8X4),
                rhs_scale=hs[:],
                start=True,
                stop=True,
            )
            relu = work.tile([P, SENDERS, P], F32, name="relu", bufs=12, align_bytes=64)
            relu_of[unit, c] = relu
            flat = relu[:].rearrange("p j r -> p (j r)")
            if unit == LAST or (unit == LAST - 1 and c >= 2):
                before = relu_of[unit - 1, c][:].rearrange("p j r -> p (j r)")
                nc.vector.scalar_tensor_tensor(out=flat, in0=bank[:], scalar=b2neg[:, c : c + 1], in1=before, op0=ALU.max, op1=ALU.add)
            else:
                nc.scalar.activation(out=flat, in_=bank[:], func=ACT.Relu, bias=b2c[:, c : c + 1], scale=1.0)

        def linear(unit, j):
            m, place = divmod(unit, PLACES)
            node = SENDERS * place + j
            hq, hs = hq_of[unit]
            if node == 0:
                lin = ps.tile([P, C], F32, name="lin", tag=ring_bank(m))
                lin_of[m] = lin
            nc.tensor.matmul_mx(
                out=lin_of[m][:],
                lhsT=hq[:, P * j : P * (j + 1)].bitcast(FP8X4),
                lhsT_scale=hs[:, P * j : P * (j + 1)],
                rhs=w2[:].bitcast(FP4X4),
                rhs_scale=w2s[:],
                start=(node == 0),
                stop=(node == NODES - 1),
            )

        def open_sum(m, first, count, times, tag):
            total = ps.tile([P, count, P], F32, name="total", tag=tag)
            total_of[m, first] = total
            for i in range(count):
                sum_of[m, first + i] = total[:, i, :]
            b2_part = b2row[:, P * first : P * (first + count)]
            nc.tensor.matmul(total[:].rearrange("p c r -> p (c r)"), lhsT=times[:], rhs=b2_part, start=True, stop=False)

        def add_up(unit, c, closing=False):
            for j in range(SENDERS):
                stop = closing and j == SENDERS - 1
                nc.tensor.matmul(sum_of[unit // PLACES, c], lhsT=relu_of[unit, c][:, j, :], rhs=ident[:], is_transpose=True, start=False, stop=stop)

        def leave_linear(m):
            fifth = work.tile([P, C], F32, name="fifth", bufs=2)
            fifth_of[m] = fifth
            nc.scalar.activation(out=fifth[:], in_=lin_of[m][:], func=ACT.Copy, scale=SLOPE)

        def finish(m, first, end, queue):
            cols = slice(P * first, P * end)
            st = work.tile([P, P * (end - first)], F32, name="st", bufs=TILES + 1)
            nc.vector.scalar_tensor_tensor(
                out=st[:],
                in0=total_of[m, first][:].rearrange("p c r -> p (c r)"),
                scalar=1.0 - SLOPE,
                in1=fifth_of[m][:, cols],
                op0=ALU.mult,
                op1=ALU.add,
            )
            queue.dma_start(out=tokens(out, m)[:, :, cols], in_=st[:])

        widen(0, nc.vector.tensor_copy)
        widen(1, nc.vector.tensor_copy)
        permute_words(RECEIVERS)
        permute_words(SENDING)
        turn_f(0, sum_bank(1))
        turn_f(1, ring_bank(0))
        nc.sync.dma_start(out=b2row[0:1, :], in_=b2.rearrange("(o c) -> o c", o=1))
        scale_f(0)
        permute_scales(RECEIVERS)
        quantise_f(0)
        permute_scales(SENDING)
        for m in range(2, TILES // 2):
            widen(m, nc.scalar.copy)
        receivers(0)
        senders(0)
        copy_senders(0, first_product(0, SENDING, sum_bank(1)))
        scale_f(1)
        leave_receivers(0)
        quantise_f(1)
        turn_f(2, sum_bank(0))
        receivers(1)
        turned_b2 = turn_b2()
        for m in range(TILES // 2, TILES - 1):
            widen(m, nc.scalar.copy)
        leave_b2(turned_b2)

        for step in range(LAST + 1):
            tile, place = divmod(step, PLACES)
            behind = step - LAG
            receives = place == 1 and 1 <= tile < TILES - 1
            scales = place == 2 and 1 <= tile < TILES - 2
            finishes = place == 3 and tile >= 1
            ends_tile = place == PLACES - 1

            adds(step, FIRST_SHARE if step == 0 else WIDE if receives or scales or finishes else SHARE)
            if step == 0:
                leave_receivers(1)
            if step == 1:
                scale_f(2)
            if scales:
                scale_f(tile + 2)
            if receives:
                leave_receivers(tile + 1)
            if finishes:
                finish(tile - 1, 0, CHUNKS, nc.sync)

            if behind >= 0:
                message(behind, 0)
                message(behind, 1)
                if ends_tile and 1 <= tile < TILES - 1:
                    senders(tile + 1)
                    copy_senders(tile + 1, b_bank_of[tile + 1])
                if behind >= 1:
                    linear(behind - 1, 2)
                    linear(behind - 1, 3)
                message(behind, 2)
                linear(behind, 0)
                message(behind, 3)
                if place == 0 and tile + 1 < TILES:
                    receivers(tile + 1)
                linear(behind, 1)
            opens_tile = place == LAG
            if opens_tile and tile >= 1:
                leave_linear(tile - 1)
            scalar_parts(step)
            if step == 1:
                widen(TILES - 1, nc.scalar.copy)
                open_sum(0, 0, CHUNKS, fours, sum_bank(0))
                senders(1)
                copy_senders(1, b_bank_of[1])

            if step == LAST:
                open_sum(tile, 2, 2, twelves, ring_bank(tile - 1))
            if opens_tile and 1 <= tile < TILES - 1:
                open_sum(tile, 0, CHUNKS, fours, sum_bank(tile))
            if opens_tile and tile == TILES - 1:
                open_sum(tile, 0, 2, eights, sum_bank(tile))
            if behind >= 1:
                add_up(behind - 1, 2)
                add_up(behind - 1, 3, closing=opens_tile)
            if behind >= 0:
                add_up(behind, 0)
                add_up(behind, 1)
            if ends_tile and tile + 3 < TILES:
                turn_f(tile + 3, sum_bank(tile + 1))

            if step >= 1:
                join(step - 1)
            if step == 1:
                quantise_f(2)
            if scales:
                quantise_f(tile + 2)
            if step == 0:
                leaky(step)
            elif step < LAST - 1:
                leaky(step)
                quantise_h(step - 1)
            elif step == LAST - 1:
                leaky(step, LOW)
                quantise_h(step - 1)
                leaky(step, HIGH)
                quantise_h(step, LOW)
            else:
                quantise_h(step - 1, HIGH)
                leaky(step, LOW)
                leaky(step, HIGH)
                quantise_h(step, LOW)
                quantise_h(step, HIGH)

        linear(LAST - 2, 2)
        linear(LAST - 2, 3)
        linear(LAST - 1, 0)
        message(LAST - 1, 0)
        message(LAST - 1, 1)
        message(LAST - 1, 2)
        message(LAST - 1, 3, ring_bank(TILES), 1)
        for j in range(1, SENDERS):
            linear(LAST - 1, j)
        linear(LAST, 0)
        message(LAST, 2, sum_bank(TILES), 1)
        for c in (3, 0, 1):
            message(LAST, c)
        for j in range(1, SENDERS):
            linear(LAST, j)
        leave_linear(TILES - 1)
        for first, queue in ((2, nc.sync), (0, nc.scalar)):
            add_up(LAST, first)
            add_up(LAST, first + 1, closing=True)
            finish(TILES - 1, first, first + 2, queue)
